import numpy as np
import ml_dtypes


def mxq(x, axis, fmt="e4m3"):
    dtype, down = {"e4m3": (ml_dtypes.float8_e4m3fn, 7), "e5m2": (ml_dtypes.float8_e5m2, 14)}[fmt]
    v = np.moveaxis(np.asarray(x, np.float32).astype(ml_dtypes.bfloat16).astype(np.float64), axis, -1)
    blocks = v.reshape(v.shape[:-1] + (-1, 32))
    amax = np.abs(blocks).max(-1, keepdims=True)
    byte = np.maximum(np.where(amax > 0, np.frexp(amax)[1] - 1 + 127, 0) - down, 1)
    scale = np.exp2(byte - 127.0)
    codes = (blocks / scale).astype(np.float32).astype(dtype).astype(np.float64)
    return np.moveaxis((codes * scale).reshape(v.shape), -1, axis)


WIDE = False


def mx_kscale(k):
    if not WIDE:
        return np.ones(k)
    levels = np.array([20, -20, 10, -10, 0])
    a = np.random.permutation(np.resize(levels, k // 512 * 4)).reshape(k // 512, 4)
    idx = np.arange(k)
    return np.exp2(a[idx // 512, idx % 128 // 32])


BF16 = ml_dtypes.bfloat16


def bf(x):
    return np.asarray(x, np.float32).astype(BF16)


def f64(x):
    return np.asarray(x).astype(np.float64)


L, F, O, N, B, D = 2, 512, 512, 1024, 1, 3
G = O + O + O
T = D * B * N


def sigmoid(v):
    return 1.0 / (1.0 + np.exp(-v))


def gru_parts(agg, x, wih, whh, bih, bhh):
    h = f64(x).transpose(1, 0, 2)[None]
    gi = f64(agg) @ f64(wih).T + f64(bih)
    gh = h @ f64(whh).T + f64(bhh)
    r = sigmoid(gi[..., :O] + gh[..., :O])
    z = sigmoid(gi[..., O:O + O] + gh[..., O:O + O])
    c = np.tanh(gi[..., O + O:] + r * gh[..., O + O:])
    return r, z, c, gh[0, ..., O + O:]


def setup_inputs():
    s = mx_kscale(N)
    agg0 = bf(np.random.standard_normal((D, B, N, O)))
    x = bf(np.random.standard_normal((N, B, F)))
    wih = bf(np.random.standard_normal((G, O)) * 0.7 / np.sqrt(O))
    whh = bf(np.random.standard_normal((G, O)) * 0.7 / np.sqrt(O))
    bih = bf(np.random.standard_normal(G) * 0.3)
    bhh = bf(np.random.standard_normal(G) * 0.3)
    wh = bf(np.random.standard_normal((F, O)) * 0.5 / np.sqrt(F))
    bh = bf(0.3 + np.random.standard_normal(O) * 0.2)
    g = bf(np.random.standard_normal((N, B, O)) * np.exp2(np.random.randint(-12, 1, (N, B, 1))) * 8.0 / s[:, None, None])
    r, z, c, hn = gru_parts(agg0, x, wih, whh, bih, bhh)
    gates = np.concatenate([r, z, c], axis=-1)
    t = np.maximum(f64(x) @ f64(wh) + f64(bh), 0.0)
    return {"agg": bf(f64(agg0) * s[None, None, :, None]), "x": x, "wih": wih, "whh": whh,
            "bih": bih, "bhh": bhh, "wh": wh, "bh": bh,
            "gates": np.asarray(gates, np.float32), "hn": np.asarray(hn, np.float32),
            "t": np.asarray(t, np.float32), "grad_out": g}


def reference(agg, x, wih, whh, bih, bhh, wh, bh, gates, hn, t, grad_out):
    h = f64(x).transpose(1, 0, 2)[None]
    gt = f64(gates)
    r, z, c = gt[..., :O], gt[..., O:O + O], gt[..., O + O:]
    tot = ((1.0 - z) * c + z * h).sum(0)
    live = np.where(tot > 0.0, 1.0, 0.0)
    dh = ((f64(grad_out) * f64(t)).transpose(1, 0, 2) * live)[None]
    dc = dh * (1.0 - z) * (1.0 - c * c)
    dr = dc * f64(hn)[None] * r * (1.0 - r)
    dz = dh * (h - c) * z * (1.0 - z)
    dgi = np.concatenate([dr, dz, dc], axis=-1).reshape(T, G)
    a = f64(agg).reshape(T, O)
    return mxq(dgi, 0, "e5m2").T @ mxq(a, 0, "e4m3")

@@ -1,0 +1,199 @@
+from contextlib import ExitStack
+
+import concourse.mybir as mybir
+
+F32 = mybir.dt.float32
+BF16 = mybir.dt.bfloat16
+U32 = mybir.dt.uint32
+U8 = mybir.dt.uint8
+E4M3_X4 = mybir.dt.float8_e4m3fn_x4
+E5M2_X4 = mybir.dt.float8_e5m2_x4
+ALU = mybir.AluOpType
+ACT = mybir.ActivationFunctionType
+
+P = 128
+PACK = 4
+K_PASS = P * PACK
+DIRS = 3
+NODES = 1024
+FEAT = 512
+GATES = 3
+R = 0
+Z = 1
+C = 2
+NODE_BLOCKS = NODES // K_PASS
+COLS = 256
+COL_BLOCKS = FEAT // COLS
+M_TILE = 128
+M_TILES = COLS // M_TILE
+RUN = 4
+
+FLOPS = 2 * DIRS * NODES * GATES * FEAT * FEAT
+BYTES = (
+    2 * DIRS * NODES * FEAT
+    + 2 * 2 * NODES * FEAT
+    + 4 * DIRS * NODES * GATES * FEAT
+    + 2 * 4 * NODES * FEAT
+    + 4 * GATES * FEAT * FEAT
+)
+
+
+def load_rows(nc, pool, rows, dtype, name):
+    width = rows.shape[1]
+    held = pool.tile([P, PACK, width], dtype, name=name, tag=name)
+    nc.sync.dma_start(out=held[:], in_=rows.rearrange("(p j) o -> p j o", j=PACK))
+    return held
+
+
+def quantise(nc, pools, values, x4_dtype, codes, scales):
+    width = values.shape[2]
+    grouped = pools["grouped"].tile(
+        [P, width, PACK], BF16, name="grouped%d" % width, tag="grouped%d" % width, align_bytes=64
+    )
+    nc.scalar.copy(
+        out=grouped[:].rearrange("p (c i) j -> p c j i", i=RUN),
+        in_=values.rearrange("p j (c i) -> p c j i", i=RUN),
+    )
+    nc.vector.quantize_mx(
+        out=codes.bitcast(x4_dtype),
+        scales=scales,
+        in_=grouped[:].rearrange("p o j -> p (o j)"),
+    )
+
+
+def tile_graphconvolution_pb_v_kernel(
+    tc, agg, x, wih, whh, bih, bhh, wh, bh, gates, hn, t, grad_out, out
+):
+    nc = tc.nc
+    with ExitStack() as ctx:
+        pools = {
+            "gate": ctx.enter_context(tc.tile_pool(name="gate", bufs=2 * DIRS)),
+            "node": ctx.enter_context(tc.tile_pool(name="node", bufs=2)),
+            "work": ctx.enter_context(tc.tile_pool(name="work", bufs=2)),
+            "grouped": ctx.enter_context(tc.tile_pool(name="grouped", bufs=4)),
+            "dgi_mx": ctx.enter_context(tc.tile_pool(name="dgi_mx", bufs=GATES * DIRS)),
+            "agg_mx": ctx.enter_context(tc.tile_pool(name="agg_mx", bufs=1)),
+            "result": ctx.enter_context(tc.tile_pool(name="result", bufs=4)),
+        }
+        psum = ctx.enter_context(tc.psum_pool(name="psum", bufs=1))
+
+        agg_codes = pools["agg_mx"].tile([P, NODE_BLOCKS, DIRS, FEAT], U32, align_bytes=64)
+        agg_scales = pools["agg_mx"].tile([P, NODE_BLOCKS, DIRS, FEAT], U8, align_bytes=64)
+
+        for cb in range(COL_BLOCKS):
+            cols = slice(cb * COLS, (cb + 1) * COLS)
+            acc = {}
+            for gate in range(GATES):
+                for m in range(M_TILES):
+                    acc[(gate, m)] = psum.tile(
+                        [M_TILE, FEAT], F32, name="acc%d%d" % (gate, m), tag="acc%d%d" % (gate, m)
+                    )
+
+            for nb in range(NODE_BLOCKS):
+                rows = slice(nb * K_PASS, (nb + 1) * K_PASS)
+
+                def load_gate(d, gate, name):
+                    first = gate * FEAT + cb * COLS
+                    return load_rows(
+                        nc, pools["gate"], gates[d, 0, rows, first : first + COLS], F32, name
+                    )
+
+                h = load_rows(nc, pools["node"], x[rows, 0, cols], BF16, "h")
+                c = []
+                z = []
+                for d in range(DIRS):
+                    c.append(load_gate(d, C, "c"))
+                    z.append(load_gate(d, Z, "z"))
+                r = [load_gate(d, R, "r") for d in range(DIRS)]
+                g = load_rows(nc, pools["node"], grad_out[rows, 0, cols], BF16, "g")
+                gt = load_rows(nc, pools["node"], t[rows, 0, cols], F32, "gt")
+                h_n = load_rows(nc, pools["node"], hn[0, rows, cols], F32, "h_n")
+
+                if cb == 0:
+                    for d in range(DIRS):
+                        agg_rows = load_rows(nc, pools["work"], agg[d, 0, rows, :], BF16, "agg_rows")
+                        quantise(
+                            nc, pools, agg_rows[:], E4M3_X4,
+                            agg_codes[:, nb, d, :], agg_scales[:, nb, d, :],
+                        )
+
+
+                zch = []
+                for d in range(DIRS):
+                    zch.append(
+                        pools["work"].tile([P, PACK, COLS], F32, name="zch", tag="zch", bufs=2 * DIRS)
+                    )
+                    nc.vector.tensor_tensor(out=zch[d][:], in0=c[d][:], in1=h[:], op=ALU.subtract)
+                for d in range(DIRS):
+                    nc.vector.tensor_tensor(out=zch[d][:], in0=z[d][:], in1=zch[d][:], op=ALU.mult)
+
+                for d in range(DIRS):
+                    nc.vector.scalar_tensor_tensor(
+                        out=r[d][:], in0=r[d][:], scalar=1.0, in1=r[d][:],
+                        op0=ALU.subtract, op1=ALU.mult,
+                    )
+
+                new = []
+                for d in range(DIRS):
+                    new.append(
+                        pools["work"].tile([P, PACK, COLS], F32, name="new", tag="new", bufs=2 * DIRS)
+                    )
+                    nc.vector.tensor_tensor(out=new[d][:], in0=c[d][:], in1=zch[d][:], op=ALU.subtract)
+                    nc.scalar.activation(out=c[d][:], in_=c[d][:], func=ACT.Square)
+
+                def times_hn(d):
+                    nc.vector.scalar_tensor_tensor(
+                        out=r[d][:], in0=r[d][:], scalar=-1.0, in1=h_n[:],
+                        op0=ALU.mult, op1=ALU.mult,
+                    )
+
+                tot = new[0]
+                nc.vector.tensor_tensor(out=gt[:], in0=g[:], in1=gt[:], op=ALU.mult)
+                nc.vector.tensor_tensor(out=tot[:], in0=new[0][:], in1=new[1][:], op=ALU.add)
+                times_hn(0)
+                nc.vector.tensor_tensor(out=tot[:], in0=tot[:], in1=new[2][:], op=ALU.add)
+                times_hn(1)
+                dh = new[1]
+                nc.vector.scalar_tensor_tensor(
+                    out=dh[:], in0=tot[:], scalar=0.0, in1=gt[:], op0=ALU.is_gt, op1=ALU.mult
+                )
+                times_hn(2)
+
+                for d in range(DIRS):
+                    nc.vector.scalar_tensor_tensor(
+                        out=z[d][:], in0=z[d][:], scalar=1.0, in1=dh[:],
+                        op0=ALU.subtract, op1=ALU.mult,
+                    )
+                for d in range(DIRS):
+                    nc.vector.tensor_tensor(out=zch[d][:], in0=z[d][:], in1=zch[d][:], op=ALU.mult)
+                for d in range(DIRS):
+                    nc.vector.scalar_tensor_tensor(
+                        out=c[d][:], in0=c[d][:], scalar=1.0, in1=z[d][:],
+                        op0=ALU.subtract, op1=ALU.mult,
+                    )
+                for d in range(DIRS):
+                    nc.vector.tensor_tensor(out=r[d][:], in0=c[d][:], in1=r[d][:], op=ALU.mult)
+
+                for gate, dgi in ((Z, zch), (C, c), (R, r)):
+                    for d in range(DIRS):
+                        codes = pools["dgi_mx"].tile([P, COLS], U32, name="codes", align_bytes=64)
+                        scales = pools["dgi_mx"].tile([P, COLS], U8, name="scales", align_bytes=64)
+                        quantise(nc, pools, dgi[d][:], E5M2_X4, codes[:], scales[:])
+                        for m in range(M_TILES):
+                            m_cols = slice(m * M_TILE, (m + 1) * M_TILE)
+                            nc.tensor.matmul_mx(
+                                out=acc[(gate, m)][:],
+                                lhsT=codes[:, m_cols].bitcast(E5M2_X4),
+                                lhsT_scale=scales[:, m_cols],
+                                rhs=agg_codes[:, nb, d, :].bitcast(E4M3_X4),
+                                rhs_scale=agg_scales[:, nb, d, :],
+                                start=(nb == 0 and d == 0),
+                                stop=(nb == NODE_BLOCKS - 1 and d == DIRS - 1),
+                            )
+
+            for gate in (Z, C, R):
+                for m in range(M_TILES):
+                    result = pools["result"].tile([M_TILE, FEAT], F32, name="result")
+                    nc.scalar.copy(out=result[:], in_=acc[(gate, m)][:])
+                    first = gate * FEAT + cb * COLS + m * M_TILE
+                    nc.sync.dma_start(out=out[first : first + M_TILE, :], in_=result[:])

@@ -1,6 +1,7 @@
 from contextlib import ExitStack
 
 import concourse.mybir as mybir
+from concourse.masks import make_identity
 
 F32 = mybir.dt.float32
 BF16 = mybir.dt.bfloat16
@@ -26,6 +27,8 @@ COLS = 256
 COL_BLOCKS = FEAT // COLS
 M_TILE = 128
 M_TILES = COLS // M_TILE
+BANK = 512
+BANKS_OF_CHUNK = PACK * COLS // BANK
 RUN = 4
 
 FLOPS = 2 * DIRS * NODES * GATES * FEAT * FEAT
@@ -77,6 +80,9 @@ def tile_graphconvolution_pb_v_kernel(
         }
         psum = ctx.enter_context(tc.psum_pool(name="psum", bufs=1))
 
+        identity = pools["agg_mx"].tile([P, P], F32)
+        make_identity(nc, identity[:])
+
         agg_codes = pools["agg_mx"].tile([P, NODE_BLOCKS, DIRS, FEAT], U32, align_bytes=64)
         agg_scales = pools["agg_mx"].tile([P, NODE_BLOCKS, DIRS, FEAT], U8, align_bytes=64)
 
@@ -118,6 +124,21 @@ def tile_graphconvolution_pb_v_kernel(
                         )
 
 
+                def flat(held):
+                    return held[:].rearrange("p j o -> p (j o)")
+
+                c_sum = []
+                for b in range(BANKS_OF_CHUNK):
+                    c_sum.append(psum.tile([P, BANK], F32, name="c_sum%d" % b, tag="c_sum%d" % b))
+                    for d in range(DIRS):
+                        nc.tensor.matmul(
+                            out=c_sum[b][:],
+                            lhsT=identity[:],
+                            rhs=flat(c[d])[:, b * BANK : (b + 1) * BANK],
+                            start=(d == 0),
+                            stop=(d == DIRS - 1),
+                        )
+
                 zch = []
                 for d in range(DIRS):
                     zch.append(
@@ -126,34 +147,29 @@ def tile_graphconvolution_pb_v_kernel(
                     nc.vector.tensor_tensor(out=zch[d][:], in0=c[d][:], in1=h[:], op=ALU.subtract)
                 for d in range(DIRS):
                     nc.vector.tensor_tensor(out=zch[d][:], in0=z[d][:], in1=zch[d][:], op=ALU.mult)
-
-                for d in range(DIRS):
-                    nc.vector.scalar_tensor_tensor(
-                        out=r[d][:], in0=r[d][:], scalar=1.0, in1=r[d][:],
-                        op0=ALU.subtract, op1=ALU.mult,
-                    )
-
-                new = []
-                for d in range(DIRS):
-                    new.append(
-                        pools["work"].tile([P, PACK, COLS], F32, name="new", tag="new", bufs=2 * DIRS)
-                    )
-                    nc.vector.tensor_tensor(out=new[d][:], in0=c[d][:], in1=zch[d][:], op=ALU.subtract)
                     nc.scalar.activation(out=c[d][:], in_=c[d][:], func=ACT.Square)
+                for d in range(DIRS):
+                    nc.scalar.activation(out=r[d][:], in_=r[d][:], func=ACT.Square, bias=-0.5)
 
                 def times_hn(d):
                     nc.vector.scalar_tensor_tensor(
-                        out=r[d][:], in0=r[d][:], scalar=-1.0, in1=h_n[:],
-                        op0=ALU.mult, op1=ALU.mult,
+                        out=r[d][:], in0=r[d][:], scalar=0.25, in1=h_n[:],
+                        op0=ALU.subtract, op1=ALU.mult,
                     )
 
-                tot = new[0]
+                tot = pools["work"].tile([P, PACK, COLS], F32, name="tot")
+                dh = pools["work"].tile([P, PACK, COLS], F32, name="dh")
+                nc.vector.tensor_tensor(out=tot[:], in0=zch[0][:], in1=zch[1][:], op=ALU.add)
                 nc.vector.tensor_tensor(out=gt[:], in0=g[:], in1=gt[:], op=ALU.mult)
-                nc.vector.tensor_tensor(out=tot[:], in0=new[0][:], in1=new[1][:], op=ALU.add)
+                nc.vector.tensor_tensor(out=tot[:], in0=tot[:], in1=zch[2][:], op=ALU.add)
                 times_hn(0)
-                nc.vector.tensor_tensor(out=tot[:], in0=tot[:], in1=new[2][:], op=ALU.add)
+                for b in range(BANKS_OF_CHUNK):
+                    bank_cols = slice(b * BANK, (b + 1) * BANK)
+                    nc.vector.tensor_tensor(
+                        out=flat(tot)[:, bank_cols], in0=c_sum[b][:], in1=flat(tot)[:, bank_cols],
+                        op=ALU.subtract,
+                    )
                 times_hn(1)
-                dh = new[1]
                 nc.vector.scalar_tensor_tensor(
                     out=dh[:], in0=tot[:], scalar=0.0, in1=gt[:], op0=ALU.is_gt, op1=ALU.mult
                 )
@@ -172,7 +188,10 @@ def tile_graphconvolution_pb_v_kernel(
                         op0=ALU.subtract, op1=ALU.mult,
                     )
                 for d in range(DIRS):
-                    nc.vector.tensor_tensor(out=r[d][:], in0=c[d][:], in1=r[d][:], op=ALU.mult)
+                    nc.vector.scalar_tensor_tensor(
+                        out=r[d][:], in0=r[d][:], scalar=-1.0, in1=c[d][:],
+                        op0=ALU.mult, op1=ALU.mult,
+                    )
 
                 for gate, dgi in ((Z, zch), (C, c), (R, r)):
                     for d in range(DIRS):

@@ -48,15 +48,18 @@ def load_rows(nc, pool, rows, dtype, name):
     return held
 
 
-def quantise(nc, pools, values, x4_dtype, codes, scales):
+def regroup(nc, pool, values):
     width = values.shape[2]
-    grouped = pools["grouped"].tile(
-        [P, width, PACK], BF16, name="grouped%d" % width, tag="grouped%d" % width, align_bytes=64
-    )
+    name = "grouped%d" % width
+    grouped = pool.tile([P, width, PACK], BF16, name=name, tag=name, align_bytes=64)
     nc.scalar.copy(
         out=grouped[:].rearrange("p (c i) j -> p c j i", i=RUN),
         in_=values.rearrange("p j (c i) -> p c j i", i=RUN),
     )
+    return grouped
+
+
+def quantise(nc, grouped, x4_dtype, codes, scales):
     nc.vector.quantize_mx(
         out=codes.bitcast(x4_dtype),
         scales=scales,
@@ -73,7 +76,8 @@ def tile_graphconvolution_pb_v_kernel(
             "gate": ctx.enter_context(tc.tile_pool(name="gate", bufs=2 * DIRS)),
             "node": ctx.enter_context(tc.tile_pool(name="node", bufs=2)),
             "work": ctx.enter_context(tc.tile_pool(name="work", bufs=2)),
-            "grouped": ctx.enter_context(tc.tile_pool(name="grouped", bufs=4)),
+            "grouped": ctx.enter_context(tc.tile_pool(name="grouped", bufs=2 * DIRS)),
+            "agg_grouped": ctx.enter_context(tc.tile_pool(name="agg_grouped", bufs=2)),
             "dgi_mx": ctx.enter_context(tc.tile_pool(name="dgi_mx", bufs=GATES * DIRS)),
             "agg_mx": ctx.enter_context(tc.tile_pool(name="agg_mx", bufs=1)),
             "result": ctx.enter_context(tc.tile_pool(name="result", bufs=4)),
@@ -119,7 +123,7 @@ def tile_graphconvolution_pb_v_kernel(
                     for d in range(DIRS):
                         agg_rows = load_rows(nc, pools["work"], agg[d, 0, rows, :], BF16, "agg_rows")
                         quantise(
-                            nc, pools, agg_rows[:], E4M3_X4,
+                            nc, regroup(nc, pools["agg_grouped"], agg_rows[:]), E4M3_X4,
                             agg_codes[:, nb, d, :], agg_scales[:, nb, d, :],
                         )
 
@@ -180,39 +184,48 @@ def tile_graphconvolution_pb_v_kernel(
                         out=z[d][:], in0=z[d][:], scalar=1.0, in1=dh[:],
                         op0=ALU.subtract, op1=ALU.mult,
                     )
+                def multiply(gate, d, grouped):
+                    codes = pools["dgi_mx"].tile([P, COLS], U32, name="codes", align_bytes=64)
+                    scales = pools["dgi_mx"].tile([P, COLS], U8, name="scales", align_bytes=64)
+                    quantise(nc, grouped, E5M2_X4, codes[:], scales[:])
+                    last = nb == NODE_BLOCKS - 1 and d == DIRS - 1
+                    for m in range(M_TILES):
+                        m_cols = slice(m * M_TILE, (m + 1) * M_TILE)
+                        nc.tensor.matmul_mx(
+                            out=acc[(gate, m)][:],
+                            lhsT=codes[:, m_cols].bitcast(E5M2_X4),
+                            lhsT_scale=scales[:, m_cols],
+                            rhs=agg_codes[:, nb, d, :].bitcast(E4M3_X4),
+                            rhs_scale=agg_scales[:, nb, d, :],
+                            start=(nb == 0 and d == 0),
+                            stop=last,
+                        )
+                        if last:
+                            result = pools["result"].tile([M_TILE, FEAT], F32, name="result")
+                            nc.scalar.copy(out=result[:], in_=acc[(gate, m)][:])
+                            first = gate * FEAT + cb * COLS + m * M_TILE
+                            nc.sync.dma_start(out=out[first : first + M_TILE, :], in_=result[:])
+
+
+                dz = []
                 for d in range(DIRS):
                     nc.vector.tensor_tensor(out=zch[d][:], in0=z[d][:], in1=zch[d][:], op=ALU.mult)
+                    dz.append(regroup(nc, pools["grouped"], zch[d][:]))
+                dc = []
                 for d in range(DIRS):
                     nc.vector.scalar_tensor_tensor(
                         out=c[d][:], in0=c[d][:], scalar=1.0, in1=z[d][:],
                         op0=ALU.subtract, op1=ALU.mult,
                     )
+                    dc.append(regroup(nc, pools["grouped"], c[d][:]))
+                    multiply(Z, d, dz[d])
+                dr = []
                 for d in range(DIRS):
                     nc.vector.scalar_tensor_tensor(
                         out=r[d][:], in0=r[d][:], scalar=-1.0, in1=c[d][:],
                         op0=ALU.mult, op1=ALU.mult,
                     )
-
-                for gate, dgi in ((Z, zch), (C, c), (R, r)):
-                    for d in range(DIRS):
-                        codes = pools["dgi_mx"].tile([P, COLS], U32, name="codes", align_bytes=64)
-                        scales = pools["dgi_mx"].tile([P, COLS], U8, name="scales", align_bytes=64)
-                        quantise(nc, pools, dgi[d][:], E5M2_X4, codes[:], scales[:])
-                        for m in range(M_TILES):
-                            m_cols = slice(m * M_TILE, (m + 1) * M_TILE)
-                            nc.tensor.matmul_mx(
-                                out=acc[(gate, m)][:],
-                                lhsT=codes[:, m_cols].bitcast(E5M2_X4),
-                                lhsT_scale=scales[:, m_cols],
-                                rhs=agg_codes[:, nb, d, :].bitcast(E4M3_X4),
-                                rhs_scale=agg_scales[:, nb, d, :],
-                                start=(nb == 0 and d == 0),
-                                stop=(nb == NODE_BLOCKS - 1 and d == DIRS - 1),
-                            )
-
-            for gate in (Z, C, R):
-                for m in range(M_TILES):
-                    result = pools["result"].tile([M_TILE, FEAT], F32, name="result")
-                    nc.scalar.copy(out=result[:], in_=acc[(gate, m)][:])
-                    first = gate * FEAT + cb * COLS + m * M_TILE
-                    nc.sync.dma_start(out=out[first : first + M_TILE, :], in_=result[:])
+                    dr.append(regroup(nc, pools["grouped"], r[d][:]))
+                    multiply(C, d, dc[d])
+                for d in range(DIRS):
+                    multiply(R, d, dr[d])

@@ -48,14 +48,22 @@ def load_rows(nc, pool, rows, dtype, name):
     return held
 
 
-def regroup(nc, pool, values):
-    width = values.shape[2]
+def grouped_tile(pool, width):
     name = "grouped%d" % width
-    grouped = pool.tile([P, width, PACK], BF16, name=name, tag=name, align_bytes=64)
-    nc.scalar.copy(
-        out=grouped[:].rearrange("p (c i) j -> p c j i", i=RUN),
-        in_=values.rearrange("p j (c i) -> p c j i", i=RUN),
-    )
+    return pool.tile([P, width, PACK], BF16, name=name, tag=name, align_bytes=64)
+
+
+def by_token(values):
+    return values.rearrange("p j (c i) -> p c j i", i=RUN)
+
+
+def by_column(grouped):
+    return grouped[:].rearrange("p (c i) j -> p c j i", i=RUN)
+
+
+def regroup(nc, pool, values):
+    grouped = grouped_tile(pool, values.shape[2])
+    nc.scalar.copy(out=by_column(grouped), in_=by_token(values))
     return grouped
 
 
@@ -155,6 +163,8 @@ def tile_graphconvolution_pb_v_kernel(
                 for d in range(DIRS):
                     nc.scalar.activation(out=r[d][:], in_=r[d][:], func=ACT.Square, bias=-0.5)
 
+                nc.scalar.mul(out=h_n[:], in_=h_n[:], mul=-1.0)
+
                 def times_hn(d):
                     nc.vector.scalar_tensor_tensor(
                         out=r[d][:], in0=r[d][:], scalar=0.25, in1=h_n[:],
@@ -209,8 +219,11 @@ def tile_graphconvolution_pb_v_kernel(
 
                 dz = []
                 for d in range(DIRS):
-                    nc.vector.tensor_tensor(out=zch[d][:], in0=z[d][:], in1=zch[d][:], op=ALU.mult)
-                    dz.append(regroup(nc, pools["grouped"], zch[d][:]))
+                    dz.append(grouped_tile(pools["grouped"], COLS))
+                    nc.vector.tensor_tensor(
+                        out=by_column(dz[d]), in0=by_token(z[d][:]), in1=by_token(zch[d][:]),
+                        op=ALU.mult,
+                    )
                 dc = []
                 for d in range(DIRS):
                     nc.vector.scalar_tensor_tensor(
@@ -221,11 +234,11 @@ def tile_graphconvolution_pb_v_kernel(
                     multiply(Z, d, dz[d])
                 dr = []
                 for d in range(DIRS):
-                    nc.vector.scalar_tensor_tensor(
-                        out=r[d][:], in0=r[d][:], scalar=-1.0, in1=c[d][:],
-                        op0=ALU.mult, op1=ALU.mult,
+                    dr.append(grouped_tile(pools["grouped"], COLS))
+                    nc.vector.tensor_tensor(
+                        out=by_column(dr[d]), in0=by_token(r[d][:]), in1=by_token(c[d][:]),
+                        op=ALU.mult,
                     )
-                    dr.append(regroup(nc, pools["grouped"], r[d][:]))
                     multiply(C, d, dc[d])
                 for d in range(DIRS):
                     multiply(R, d, dr[d])

@@ -48,22 +48,14 @@ def load_rows(nc, pool, rows, dtype, name):
     return held
 
 
-def grouped_tile(pool, width):
-    name = "grouped%d" % width
-    return pool.tile([P, width, PACK], BF16, name=name, tag=name, align_bytes=64)
-
-
-def by_token(values):
-    return values.rearrange("p j (c i) -> p c j i", i=RUN)
-
-
-def by_column(grouped):
-    return grouped[:].rearrange("p (c i) j -> p c j i", i=RUN)
-
-
 def regroup(nc, pool, values):
-    grouped = grouped_tile(pool, values.shape[2])
-    nc.scalar.copy(out=by_column(grouped), in_=by_token(values))
+    width = values.shape[2]
+    name = "grouped%d" % width
+    grouped = pool.tile([P, width, PACK], BF16, name=name, tag=name, align_bytes=64)
+    nc.scalar.copy(
+        out=grouped[:].rearrange("p (c i) j -> p c j i", i=RUN),
+        in_=values.rearrange("p j (c i) -> p c j i", i=RUN),
+    )
     return grouped
 
 
@@ -85,7 +77,7 @@ def tile_graphconvolution_pb_v_kernel(
             "node": ctx.enter_context(tc.tile_pool(name="node", bufs=2)),
             "work": ctx.enter_context(tc.tile_pool(name="work", bufs=2)),
             "grouped": ctx.enter_context(tc.tile_pool(name="grouped", bufs=2 * DIRS)),
-            "agg_grouped": ctx.enter_context(tc.tile_pool(name="agg_grouped", bufs=2)),
+            "agg_grouped": ctx.enter_context(tc.tile_pool(name="agg_grouped", bufs=DIRS)),
             "dgi_mx": ctx.enter_context(tc.tile_pool(name="dgi_mx", bufs=GATES * DIRS)),
             "agg_mx": ctx.enter_context(tc.tile_pool(name="agg_mx", bufs=1)),
             "result": ctx.enter_context(tc.tile_pool(name="result", bufs=4)),
@@ -122,18 +114,15 @@ def tile_graphconvolution_pb_v_kernel(
                 for d in range(DIRS):
                     c.append(load_gate(d, C, "c"))
                     z.append(load_gate(d, Z, "z"))
-                r = [load_gate(d, R, "r") for d in range(DIRS)]
                 g = load_rows(nc, pools["node"], grad_out[rows, 0, cols], BF16, "g")
                 gt = load_rows(nc, pools["node"], t[rows, 0, cols], F32, "gt")
                 h_n = load_rows(nc, pools["node"], hn[0, rows, cols], F32, "h_n")
-
+                r = [load_gate(d, R, "r") for d in range(DIRS)]
+                agg_grouped = []
                 if cb == 0:
                     for d in range(DIRS):
                         agg_rows = load_rows(nc, pools["work"], agg[d, 0, rows, :], BF16, "agg_rows")
-                        quantise(
-                            nc, regroup(nc, pools["agg_grouped"], agg_rows[:]), E4M3_X4,
-                            agg_codes[:, nb, d, :], agg_scales[:, nb, d, :],
-                        )
+                        agg_grouped.append(regroup(nc, pools["agg_grouped"], agg_rows[:]))
 
 
                 def flat(held):
@@ -163,31 +152,20 @@ def tile_graphconvolution_pb_v_kernel(
                 for d in range(DIRS):
                     nc.scalar.activation(out=r[d][:], in_=r[d][:], func=ACT.Square, bias=-0.5)
 
-                nc.scalar.mul(out=h_n[:], in_=h_n[:], mul=-1.0)
-
-                def times_hn(d):
-                    nc.vector.scalar_tensor_tensor(
-                        out=r[d][:], in0=r[d][:], scalar=0.25, in1=h_n[:],
-                        op0=ALU.subtract, op1=ALU.mult,
-                    )
-
                 tot = pools["work"].tile([P, PACK, COLS], F32, name="tot")
                 dh = pools["work"].tile([P, PACK, COLS], F32, name="dh")
                 nc.vector.tensor_tensor(out=tot[:], in0=zch[0][:], in1=zch[1][:], op=ALU.add)
                 nc.vector.tensor_tensor(out=gt[:], in0=g[:], in1=gt[:], op=ALU.mult)
                 nc.vector.tensor_tensor(out=tot[:], in0=tot[:], in1=zch[2][:], op=ALU.add)
-                times_hn(0)
                 for b in range(BANKS_OF_CHUNK):
                     bank_cols = slice(b * BANK, (b + 1) * BANK)
                     nc.vector.tensor_tensor(
                         out=flat(tot)[:, bank_cols], in0=c_sum[b][:], in1=flat(tot)[:, bank_cols],
                         op=ALU.subtract,
                     )
-                times_hn(1)
                 nc.vector.scalar_tensor_tensor(
                     out=dh[:], in0=tot[:], scalar=0.0, in1=gt[:], op0=ALU.is_gt, op1=ALU.mult
                 )
-                times_hn(2)
 
                 for d in range(DIRS):
                     nc.vector.scalar_tensor_tensor(
@@ -219,10 +197,12 @@ def tile_graphconvolution_pb_v_kernel(
 
                 dz = []
                 for d in range(DIRS):
-                    dz.append(grouped_tile(pools["grouped"], COLS))
-                    nc.vector.tensor_tensor(
-                        out=by_column(dz[d]), in0=by_token(z[d][:]), in1=by_token(zch[d][:]),
-                        op=ALU.mult,
+                    nc.vector.tensor_tensor(out=zch[d][:], in0=z[d][:], in1=zch[d][:], op=ALU.mult)
+                    dz.append(regroup(nc, pools["grouped"], zch[d][:]))
+                for d in range(DIRS):
+                    nc.vector.scalar_tensor_tensor(
+                        out=r[d][:], in0=r[d][:], scalar=0.25, in1=h_n[:],
+                        op0=ALU.subtract, op1=ALU.mult,
                     )
                 dc = []
                 for d in range(DIRS):
@@ -231,14 +211,19 @@ def tile_graphconvolution_pb_v_kernel(
                         op0=ALU.subtract, op1=ALU.mult,
                     )
                     dc.append(regroup(nc, pools["grouped"], c[d][:]))
+                    if cb == 0:
+                        quantise(
+                            nc, agg_grouped[d], E4M3_X4,
+                            agg_codes[:, nb, d, :], agg_scales[:, nb, d, :],
+                        )
                     multiply(Z, d, dz[d])
                 dr = []
                 for d in range(DIRS):
-                    dr.append(grouped_tile(pools["grouped"], COLS))
-                    nc.vector.tensor_tensor(
-                        out=by_column(dr[d]), in0=by_token(r[d][:]), in1=by_token(c[d][:]),
-                        op=ALU.mult,
+                    nc.vector.scalar_tensor_tensor(
+                        out=r[d][:], in0=r[d][:], scalar=-1.0, in1=c[d][:],
+                        op0=ALU.mult, op1=ALU.mult,
                     )
+                    dr.append(regroup(nc, pools["grouped"], r[d][:]))
                     multiply(C, d, dc[d])
                 for d in range(DIRS):
                     multiply(R, d, dr[d])

@@ -128,44 +128,60 @@ def tile_graphconvolution_pb_v_kernel(
                 def flat(held):
                     return held[:].rearrange("p j o -> p (j o)")
 
-                c_sum = []
-                for b in range(BANKS_OF_CHUNK):
-                    c_sum.append(psum.tile([P, BANK], F32, name="c_sum%d" % b, tag="c_sum%d" % b))
-                    for d in range(DIRS):
-                        nc.tensor.matmul(
-                            out=c_sum[b][:],
-                            lhsT=identity[:],
-                            rhs=flat(c[d])[:, b * BANK : (b + 1) * BANK],
-                            start=(d == 0),
-                            stop=(d == DIRS - 1),
-                        )
+                tot_t = []
+                for fb in range(M_TILES):
+                    tot_t.append(psum.tile([P, BANK], F32, name="spare%d" % fb, tag="spare%d" % fb))
+
+                def add_transposed(held, first, last):
+                    for fb in range(M_TILES):
+                        for j in range(PACK):
+                            nc.tensor.matmul(
+                                out=tot_t[fb][:, j * P : (j + 1) * P],
+                                lhsT=held[:, j, fb * P : (fb + 1) * P],
+                                rhs=identity[:],
+                                is_transpose=True,
+                                start=(first and j == 0),
+                                stop=(last and j == PACK - 1),
+                            )
+
+                for d in range(DIRS):
+                    add_transposed(c[d], d == 0, False)
+                for d in range(DIRS):
+                    nc.scalar.activation(out=r[d][:], in_=r[d][:], func=ACT.Square, bias=-0.5)
 
                 zch = []
                 for d in range(DIRS):
                     zch.append(
                         pools["work"].tile([P, PACK, COLS], F32, name="zch", tag="zch", bufs=2 * DIRS)
                     )
-                    nc.vector.tensor_tensor(out=zch[d][:], in0=c[d][:], in1=h[:], op=ALU.subtract)
+                    nc.vector.tensor_tensor(out=zch[d][:], in0=h[:], in1=c[d][:], op=ALU.subtract)
                 for d in range(DIRS):
                     nc.vector.tensor_tensor(out=zch[d][:], in0=z[d][:], in1=zch[d][:], op=ALU.mult)
-                    nc.scalar.activation(out=c[d][:], in_=c[d][:], func=ACT.Square)
-                for d in range(DIRS):
-                    nc.scalar.activation(out=r[d][:], in_=r[d][:], func=ACT.Square, bias=-0.5)
+                    add_transposed(zch[d], False, d == DIRS - 1)
 
-                tot = pools["work"].tile([P, PACK, COLS], F32, name="tot")
                 dh = pools["work"].tile([P, PACK, COLS], F32, name="dh")
-                nc.vector.tensor_tensor(out=tot[:], in0=zch[0][:], in1=zch[1][:], op=ALU.add)
                 nc.vector.tensor_tensor(out=gt[:], in0=g[:], in1=gt[:], op=ALU.mult)
-                nc.vector.tensor_tensor(out=tot[:], in0=tot[:], in1=zch[2][:], op=ALU.add)
-                for b in range(BANKS_OF_CHUNK):
-                    bank_cols = slice(b * BANK, (b + 1) * BANK)
-                    nc.vector.tensor_tensor(
-                        out=flat(tot)[:, bank_cols], in0=c_sum[b][:], in1=flat(tot)[:, bank_cols],
-                        op=ALU.subtract,
+                for d in range(DIRS):
+                    nc.vector.scalar_tensor_tensor(
+                        out=r[d][:], in0=r[d][:], scalar=0.25, in1=h_n[:],
+                        op0=ALU.subtract, op1=ALU.mult,
                     )
-                nc.vector.scalar_tensor_tensor(
-                    out=dh[:], in0=tot[:], scalar=0.0, in1=gt[:], op0=ALU.is_gt, op1=ALU.mult
-                )
+                for fb in range(M_TILES):
+                    tot_t_sb = pools["work"].tile([P, BANK], F32, name="tot_t_sb")
+                    nc.scalar.copy(out=tot_t_sb[:], in_=tot_t[fb][:])
+                    tot = psum.tile([P, BANK], F32, name="spare%d" % fb, tag="spare%d" % fb)
+                    for j in range(PACK):
+                        nc.tensor.transpose(
+                            tot[:, j * P : (j + 1) * P], tot_t_sb[:, j * P : (j + 1) * P], identity[:]
+                        )
+                    f_cols = slice(fb * P, (fb + 1) * P)
+                    nc.vector.scalar_tensor_tensor(
+                        out=dh[:, :, f_cols], in0=tot[:].rearrange("p (j o) -> p j o", j=PACK),
+                        scalar=0.0, in1=gt[:, :, f_cols], op0=ALU.is_gt, op1=ALU.mult,
+                    )
+
+                for d in range(DIRS):
+                    nc.scalar.activation(out=c[d][:], in_=c[d][:], func=ACT.Square)
 
                 for d in range(DIRS):
                     nc.vector.scalar_tensor_tensor(
@@ -197,13 +213,11 @@ def tile_graphconvolution_pb_v_kernel(
 
                 dz = []
                 for d in range(DIRS):
-                    nc.vector.tensor_tensor(out=zch[d][:], in0=z[d][:], in1=zch[d][:], op=ALU.mult)
-                    dz.append(regroup(nc, pools["grouped"], zch[d][:]))
-                for d in range(DIRS):
                     nc.vector.scalar_tensor_tensor(
-                        out=r[d][:], in0=r[d][:], scalar=0.25, in1=h_n[:],
-                        op0=ALU.subtract, op1=ALU.mult,
+                        out=zch[d][:], in0=z[d][:], scalar=-1.0, in1=zch[d][:],
+                        op0=ALU.mult, op1=ALU.mult,
                     )
+                    dz.append(regroup(nc, pools["grouped"], zch[d][:]))
                 dc = []
                 for d in range(DIRS):
                     nc.vector.scalar_tensor_tensor(

@@ -28,7 +28,8 @@ COL_BLOCKS = FEAT // COLS
 M_TILE = 128
 M_TILES = COLS // M_TILE
 BANK = 512
-BANKS_OF_CHUNK = PACK * COLS // BANK
+WIDTH = PACK * COLS
+HALVES = WIDTH // BANK
 RUN = 4
 
 FLOPS = 2 * DIRS * NODES * GATES * FEAT * FEAT
@@ -41,203 +42,410 @@ BYTES = (
 )
 
 
-def load_rows(nc, pool, rows, dtype, name):
-    width = rows.shape[1]
-    held = pool.tile([P, PACK, width], dtype, name=name, tag=name)
-    nc.sync.dma_start(out=held[:], in_=rows.rearrange("(p j) o -> p j o", j=PACK))
-    return held
-
-
-def regroup(nc, pool, values):
-    width = values.shape[2]
-    name = "grouped%d" % width
-    grouped = pool.tile([P, width, PACK], BF16, name=name, tag=name, align_bytes=64)
-    nc.scalar.copy(
-        out=grouped[:].rearrange("p (c i) j -> p c j i", i=RUN),
-        in_=values.rearrange("p j (c i) -> p c j i", i=RUN),
-    )
-    return grouped
-
-
-def quantise(nc, grouped, x4_dtype, codes, scales):
-    nc.vector.quantize_mx(
-        out=codes.bitcast(x4_dtype),
-        scales=scales,
-        in_=grouped[:].rearrange("p o j -> p (o j)"),
-    )
-
-
 def tile_graphconvolution_pb_v_kernel(
     tc, agg, x, wih, whh, bih, bhh, wh, bh, gates, hn, t, grad_out, out
 ):
     nc = tc.nc
+    chunks = [(cb, nb) for cb in range(COL_BLOCKS) for nb in range(NODE_BLOCKS)]
+    n_chunks = len(chunks)
+    all_dirs = slice(0, DIRS)
     with ExitStack() as ctx:
-        pools = {
-            "gate": ctx.enter_context(tc.tile_pool(name="gate", bufs=2 * DIRS)),
-            "node": ctx.enter_context(tc.tile_pool(name="node", bufs=2)),
-            "work": ctx.enter_context(tc.tile_pool(name="work", bufs=2)),
-            "grouped": ctx.enter_context(tc.tile_pool(name="grouped", bufs=2 * DIRS)),
-            "agg_grouped": ctx.enter_context(tc.tile_pool(name="agg_grouped", bufs=DIRS)),
-            "dgi_mx": ctx.enter_context(tc.tile_pool(name="dgi_mx", bufs=GATES * DIRS)),
-            "agg_mx": ctx.enter_context(tc.tile_pool(name="agg_mx", bufs=1)),
-            "result": ctx.enter_context(tc.tile_pool(name="result", bufs=4)),
-        }
+        gate_pool = ctx.enter_context(tc.tile_pool(name="gate", bufs=2))
+        node_pool = ctx.enter_context(tc.tile_pool(name="node", bufs=2))
+        work_pool = ctx.enter_context(tc.tile_pool(name="work", bufs=2))
+        grouped_pool = ctx.enter_context(tc.tile_pool(name="grouped", bufs=3 * DIRS))
+        agg_pool = ctx.enter_context(tc.tile_pool(name="agg", bufs=DIRS))
+        mx_pool = ctx.enter_context(tc.tile_pool(name="dgi_mx", bufs=GATES * DIRS))
+        keep_pool = ctx.enter_context(tc.tile_pool(name="keep", bufs=1))
+        result_pool = ctx.enter_context(tc.tile_pool(name="result", bufs=GATES * M_TILES))
         psum = ctx.enter_context(tc.psum_pool(name="psum", bufs=1))
+        ctx.enter_context(tc.manual_schedule())
 
-        identity = pools["agg_mx"].tile([P, P], F32)
+        identity = keep_pool.tile([P, P], F32, name="identity")
         make_identity(nc, identity[:])
+        identity_bf = keep_pool.tile([P, P], BF16, name="identity_bf")
+        make_identity(nc, identity_bf[:])
+        minus_identity = keep_pool.tile([P, P], F32, name="minus_identity")
+        nc.scalar.mul(out=minus_identity[:], in_=identity[:], mul=-1.0)
+        agg_codes = keep_pool.tile([P, NODE_BLOCKS, DIRS, FEAT], U32, name="agg_codes", align_bytes=64)
+        agg_scales = keep_pool.tile([P, NODE_BLOCKS, DIRS, FEAT], U8, name="agg_scales", align_bytes=64)
 
-        agg_codes = pools["agg_mx"].tile([P, NODE_BLOCKS, DIRS, FEAT], U32, align_bytes=64)
-        agg_scales = pools["agg_mx"].tile([P, NODE_BLOCKS, DIRS, FEAT], U8, align_bytes=64)
+        state = [dict() for i in range(n_chunks)]
+        acc = {}
 
-        for cb in range(COL_BLOCKS):
-            cols = slice(cb * COLS, (cb + 1) * COLS)
-            acc = {}
-            for gate in range(GATES):
-                for m in range(M_TILES):
+        def rows_view(rows):
+            return rows.rearrange("(p j) o -> p j o", j=PACK)
+
+        def where(i):
+            cb, nb = chunks[i]
+            return slice(nb * K_PASS, (nb + 1) * K_PASS), slice(cb * COLS, (cb + 1) * COLS)
+
+        def load_node(i, name, dtype, src, bufs):
+            held = node_pool.tile([P, PACK, COLS], dtype, name=name, tag=name, bufs=bufs)
+            nc.sync.dma_start(out=held[:], in_=rows_view(src))
+            state[i][name] = held
+
+        def load_h(i):
+            rows, cols = where(i)
+            load_node(i, "h", BF16, x[rows, 0, cols], n_chunks)
+
+        def load_gate(i, name, gate, dirs=(0, 1, 2)):
+            cb, nb = chunks[i]
+            rows, cols = where(i)
+            if name not in state[i]:
+                state[i][name] = gate_pool.tile([P, DIRS, PACK, COLS], F32, name=name, tag=name)
+            first = gate * FEAT + cb * COLS
+            for d in dirs:
+                nc.sync.dma_start(
+                    out=state[i][name][:, d], in_=rows_view(gates[d, 0, rows, first : first + COLS])
+                )
+
+        def load_dh_inputs(i):
+            rows, cols = where(i)
+            load_node(i, "g", BF16, grad_out[rows, 0, cols], 2)
+            load_node(i, "gt", F32, t[rows, 0, cols], 2)
+
+        def load_r(i):
+            rows, cols = where(i)
+            load_gate(i, "r", R)
+            load_node(i, "h_n", F32, hn[0, rows, cols], 2)
+
+        def load_agg(i, dirs=(0, 1, 2)):
+            cb, nb = chunks[i]
+            rows, cols = where(i)
+            if cb > 0:
+                return
+            state[i].setdefault("agg_rows", [])
+            for d in dirs:
+                agg_rows = agg_pool.tile([P, PACK, FEAT], BF16, name="agg_rows", tag="agg_rows")
+                nc.sync.dma_start(out=agg_rows[:], in_=rows_view(agg[d, 0, rows, :]))
+                state[i]["agg_rows"].append(agg_rows)
+
+        def pieces(split):
+            if split:
+                return [slice(d, d + 1) for d in range(DIRS)]
+            return [all_dirs]
+
+        def wide(held, ds):
+            return held[:, ds].rearrange("p d j o -> p d (j o)")
+
+        def shared(held, ds):
+            n = ds.stop - ds.start
+            return held[:].rearrange("p j o -> p (j o)").unsqueeze(1).to_broadcast([P, n, WIDTH])
+
+        def regroup(pool, values, tag, factor):
+            width = values.shape[2]
+            grouped = pool.tile([P, width, PACK], BF16, name=tag, tag=tag, align_bytes=64)
+            nc.scalar.activation(
+                out=grouped[:].rearrange("p (c i) j -> p c j i", i=RUN),
+                in_=values.rearrange("p j (c i) -> p c j i", i=RUN),
+                func=ACT.Copy, scale=factor,
+            )
+            return grouped
+
+        def quantise(grouped, x4_dtype, codes, scales):
+            nc.vector.quantize_mx(
+                out=codes.bitcast(x4_dtype), scales=scales,
+                in_=grouped[:].rearrange("p o j -> p (o j)"),
+            )
+
+        def spare(b, dtype, width):
+            return psum.tile([P, width], dtype, name="spare%d" % b, tag="spare%d" % b)
+
+        def transpose_h(i, bank):
+            h = state[i]["h"]
+            for fb in range(M_TILES):
+                for j in range(PACK):
+                    k = fb * PACK + j
+                    nc.tensor.transpose(
+                        bank[:, k * P : (k + 1) * P], h[:, j, fb * P : (fb + 1) * P], identity_bf[:]
+                    )
+            h_t = work_pool.tile([P, M_TILES, PACK, P], F32, name="h_t", tag="h_t")
+            nc.scalar.copy(out=h_t[:].rearrange("p f j q -> p (f j q)"), in_=bank[:])
+            state[i]["h_t"] = h_t
+
+        def difference(i, d, b):
+            st = state[i]
+            bank = spare(b, F32, BANK)
+            nc.tensor.matmul(
+                out=bank[:], lhsT=minus_identity[:],
+                rhs=st["c"][:, d].rearrange("p j o -> p (j o)")[:, b * BANK : (b + 1) * BANK],
+                start=True, stop=False,
+            )
+            per_bank = PACK // HALVES
+            for jj in range(per_bank):
+                for fb in range(M_TILES):
+                    first = jj * COLS + fb * P
+                    nc.tensor.matmul(
+                        out=bank[:, first : first + P], lhsT=st["h_t"][:, fb, b * per_bank + jj, :],
+                        rhs=identity[:], is_transpose=True,
+                        start=False, stop=(jj == per_bank - 1 and fb == M_TILES - 1),
+                    )
+            return bank
+
+        def new_zch(i):
+            state[i]["zch"] = work_pool.tile([P, DIRS, PACK, COLS], F32, name="zch", tag="zch")
+
+        def gated_difference(i, d, b, bank):
+            st = state[i]
+            part = slice(b * BANK, (b + 1) * BANK)
+            nc.vector.tensor_tensor(
+                out=st["zch"][:, d].rearrange("p j o -> p (j o)")[:, part],
+                in0=st["z"][:, d].rearrange("p j o -> p (j o)")[:, part],
+                in1=bank[:], op=ALU.mult,
+            )
+
+        def add_transposed(tot_t, fb, held, ds, first, last):
+            for d in range(ds.start, ds.stop):
+                for j in range(PACK):
+                    nc.tensor.matmul(
+                        out=tot_t[:, j * P : (j + 1) * P],
+                        lhsT=held[:, d, j, fb * P : (fb + 1) * P],
+                        rhs=identity[:],
+                        is_transpose=True,
+                        start=(first and d == ds.start and j == 0),
+                        stop=(last and d == ds.stop - 1 and j == PACK - 1),
+                    )
+
+        def square(i, name, bias):
+            held = state[i][name]
+            nc.scalar.activation(
+                out=wide(held, all_dirs), in_=wide(held, all_dirs), func=ACT.Square, bias=bias
+            )
+
+        def tot_back(i, fb):
+            st = state[i]
+            tot_t_sb = work_pool.tile([P, BANK], F32, name="tot_t_sb", tag="tot_t_sb")
+            nc.scalar.copy(out=tot_t_sb[:], in_=st["tot_t"][fb][:])
+            tot = spare(fb, F32, BANK)
+            for j in range(PACK):
+                nc.tensor.transpose(
+                    tot[:, j * P : (j + 1) * P], tot_t_sb[:, j * P : (j + 1) * P], identity[:]
+                )
+            st["tot"][fb] = tot
+
+        def mask(i, fb):
+            st = state[i]
+            f_cols = slice(fb * P, (fb + 1) * P)
+            nc.vector.scalar_tensor_tensor(
+                out=st["dh"][:, :, f_cols], in0=st["tot"][fb][:].rearrange("p (j o) -> p j o", j=PACK),
+                scalar=0.0, in1=st["gt"][:, :, f_cols], op0=ALU.is_gt, op1=ALU.mult,
+            )
+
+        def regroup_agg(i, d):
+            st = state[i]
+            st.setdefault("agg_grouped", []).append(regroup(agg_pool, st["agg_rows"][d][:], "agg_grouped", 1.0))
+
+        def quantise_agg(i):
+            cb, nb = chunks[i]
+            if cb > 0:
+                return
+            for d in range(DIRS):
+                quantise(
+                    state[i]["agg_grouped"][d], E4M3_X4,
+                    agg_codes[:, nb, d, :], agg_scales[:, nb, d, :],
+                )
+
+        def product(i, out_name, in0_name, scalar, op0, in1_name, ds, in1_shared=False):
+            st = state[i]
+            in1 = shared(st[in1_name], ds) if in1_shared else wide(st[in1_name], ds)
+            nc.vector.scalar_tensor_tensor(
+                out=wide(st[out_name], ds), in0=wide(st[in0_name], ds), scalar=scalar, in1=in1,
+                op0=op0, op1=ALU.mult,
+            )
+
+        def product_grouped(i, name, in0_name, in1_name, d):
+            st = state[i]
+            grouped = grouped_pool.tile([P, COLS, PACK], BF16, name="grouped", tag="grouped", align_bytes=64)
+            nc.vector.tensor_tensor(
+                out=grouped[:].rearrange("p (c i) j -> p c j i", i=RUN),
+                in0=st[in0_name][:, d].rearrange("p j (c i) -> p c j i", i=RUN),
+                in1=st[in1_name][:, d].rearrange("p j (c i) -> p c j i", i=RUN),
+                op=ALU.mult,
+            )
+            st.setdefault("grouped_" + name, []).append(grouped)
+
+        def regroup_gate(i, name, d):
+            st = state[i]
+            st.setdefault("grouped_" + name, []).append(regroup(grouped_pool, st[name][:, d], "grouped", -1.0))
+
+        def multiply(i, gate, name, d):
+            cb, nb = chunks[i]
+            codes = mx_pool.tile([P, COLS], U32, name="codes", tag="codes", align_bytes=64)
+            scales = mx_pool.tile([P, COLS], U8, name="scales", tag="scales", align_bytes=64)
+            quantise(state[i]["grouped_" + name][d], E5M2_X4, codes[:], scales[:])
+            for m in range(M_TILES):
+                if nb == 0 and d == 0:
                     acc[(gate, m)] = psum.tile(
                         [M_TILE, FEAT], F32, name="acc%d%d" % (gate, m), tag="acc%d%d" % (gate, m)
                     )
+                m_cols = slice(m * M_TILE, (m + 1) * M_TILE)
+                nc.tensor.matmul_mx(
+                    out=acc[(gate, m)][:],
+                    lhsT=codes[:, m_cols].bitcast(E5M2_X4),
+                    lhsT_scale=scales[:, m_cols],
+                    rhs=agg_codes[:, nb, d, :].bitcast(E4M3_X4),
+                    rhs_scale=agg_scales[:, nb, d, :],
+                    start=(nb == 0 and d == 0),
+                    stop=(nb == NODE_BLOCKS - 1 and d == DIRS - 1),
+                )
 
-            for nb in range(NODE_BLOCKS):
-                rows = slice(nb * K_PASS, (nb + 1) * K_PASS)
+        def store(i, gate, shared_out=False):
+            cb, nb = chunks[i]
+            if nb < NODE_BLOCKS - 1:
+                return
+            for m in range(M_TILES):
+                result = result_pool.tile([M_TILE, FEAT], F32, name="result", tag="result")
+                if shared_out and m == 0:
+                    nc.vector.tensor_copy(out=result[:], in_=acc[(gate, m)][:])
+                else:
+                    nc.scalar.copy(out=result[:], in_=acc[(gate, m)][:])
+                first = gate * FEAT + cb * COLS + m * M_TILE
+                nc.sync.dma_start(out=out[first : first + M_TILE, :], in_=result[:])
 
-                def load_gate(d, gate, name):
-                    first = gate * FEAT + cb * COLS
-                    return load_rows(
-                        nc, pools["gate"], gates[d, 0, rows, first : first + COLS], F32, name
-                    )
 
-                h = load_rows(nc, pools["node"], x[rows, 0, cols], BF16, "h")
-                c = []
-                z = []
+        def sum_into(i, fb, with_c, ds, last):
+            st = state[i]
+            if with_c:
+                st.setdefault("tot_t", {})[fb] = spare(fb, F32, BANK)
+                add_transposed(st["tot_t"][fb], fb, st["c"], all_dirs, True, False)
+            if ds is not None:
+                add_transposed(st["tot_t"][fb], fb, st["zch"], ds, False, last)
+
+        def new_dh(i):
+            state[i]["dh"] = work_pool.tile([P, PACK, COLS], F32, name="dh", tag="dh")
+            state[i]["tot"] = {}
+
+        def times_t(i):
+            st = state[i]
+            nc.vector.scalar_tensor_tensor(
+                out=st["gt"][:].rearrange("p j o -> p (j o)"), in0=st["g"][:].rearrange("p j o -> p (j o)"),
+                scalar=-1.0, in1=st["gt"][:].rearrange("p j o -> p (j o)"), op0=ALU.mult, op1=ALU.mult,
+            )
+
+        def times_hn(i):
+            product(i, "r", "r", 0.25, ALU.subtract, "h_n", all_dirs, in1_shared=True)
+
+        load_h(0)
+        load_gate(0, "c", C)
+        load_gate(0, "z", Z)
+        load_dh_inputs(0)
+        load_h(1)
+        load_gate(1, "c", C, (0,))
+        load_gate(1, "z", Z, (0,))
+        load_r(0)
+        load_gate(1, "c", C, (1,))
+        load_gate(1, "z", Z, (1,))
+        load_agg(0, (0, 1))
+        load_gate(1, "c", C, (2,))
+        load_agg(0, (2,))
+        load_gate(1, "z", Z, (2,))
+        load_h(2)
+        load_h(3)
+        load_dh_inputs(1)
+        load_r(1)
+        load_agg(1)
+
+        st = state[0]
+        for fb in range(M_TILES):
+            sum_into(0, fb, True, None, False)
+        new_zch(0)
+        for ds in pieces(True):
+            nc.vector.tensor_tensor(
+                out=wide(st["zch"], ds), in0=shared(st["h"], ds), in1=wide(st["c"], ds), op=ALU.subtract
+            )
+        square(0, "c", 0.0)
+        for ds in pieces(True):
+            nc.vector.tensor_tensor(
+                out=wide(st["zch"], ds), in0=wide(st["z"], ds), in1=wide(st["zch"], ds), op=ALU.mult
+            )
+            for fb in range(M_TILES):
+                sum_into(0, fb, False, ds, ds.stop == DIRS)
+        times_t(0)
+        new_dh(0)
+        for fb in range(M_TILES):
+            tot_back(0, fb)
+            mask(0, fb)
+        early_bank = psum.tile([P, 2 * BANK], BF16, name="acc00", tag="acc00")
+        transpose_h(1, early_bank)
+
+        for i in range(n_chunks):
+            nxt = i + 1
+            has_next = nxt < n_chunks
+            split = not has_next
+            banks = {}
+            has_agg = chunks[i][0] == 0
+
+            def differences(d):
+                if has_next:
+                    for b in range(HALVES):
+                        banks[b] = difference(nxt, d, b)
+
+            def gated_differences(d):
+                if has_next:
+                    for b in range(HALVES):
+                        gated_difference(nxt, d, b, banks[b])
+
+            if i > 0:
+                square(i, "c", 0.0)
+            if has_next:
+                new_zch(nxt)
+            differences(0)
+            product(i, "z", "z", 1.0, ALU.subtract, "dh", all_dirs, in1_shared=True)
+            if i == 0:
+                square(0, "r", -0.5)
+            if has_agg:
                 for d in range(DIRS):
-                    c.append(load_gate(d, C, "c"))
-                    z.append(load_gate(d, Z, "z"))
-                g = load_rows(nc, pools["node"], grad_out[rows, 0, cols], BF16, "g")
-                gt = load_rows(nc, pools["node"], t[rows, 0, cols], F32, "gt")
-                h_n = load_rows(nc, pools["node"], hn[0, rows, cols], F32, "h_n")
-                r = [load_gate(d, R, "r") for d in range(DIRS)]
-                agg_grouped = []
-                if cb == 0:
-                    for d in range(DIRS):
-                        agg_rows = load_rows(nc, pools["work"], agg[d, 0, rows, :], BF16, "agg_rows")
-                        agg_grouped.append(regroup(nc, pools["agg_grouped"], agg_rows[:]))
-
-
-                def flat(held):
-                    return held[:].rearrange("p j o -> p (j o)")
-
-                tot_t = []
-                for fb in range(M_TILES):
-                    tot_t.append(psum.tile([P, BANK], F32, name="spare%d" % fb, tag="spare%d" % fb))
-
-                def add_transposed(held, first, last):
-                    for fb in range(M_TILES):
-                        for j in range(PACK):
-                            nc.tensor.matmul(
-                                out=tot_t[fb][:, j * P : (j + 1) * P],
-                                lhsT=held[:, j, fb * P : (fb + 1) * P],
-                                rhs=identity[:],
-                                is_transpose=True,
-                                start=(first and j == 0),
-                                stop=(last and j == PACK - 1),
-                            )
-
+                    regroup_agg(i, d)
+            if i > 0 and has_next:
+                square(nxt, "r", -0.5)
+            gated_differences(0)
+            differences(1)
+            for d in range(DIRS):
+                product_grouped(i, "zch", "z", "zch", d)
+            gated_differences(1)
+            differences(2)
+            for ds in pieces(split):
+                product(i, "c", "c", 1.0, ALU.subtract, "z", ds)
+                if split:
+                    regroup_gate(i, "c", ds.start)
+            gated_differences(2)
+            if nxt + 1 < n_chunks:
+                transpose_h(nxt + 1, spare(0, BF16, 2 * BANK))
+            if not split:
                 for d in range(DIRS):
-                    add_transposed(c[d], d == 0, False)
-                for d in range(DIRS):
-                    nc.scalar.activation(out=r[d][:], in_=r[d][:], func=ACT.Square, bias=-0.5)
-
-                zch = []
-                for d in range(DIRS):
-                    zch.append(
-                        pools["work"].tile([P, PACK, COLS], F32, name="zch", tag="zch", bufs=2 * DIRS)
-                    )
-                    nc.vector.tensor_tensor(out=zch[d][:], in0=h[:], in1=c[d][:], op=ALU.subtract)
-                for d in range(DIRS):
-                    nc.vector.tensor_tensor(out=zch[d][:], in0=z[d][:], in1=zch[d][:], op=ALU.mult)
-                    add_transposed(zch[d], False, d == DIRS - 1)
-
-                dh = pools["work"].tile([P, PACK, COLS], F32, name="dh")
-                nc.vector.tensor_tensor(out=gt[:], in0=g[:], in1=gt[:], op=ALU.mult)
-                for d in range(DIRS):
-                    nc.vector.scalar_tensor_tensor(
-                        out=r[d][:], in0=r[d][:], scalar=0.25, in1=h_n[:],
-                        op0=ALU.subtract, op1=ALU.mult,
-                    )
-                for fb in range(M_TILES):
-                    tot_t_sb = pools["work"].tile([P, BANK], F32, name="tot_t_sb")
-                    nc.scalar.copy(out=tot_t_sb[:], in_=tot_t[fb][:])
-                    tot = psum.tile([P, BANK], F32, name="spare%d" % fb, tag="spare%d" % fb)
-                    for j in range(PACK):
-                        nc.tensor.transpose(
-                            tot[:, j * P : (j + 1) * P], tot_t_sb[:, j * P : (j + 1) * P], identity[:]
-                        )
-                    f_cols = slice(fb * P, (fb + 1) * P)
-                    nc.vector.scalar_tensor_tensor(
-                        out=dh[:, :, f_cols], in0=tot[:].rearrange("p (j o) -> p j o", j=PACK),
-                        scalar=0.0, in1=gt[:, :, f_cols], op0=ALU.is_gt, op1=ALU.mult,
-                    )
-
-                for d in range(DIRS):
-                    nc.scalar.activation(out=c[d][:], in_=c[d][:], func=ACT.Square)
-
-                for d in range(DIRS):
-                    nc.vector.scalar_tensor_tensor(
-                        out=z[d][:], in0=z[d][:], scalar=1.0, in1=dh[:],
-                        op0=ALU.subtract, op1=ALU.mult,
-                    )
-                def multiply(gate, d, grouped):
-                    codes = pools["dgi_mx"].tile([P, COLS], U32, name="codes", align_bytes=64)
-                    scales = pools["dgi_mx"].tile([P, COLS], U8, name="scales", align_bytes=64)
-                    quantise(nc, grouped, E5M2_X4, codes[:], scales[:])
-                    last = nb == NODE_BLOCKS - 1 and d == DIRS - 1
-                    for m in range(M_TILES):
-                        m_cols = slice(m * M_TILE, (m + 1) * M_TILE)
-                        nc.tensor.matmul_mx(
-                            out=acc[(gate, m)][:],
-                            lhsT=codes[:, m_cols].bitcast(E5M2_X4),
-                            lhsT_scale=scales[:, m_cols],
-                            rhs=agg_codes[:, nb, d, :].bitcast(E4M3_X4),
-                            rhs_scale=agg_scales[:, nb, d, :],
-                            start=(nb == 0 and d == 0),
-                            stop=last,
-                        )
-                        if last:
-                            result = pools["result"].tile([M_TILE, FEAT], F32, name="result")
-                            nc.scalar.copy(out=result[:], in_=acc[(gate, m)][:])
-                            first = gate * FEAT + cb * COLS + m * M_TILE
-                            nc.sync.dma_start(out=out[first : first + M_TILE, :], in_=result[:])
-
-
-                dz = []
-                for d in range(DIRS):
-                    nc.vector.scalar_tensor_tensor(
-                        out=zch[d][:], in0=z[d][:], scalar=-1.0, in1=zch[d][:],
-                        op0=ALU.mult, op1=ALU.mult,
-                    )
-                    dz.append(regroup(nc, pools["grouped"], zch[d][:]))
-                dc = []
-                for d in range(DIRS):
-                    nc.vector.scalar_tensor_tensor(
-                        out=c[d][:], in0=c[d][:], scalar=1.0, in1=z[d][:],
-                        op0=ALU.subtract, op1=ALU.mult,
-                    )
-                    dc.append(regroup(nc, pools["grouped"], c[d][:]))
-                    if cb == 0:
-                        quantise(
-                            nc, agg_grouped[d], E4M3_X4,
-                            agg_codes[:, nb, d, :], agg_scales[:, nb, d, :],
-                        )
-                    multiply(Z, d, dz[d])
-                dr = []
-                for d in range(DIRS):
-                    nc.vector.scalar_tensor_tensor(
-                        out=r[d][:], in0=r[d][:], scalar=-1.0, in1=c[d][:],
-                        op0=ALU.mult, op1=ALU.mult,
-                    )
-                    dr.append(regroup(nc, pools["grouped"], r[d][:]))
-                    multiply(C, d, dc[d])
-                for d in range(DIRS):
-                    multiply(R, d, dr[d])
+                    regroup_gate(i, "c", d)
+            if i == 0:
+                square(nxt, "r", -0.5)
+            if has_next:
+                for fb in (1, 0):
+                    sum_into(nxt, fb, True, all_dirs, True)
+            if i == 0:
+                times_hn(0)
+            quantise_agg(i)
+            for d in range(DIRS):
+                multiply(i, Z, "zch", d)
+            if has_next:
+                new_dh(nxt)
+                tot_back(nxt, 1)
+                tot_back(nxt, 0)
+            for d in range(DIRS):
+                product_grouped(i, "r", "r", "c", d)
+            if i + 2 < n_chunks:
+                load_gate(i + 2, "c", C)
+                load_gate(i + 2, "z", Z)
+                load_dh_inputs(i + 2)
+                load_r(i + 2)
+            for d in range(DIRS):
+                multiply(i, C, "c", d)
+            store(i, Z)
+            if has_next:
+                times_t(nxt)
+                times_hn(nxt)
+            for d in range(DIRS):
+                multiply(i, R, "r", d)
+            store(i, C)
+            if has_next:
+                mask(nxt, 1)
+                mask(nxt, 0)
+            store(i, R, shared_out=split)

@@ -55,9 +55,9 @@ def tile_graphconvolution_pb_v_kernel(
         work_pool = ctx.enter_context(tc.tile_pool(name="work", bufs=2))
         grouped_pool = ctx.enter_context(tc.tile_pool(name="grouped", bufs=3 * DIRS))
         agg_pool = ctx.enter_context(tc.tile_pool(name="agg", bufs=DIRS))
-        mx_pool = ctx.enter_context(tc.tile_pool(name="dgi_mx", bufs=GATES * DIRS))
+        mx_pool = ctx.enter_context(tc.tile_pool(name="dgi_mx", bufs=2 * GATES * DIRS))
         keep_pool = ctx.enter_context(tc.tile_pool(name="keep", bufs=1))
-        result_pool = ctx.enter_context(tc.tile_pool(name="result", bufs=GATES * M_TILES))
+        result_pool = ctx.enter_context(tc.tile_pool(name="result", bufs=4))
         psum = ctx.enter_context(tc.psum_pool(name="psum", bufs=1))
         ctx.enter_context(tc.manual_schedule())
 
@@ -105,10 +105,13 @@ def tile_graphconvolution_pb_v_kernel(
             load_node(i, "g", BF16, grad_out[rows, 0, cols], 2)
             load_node(i, "gt", F32, t[rows, 0, cols], 2)
 
-        def load_r(i):
+        def load_hn(i):
             rows, cols = where(i)
-            load_gate(i, "r", R)
             load_node(i, "h_n", F32, hn[0, rows, cols], 2)
+
+        def load_r(i):
+            load_gate(i, "r", R)
+            load_hn(i)
 
         def load_agg(i, dirs=(0, 1, 2)):
             cb, nb = chunks[i]
@@ -269,11 +272,15 @@ def tile_graphconvolution_pb_v_kernel(
             st = state[i]
             st.setdefault("grouped_" + name, []).append(regroup(grouped_pool, st[name][:, d], "grouped", -1.0))
 
-        def multiply(i, gate, name, d):
-            cb, nb = chunks[i]
+        def quantise_gate(i, gate, name, d):
             codes = mx_pool.tile([P, COLS], U32, name="codes", tag="codes", align_bytes=64)
             scales = mx_pool.tile([P, COLS], U8, name="scales", tag="scales", align_bytes=64)
             quantise(state[i]["grouped_" + name][d], E5M2_X4, codes[:], scales[:])
+            state[i][(gate, d)] = (codes, scales)
+
+        def multiply(i, gate, d):
+            cb, nb = chunks[i]
+            codes, scales = state[i][(gate, d)]
             for m in range(M_TILES):
                 if nb == 0 and d == 0:
                     acc[(gate, m)] = psum.tile(
@@ -326,6 +333,13 @@ def tile_graphconvolution_pb_v_kernel(
         def times_hn(i):
             product(i, "r", "r", 0.25, ALU.subtract, "h_n", all_dirs, in1_shared=True)
 
+        def all_passes(i):
+            for gate in (Z, C, R):
+                for d in range(DIRS):
+                    multiply(i, gate, d)
+            for gate in (Z, C, R):
+                store(i, gate)
+
         load_h(0)
         load_gate(0, "c", C)
         load_gate(0, "z", Z)
@@ -333,18 +347,16 @@ def tile_graphconvolution_pb_v_kernel(
         load_h(1)
         load_gate(1, "c", C, (0,))
         load_gate(1, "z", Z, (0,))
-        load_r(0)
         load_gate(1, "c", C, (1,))
         load_gate(1, "z", Z, (1,))
-        load_agg(0, (0, 1))
+        load_gate(0, "r", R)
         load_gate(1, "c", C, (2,))
-        load_agg(0, (2,))
         load_gate(1, "z", Z, (2,))
+        load_hn(0)
         load_h(2)
-        load_h(3)
         load_dh_inputs(1)
         load_r(1)
-        load_agg(1)
+        load_h(3)
 
         st = state[0]
         for fb in range(M_TILES):
@@ -374,7 +386,7 @@ def tile_graphconvolution_pb_v_kernel(
             has_next = nxt < n_chunks
             split = not has_next
             banks = {}
-            has_agg = chunks[i][0] == 0
+            agg_due = i > 0 and chunks[i - 1][0] == 0
 
             def differences(d):
                 if has_next:
@@ -394,9 +406,9 @@ def tile_graphconvolution_pb_v_kernel(
             product(i, "z", "z", 1.0, ALU.subtract, "dh", all_dirs, in1_shared=True)
             if i == 0:
                 square(0, "r", -0.5)
-            if has_agg:
+            if agg_due:
                 for d in range(DIRS):
-                    regroup_agg(i, d)
+                    regroup_agg(i - 1, d)
             if i > 0 and has_next:
                 square(nxt, "r", -0.5)
             gated_differences(0)
@@ -410,6 +422,8 @@ def tile_graphconvolution_pb_v_kernel(
                 if split:
                     regroup_gate(i, "c", ds.start)
             gated_differences(2)
+            if i + 2 < n_chunks:
+                load_gate(i + 2, "z", Z)
             if nxt + 1 < n_chunks:
                 transpose_h(nxt + 1, spare(0, BF16, 2 * BANK))
             if not split:
@@ -422,30 +436,36 @@ def tile_graphconvolution_pb_v_kernel(
                     sum_into(nxt, fb, True, all_dirs, True)
             if i == 0:
                 times_hn(0)
-            quantise_agg(i)
-            for d in range(DIRS):
-                multiply(i, Z, "zch", d)
+            if agg_due:
+                quantise_agg(i - 1)
             if has_next:
                 new_dh(nxt)
                 tot_back(nxt, 1)
                 tot_back(nxt, 0)
+            if i > 0:
+                all_passes(i - 1)
+            for d in range(DIRS):
+                quantise_gate(i, Z, "zch", d)
             for d in range(DIRS):
                 product_grouped(i, "r", "r", "c", d)
             if i + 2 < n_chunks:
                 load_gate(i + 2, "c", C)
-                load_gate(i + 2, "z", Z)
+                load_agg(i)
+                load_gate(i + 2, "r", R)
                 load_dh_inputs(i + 2)
-                load_r(i + 2)
+                load_hn(i + 2)
             for d in range(DIRS):
-                multiply(i, C, "c", d)
-            store(i, Z)
+                quantise_gate(i, C, "c", d)
             if has_next:
                 times_t(nxt)
                 times_hn(nxt)
             for d in range(DIRS):
-                multiply(i, R, "r", d)
-            store(i, C)
+                quantise_gate(i, R, "r", d)
             if has_next:
                 mask(nxt, 1)
                 mask(nxt, 0)
-            store(i, R, shared_out=split)
+        last = n_chunks - 1
+        for gate in (Z, C, R):
+            for d in range(DIRS):
+                multiply(last, gate, d)
+            store(last, gate, shared_out=(gate == R))

@@ -152,26 +152,27 @@ def tile_graphconvolution_pb_v_kernel(
                 in_=grouped[:].rearrange("p o j -> p (o j)"),
             )
 
-        def spare(b, dtype, width):
-            return psum.tile([P, width], dtype, name="spare%d" % b, tag="spare%d" % b)
+        def bank(kind, k, dtype=F32, width=BANK):
+            return psum.tile([P, width], dtype, name="%s%d" % (kind, k), tag="%s%d" % (kind, k))
 
-        def transpose_h(i, bank):
+        def transpose_h(i):
             h = state[i]["h"]
+            turned = bank("m", i, BF16, 2 * BANK)
             for fb in range(M_TILES):
                 for j in range(PACK):
                     k = fb * PACK + j
                     nc.tensor.transpose(
-                        bank[:, k * P : (k + 1) * P], h[:, j, fb * P : (fb + 1) * P], identity_bf[:]
+                        turned[:, k * P : (k + 1) * P], h[:, j, fb * P : (fb + 1) * P], identity_bf[:]
                     )
-            h_t = work_pool.tile([P, M_TILES, PACK, P], F32, name="h_t", tag="h_t")
-            nc.scalar.copy(out=h_t[:].rearrange("p f j q -> p (f j q)"), in_=bank[:])
+            h_t = work_pool.tile([P, M_TILES, PACK, P], F32, name="h_t", tag="h_t", bufs=n_chunks - 1)
+            nc.scalar.copy(out=h_t[:].rearrange("p f j q -> p (f j q)"), in_=turned[:])
             state[i]["h_t"] = h_t
 
         def difference(i, d, b):
             st = state[i]
-            bank = spare(b, F32, BANK)
+            diff = bank("a", b)
             nc.tensor.matmul(
-                out=bank[:], lhsT=minus_identity[:],
+                out=diff[:], lhsT=minus_identity[:],
                 rhs=st["c"][:, d].rearrange("p j o -> p (j o)")[:, b * BANK : (b + 1) * BANK],
                 start=True, stop=False,
             )
@@ -180,22 +181,22 @@ def tile_graphconvolution_pb_v_kernel(
                 for fb in range(M_TILES):
                     first = jj * COLS + fb * P
                     nc.tensor.matmul(
-                        out=bank[:, first : first + P], lhsT=st["h_t"][:, fb, b * per_bank + jj, :],
+                        out=diff[:, first : first + P], lhsT=st["h_t"][:, fb, b * per_bank + jj, :],
                         rhs=identity[:], is_transpose=True,
                         start=False, stop=(jj == per_bank - 1 and fb == M_TILES - 1),
                     )
-            return bank
+            return diff
 
         def new_zch(i):
             state[i]["zch"] = work_pool.tile([P, DIRS, PACK, COLS], F32, name="zch", tag="zch")
 
-        def gated_difference(i, d, b, bank):
+        def gated_difference(i, d, b, diff):
             st = state[i]
             part = slice(b * BANK, (b + 1) * BANK)
             nc.vector.tensor_tensor(
                 out=st["zch"][:, d].rearrange("p j o -> p (j o)")[:, part],
                 in0=st["z"][:, d].rearrange("p j o -> p (j o)")[:, part],
-                in1=bank[:], op=ALU.mult,
+                in1=diff[:], op=ALU.mult,
             )
 
         def add_transposed(tot_t, fb, held, ds, first, last):
@@ -220,7 +221,7 @@ def tile_graphconvolution_pb_v_kernel(
             st = state[i]
             tot_t_sb = work_pool.tile([P, BANK], F32, name="tot_t_sb", tag="tot_t_sb")
             nc.scalar.copy(out=tot_t_sb[:], in_=st["tot_t"][fb][:])
-            tot = spare(fb, F32, BANK)
+            tot = bank("x", fb)
             for j in range(PACK):
                 nc.tensor.transpose(
                     tot[:, j * P : (j + 1) * P], tot_t_sb[:, j * P : (j + 1) * P], identity[:]
@@ -282,10 +283,6 @@ def tile_graphconvolution_pb_v_kernel(
             cb, nb = chunks[i]
             codes, scales = state[i][(gate, d)]
             for m in range(M_TILES):
-                if nb == 0 and d == 0:
-                    acc[(gate, m)] = psum.tile(
-                        [M_TILE, FEAT], F32, name="acc%d%d" % (gate, m), tag="acc%d%d" % (gate, m)
-                    )
                 m_cols = slice(m * M_TILE, (m + 1) * M_TILE)
                 nc.tensor.matmul_mx(
                     out=acc[(gate, m)][:],
@@ -311,16 +308,22 @@ def tile_graphconvolution_pb_v_kernel(
                 nc.sync.dma_start(out=out[first : first + M_TILE, :], in_=result[:])
 
 
-        def sum_into(i, fb, with_c, ds, last):
+        def add_c_to_tot(i, d):
+            if i >= n_chunks:
+                return
             st = state[i]
-            if with_c:
-                st.setdefault("tot_t", {})[fb] = spare(fb, F32, BANK)
-                add_transposed(st["tot_t"][fb], fb, st["c"], all_dirs, True, False)
-            if ds is not None:
-                add_transposed(st["tot_t"][fb], fb, st["zch"], ds, False, last)
+            for fb in range(M_TILES):
+                if d == 0:
+                    st.setdefault("tot_t", {})[fb] = bank("x", fb)
+                add_transposed(st["tot_t"][fb], fb, st["c"], slice(d, d + 1), d == 0, False)
+
+        def add_to_tot(i, ds):
+            st = state[i]
+            for fb in range(M_TILES):
+                add_transposed(st["tot_t"][fb], fb, st["zch"], ds, False, ds.stop == DIRS)
 
         def new_dh(i):
-            state[i]["dh"] = work_pool.tile([P, PACK, COLS], F32, name="dh", tag="dh")
+            state[i]["dh"] = work_pool.tile([P, PACK, COLS], F32, name="dh", tag="dh", bufs=1)
             state[i]["tot"] = {}
 
         def times_t(i):
@@ -333,12 +336,30 @@ def tile_graphconvolution_pb_v_kernel(
         def times_hn(i):
             product(i, "r", "r", 0.25, ALU.subtract, "h_n", all_dirs, in1_shared=True)
 
-        def all_passes(i):
-            for gate in (Z, C, R):
-                for d in range(DIRS):
-                    multiply(i, gate, d)
-            for gate in (Z, C, R):
-                store(i, gate)
+        def open_acc(gate, kind, first):
+            for m in range(M_TILES):
+                acc[(gate, m)] = bank(kind, first + m)
+
+        def passes(i, gate):
+            for d in range(DIRS):
+                multiply(i, gate, d)
+
+        diffs = {}
+
+        def differences(i, d):
+            if i < n_chunks:
+                for b in range(HALVES):
+                    diffs[b] = difference(i, d, b)
+
+        def gated_differences(i, d):
+            if i < n_chunks:
+                for b in range(HALVES):
+                    gated_difference(i, d, b, diffs[b])
+                if d + 1 < DIRS:
+                    differences(i, d + 1)
+                add_to_tot(i, slice(d, d + 1))
+                if d + 1 < DIRS:
+                    add_c_to_tot(i, d + 1)
 
         load_h(0)
         load_gate(0, "c", C)
@@ -354,13 +375,13 @@ def tile_graphconvolution_pb_v_kernel(
         load_gate(1, "z", Z, (2,))
         load_hn(0)
         load_h(2)
+        load_h(3)
         load_dh_inputs(1)
         load_r(1)
-        load_h(3)
 
         st = state[0]
-        for fb in range(M_TILES):
-            sum_into(0, fb, True, None, False)
+        for d in range(DIRS):
+            add_c_to_tot(0, d)
         new_zch(0)
         for ds in pieces(True):
             nc.vector.tensor_tensor(
@@ -371,38 +392,26 @@ def tile_graphconvolution_pb_v_kernel(
             nc.vector.tensor_tensor(
                 out=wide(st["zch"], ds), in0=wide(st["z"], ds), in1=wide(st["zch"], ds), op=ALU.mult
             )
-            for fb in range(M_TILES):
-                sum_into(0, fb, False, ds, ds.stop == DIRS)
+            add_to_tot(0, ds)
         times_t(0)
         new_dh(0)
         for fb in range(M_TILES):
             tot_back(0, fb)
             mask(0, fb)
-        early_bank = psum.tile([P, 2 * BANK], BF16, name="acc00", tag="acc00")
-        transpose_h(1, early_bank)
+        transpose_h(1)
+        differences(1, 0)
 
         for i in range(n_chunks):
             nxt = i + 1
             has_next = nxt < n_chunks
             split = not has_next
-            banks = {}
             agg_due = i > 0 and chunks[i - 1][0] == 0
 
-            def differences(d):
-                if has_next:
-                    for b in range(HALVES):
-                        banks[b] = difference(nxt, d, b)
-
-            def gated_differences(d):
-                if has_next:
-                    for b in range(HALVES):
-                        gated_difference(nxt, d, b, banks[b])
-
+            if has_next:
+                add_c_to_tot(nxt, 0)
+                new_zch(nxt)
             if i > 0:
                 square(i, "c", 0.0)
-            if has_next:
-                new_zch(nxt)
-            differences(0)
             product(i, "z", "z", 1.0, ALU.subtract, "dh", all_dirs, in1_shared=True)
             if i == 0:
                 square(0, "r", -0.5)
@@ -411,39 +420,26 @@ def tile_graphconvolution_pb_v_kernel(
                     regroup_agg(i - 1, d)
             if i > 0 and has_next:
                 square(nxt, "r", -0.5)
-            gated_differences(0)
-            differences(1)
+            gated_differences(nxt, 0)
             for d in range(DIRS):
                 product_grouped(i, "zch", "z", "zch", d)
-            gated_differences(1)
-            differences(2)
             for ds in pieces(split):
                 product(i, "c", "c", 1.0, ALU.subtract, "z", ds)
                 if split:
                     regroup_gate(i, "c", ds.start)
-            gated_differences(2)
             if i + 2 < n_chunks:
                 load_gate(i + 2, "z", Z)
-            if nxt + 1 < n_chunks:
-                transpose_h(nxt + 1, spare(0, BF16, 2 * BANK))
             if not split:
                 for d in range(DIRS):
                     regroup_gate(i, "c", d)
+            gated_differences(nxt, 1)
             if i == 0:
                 square(nxt, "r", -0.5)
-            if has_next:
-                for fb in (1, 0):
-                    sum_into(nxt, fb, True, all_dirs, True)
-            if i == 0:
+                transpose_h(2)
+                transpose_h(3)
                 times_hn(0)
             if agg_due:
                 quantise_agg(i - 1)
-            if has_next:
-                new_dh(nxt)
-                tot_back(nxt, 1)
-                tot_back(nxt, 0)
-            if i > 0:
-                all_passes(i - 1)
             for d in range(DIRS):
                 quantise_gate(i, Z, "zch", d)
             for d in range(DIRS):
@@ -454,6 +450,34 @@ def tile_graphconvolution_pb_v_kernel(
                 load_gate(i + 2, "r", R)
                 load_dh_inputs(i + 2)
                 load_hn(i + 2)
+            if i == 1:
+                open_acc(Z, "m", 0)
+                open_acc(C, "m", 2)
+                passes(0, Z)
+                passes(0, C)
+            if i == 2:
+                passes(1, Z)
+                store(1, Z)
+                passes(1, C)
+                store(1, C)
+            if i == 3:
+                open_acc(Z, "m", 0)
+                open_acc(C, "m", 2)
+                open_acc(R, "a", 0)
+                passes(2, Z)
+                passes(2, C)
+                passes(2, R)
+            gated_differences(nxt, 2)
+            if has_next:
+                new_dh(nxt)
+                for fb in range(M_TILES):
+                    tot_back(nxt, fb)
+            if i == 2:
+                open_acc(R, "m", 0)
+                passes(0, R)
+                passes(1, R)
+                store(1, R)
+            differences(i + 2, 0)
             for d in range(DIRS):
                 quantise_gate(i, C, "c", d)
             if has_next:
@@ -462,10 +486,9 @@ def tile_graphconvolution_pb_v_kernel(
             for d in range(DIRS):
                 quantise_gate(i, R, "r", d)
             if has_next:
-                mask(nxt, 1)
-                mask(nxt, 0)
+                for fb in range(M_TILES):
+                    mask(nxt, fb)
         last = n_chunks - 1
         for gate in (Z, C, R):
-            for d in range(DIRS):
-                multiply(last, gate, d)
+            passes(last, gate)
             store(last, gate, shared_out=(gate == R))

@@ -442,8 +442,9 @@ def tile_graphconvolution_pb_v_kernel(
                 quantise_agg(i - 1)
             for d in range(DIRS):
                 quantise_gate(i, Z, "zch", d)
-            for d in range(DIRS):
-                product_grouped(i, "r", "r", "c", d)
+            if has_next:
+                for d in range(DIRS):
+                    product_grouped(i, "r", "r", "c", d)
             if i + 2 < n_chunks:
                 load_gate(i + 2, "c", C)
                 load_agg(i)
@@ -478,17 +479,27 @@ def tile_graphconvolution_pb_v_kernel(
                 passes(1, R)
                 store(1, R)
             differences(i + 2, 0)
-            for d in range(DIRS):
-                quantise_gate(i, C, "c", d)
             if has_next:
+                for d in range(DIRS):
+                    quantise_gate(i, C, "c", d)
                 times_t(nxt)
                 times_hn(nxt)
-            for d in range(DIRS):
-                quantise_gate(i, R, "r", d)
-            if has_next:
+                for d in range(DIRS - 1):
+                    quantise_gate(i, R, "r", d)
                 for fb in range(M_TILES):
                     mask(nxt, fb)
+                quantise_gate(i, R, "r", DIRS - 1)
         last = n_chunks - 1
-        for gate in (Z, C, R):
-            passes(last, gate)
-            store(last, gate, shared_out=(gate == R))
+        passes(last, Z)
+        store(last, Z)
+        for d in range(DIRS):
+            product_grouped(last, "r", "r", "c", d)
+            quantise_gate(last, C, "c", d)
+            multiply(last, C, d)
+            if d > 0:
+                quantise_gate(last, R, "r", d - 1)
+                multiply(last, R, d - 1)
+        store(last, C)
+        quantise_gate(last, R, "r", DIRS - 1)
+        multiply(last, R, DIRS - 1)
+        store(last, R, shared_out=True)

@@ -31,6 +31,7 @@ BANK = 512
 WIDTH = PACK * COLS
 HALVES = WIDTH // BANK
 RUN = 4
+SIDE = 64
 
 FLOPS = 2 * DIRS * NODES * GATES * FEAT * FEAT
 BYTES = (
@@ -258,13 +259,30 @@ def tile_graphconvolution_pb_v_kernel(
                 op0=op0, op1=ALU.mult,
             )
 
-        def product_grouped(i, name, in0_name, in1_name, d):
+        def side_product(i, in0_name, in1_name, d):
+            st = state[i]
+            part = work_pool.tile([P, PACK, SIDE], F32, name="part", tag="part")
+            nc.gpsimd.tensor_tensor(
+                out=part[:], in0=st[in0_name][:, d, :, COLS - SIDE :], in1=st[in1_name][:, d, :, COLS - SIDE :],
+                op=ALU.mult,
+            )
+            return part
+
+        def side_regroup(i, name, d, part):
+            grouped = state[i]["grouped_" + name][d]
+            nc.scalar.activation(
+                out=grouped[:, COLS - SIDE :, :].rearrange("p (c i) j -> p c j i", i=RUN),
+                in_=part[:].rearrange("p j (c i) -> p c j i", i=RUN),
+                func=ACT.Copy, scale=1.0,
+            )
+
+        def product_grouped(i, name, in0_name, in1_name, d, width=COLS):
             st = state[i]
             grouped = grouped_pool.tile([P, COLS, PACK], BF16, name="grouped", tag="grouped", align_bytes=64)
             nc.vector.tensor_tensor(
-                out=grouped[:].rearrange("p (c i) j -> p c j i", i=RUN),
-                in0=st[in0_name][:, d].rearrange("p j (c i) -> p c j i", i=RUN),
-                in1=st[in1_name][:, d].rearrange("p j (c i) -> p c j i", i=RUN),
+                out=grouped[:, :width, :].rearrange("p (c i) j -> p c j i", i=RUN),
+                in0=st[in0_name][:, d, :, :width].rearrange("p j (c i) -> p c j i", i=RUN),
+                in1=st[in1_name][:, d, :, :width].rearrange("p j (c i) -> p c j i", i=RUN),
                 op=ALU.mult,
             )
             st.setdefault("grouped_" + name, []).append(grouped)
@@ -420,9 +438,14 @@ def tile_graphconvolution_pb_v_kernel(
                     regroup_agg(i - 1, d)
             if i > 0 and has_next:
                 square(nxt, "r", -0.5)
+            if has_next:
+                dz_part = side_product(i, "z", "zch", DIRS - 1)
             gated_differences(nxt, 0)
             for d in range(DIRS):
-                product_grouped(i, "zch", "z", "zch", d)
+                shared_work = has_next and d == DIRS - 1
+                product_grouped(i, "zch", "z", "zch", d, COLS - SIDE if shared_work else COLS)
+            if has_next:
+                side_regroup(i, "zch", DIRS - 1, dz_part)
             for ds in pieces(split):
                 product(i, "c", "c", 1.0, ALU.subtract, "z", ds)
                 if split:
@@ -432,6 +455,8 @@ def tile_graphconvolution_pb_v_kernel(
             if not split:
                 for d in range(DIRS):
                     regroup_gate(i, "c", d)
+            if i > 0 and has_next:
+                dr_part = side_product(i, "r", "c", DIRS - 1)
             gated_differences(nxt, 1)
             if i == 0:
                 square(nxt, "r", -0.5)
@@ -444,7 +469,10 @@ def tile_graphconvolution_pb_v_kernel(
                 quantise_gate(i, Z, "zch", d)
             if has_next:
                 for d in range(DIRS):
-                    product_grouped(i, "r", "r", "c", d)
+                    shared_work = i > 0 and d == DIRS - 1
+                    product_grouped(i, "r", "r", "c", d, COLS - SIDE if shared_work else COLS)
+                if i > 0:
+                    side_regroup(i, "r", DIRS - 1, dr_part)
             if i + 2 < n_chunks:
                 load_gate(i + 2, "c", C)
                 load_agg(i)

@@ -31,7 +31,7 @@ BANK = 512
 WIDTH = PACK * COLS
 HALVES = WIDTH // BANK
 RUN = 4
-SIDE = 64
+SIDE = 96
 
 FLOPS = 2 * DIRS * NODES * GATES * FEAT * FEAT
 BYTES = (

@@ -81,16 +81,21 @@ def tile_graphconvolution_pb_v_kernel(
             cb, nb = chunks[i]
             return slice(nb * K_PASS, (nb + 1) * K_PASS), slice(cb * COLS, (cb + 1) * COLS)
 
-        def load_node(i, name, dtype, src, bufs):
-            held = node_pool.tile([P, PACK, COLS], dtype, name=name, tag=name, bufs=bufs)
-            nc.sync.dma_start(out=held[:], in_=rows_view(src))
-            state[i][name] = held
+        def tokens(b):
+            if b is None:
+                return slice(0, PACK)
+            return slice(b * PACK // HALVES, (b + 1) * PACK // HALVES)
 
-        def load_h(i):
+        def load_node(i, name, dtype, src, bufs, b=None):
+            if name not in state[i]:
+                state[i][name] = node_pool.tile([P, PACK, COLS], dtype, name=name, tag=name, bufs=bufs)
+            nc.sync.dma_start(out=state[i][name][:, tokens(b)], in_=rows_view(src)[:, tokens(b), :])
+
+        def load_h(i, b=None):
             rows, cols = where(i)
-            load_node(i, "h", BF16, x[rows, 0, cols], n_chunks)
+            load_node(i, "h", BF16, x[rows, 0, cols], n_chunks, b)
 
-        def load_gate(i, name, gate, dirs=(0, 1, 2)):
+        def load_gate(i, name, gate, dirs=(0, 1, 2), b=None):
             cb, nb = chunks[i]
             rows, cols = where(i)
             if name not in state[i]:
@@ -98,13 +103,14 @@ def tile_graphconvolution_pb_v_kernel(
             first = gate * FEAT + cb * COLS
             for d in dirs:
                 nc.sync.dma_start(
-                    out=state[i][name][:, d], in_=rows_view(gates[d, 0, rows, first : first + COLS])
+                    out=state[i][name][:, d, tokens(b)],
+                    in_=rows_view(gates[d, 0, rows, first : first + COLS])[:, tokens(b), :],
                 )
 
-        def load_dh_inputs(i):
+        def load_dh_inputs(i, b=None):
             rows, cols = where(i)
-            load_node(i, "g", BF16, grad_out[rows, 0, cols], 2)
-            load_node(i, "gt", F32, t[rows, 0, cols], 2)
+            load_node(i, "g", BF16, grad_out[rows, 0, cols], 2, b)
+            load_node(i, "gt", F32, t[rows, 0, cols], 2, b)
 
         def load_hn(i):
             rows, cols = where(i)
@@ -130,12 +136,16 @@ def tile_graphconvolution_pb_v_kernel(
                 return [slice(d, d + 1) for d in range(DIRS)]
             return [all_dirs]
 
-        def wide(held, ds):
-            return held[:, ds].rearrange("p d j o -> p d (j o)")
+        def wide(held, ds, b=None):
+            return held[:, ds, tokens(b)].rearrange("p d j o -> p d (j o)")
 
-        def shared(held, ds):
+        def flat(held, b=None):
+            return held[:, tokens(b)].rearrange("p j o -> p (j o)")
+
+        def shared(held, ds, b=None):
             n = ds.stop - ds.start
-            return held[:].rearrange("p j o -> p (j o)").unsqueeze(1).to_broadcast([P, n, WIDTH])
+            width = WIDTH if b is None else BANK
+            return flat(held, b).unsqueeze(1).to_broadcast([P, n, width])
 
         def regroup(pool, values, tag, factor):
             width = values.shape[2]
@@ -200,41 +210,41 @@ def tile_graphconvolution_pb_v_kernel(
                 in1=diff[:], op=ALU.mult,
             )
 
-        def add_transposed(tot_t, fb, held, ds, first, last):
+        def add_transposed(tot_t, b, held, ds, first, last):
+            blocks = [(j, fb) for j in range(tokens(b).start, tokens(b).stop) for fb in range(M_TILES)]
             for d in range(ds.start, ds.stop):
-                for j in range(PACK):
+                for k, (j, fb) in enumerate(blocks):
                     nc.tensor.matmul(
-                        out=tot_t[:, j * P : (j + 1) * P],
+                        out=tot_t[:, k * P : (k + 1) * P],
                         lhsT=held[:, d, j, fb * P : (fb + 1) * P],
                         rhs=identity[:],
                         is_transpose=True,
-                        start=(first and d == ds.start and j == 0),
-                        stop=(last and d == ds.stop - 1 and j == PACK - 1),
+                        start=(first and d == ds.start and k == 0),
+                        stop=(last and d == ds.stop - 1 and k == len(blocks) - 1),
                     )
 
-        def square(i, name, bias):
+        def square(i, name, bias, b=None):
             held = state[i][name]
             nc.scalar.activation(
-                out=wide(held, all_dirs), in_=wide(held, all_dirs), func=ACT.Square, bias=bias
+                out=wide(held, all_dirs, b), in_=wide(held, all_dirs, b), func=ACT.Square, bias=bias
             )
 
-        def tot_back(i, fb):
+        def tot_back(i, b):
             st = state[i]
             tot_t_sb = work_pool.tile([P, BANK], F32, name="tot_t_sb", tag="tot_t_sb")
-            nc.scalar.copy(out=tot_t_sb[:], in_=st["tot_t"][fb][:])
-            tot = bank("x", fb)
-            for j in range(PACK):
+            nc.scalar.copy(out=tot_t_sb[:], in_=st["tot_t"][b][:])
+            tot = bank("x", b)
+            for k in range(BANK // P):
                 nc.tensor.transpose(
-                    tot[:, j * P : (j + 1) * P], tot_t_sb[:, j * P : (j + 1) * P], identity[:]
+                    tot[:, k * P : (k + 1) * P], tot_t_sb[:, k * P : (k + 1) * P], identity[:]
                 )
-            st["tot"][fb] = tot
+            st["tot"][b] = tot
 
-        def mask(i, fb):
+        def mask(i, b):
             st = state[i]
-            f_cols = slice(fb * P, (fb + 1) * P)
             nc.vector.scalar_tensor_tensor(
-                out=st["dh"][:, :, f_cols], in0=st["tot"][fb][:].rearrange("p (j o) -> p j o", j=PACK),
-                scalar=0.0, in1=st["gt"][:, :, f_cols], op0=ALU.is_gt, op1=ALU.mult,
+                out=flat(st["dh"], b), in0=st["tot"][b][:], scalar=0.0, in1=flat(st["gt"], b),
+                op0=ALU.is_gt, op1=ALU.mult,
             )
 
         def regroup_agg(i, d):
@@ -251,11 +261,11 @@ def tile_graphconvolution_pb_v_kernel(
                     agg_codes[:, nb, d, :], agg_scales[:, nb, d, :],
                 )
 
-        def product(i, out_name, in0_name, scalar, op0, in1_name, ds, in1_shared=False):
+        def product(i, out_name, in0_name, scalar, op0, in1_name, ds, in1_shared=False, b=None):
             st = state[i]
-            in1 = shared(st[in1_name], ds) if in1_shared else wide(st[in1_name], ds)
+            in1 = shared(st[in1_name], ds, b) if in1_shared else wide(st[in1_name], ds, b)
             nc.vector.scalar_tensor_tensor(
-                out=wide(st[out_name], ds), in0=wide(st[in0_name], ds), scalar=scalar, in1=in1,
+                out=wide(st[out_name], ds, b), in0=wide(st[in0_name], ds, b), scalar=scalar, in1=in1,
                 op0=op0, op1=ALU.mult,
             )
 
@@ -276,16 +286,19 @@ def tile_graphconvolution_pb_v_kernel(
                 func=ACT.Copy, scale=1.0,
             )
 
-        def product_grouped(i, name, in0_name, in1_name, d, width=COLS):
+        def product_grouped(i, name, in0_name, in1_name, d, width=COLS, b=None):
             st = state[i]
-            grouped = grouped_pool.tile([P, COLS, PACK], BF16, name="grouped", tag="grouped", align_bytes=64)
+            made = st.setdefault("grouped_" + name, [])
+            if len(made) <= d:
+                made.append(
+                    grouped_pool.tile([P, COLS, PACK], BF16, name="grouped", tag="grouped", align_bytes=64)
+                )
             nc.vector.tensor_tensor(
-                out=grouped[:, :width, :].rearrange("p (c i) j -> p c j i", i=RUN),
-                in0=st[in0_name][:, d, :, :width].rearrange("p j (c i) -> p c j i", i=RUN),
-                in1=st[in1_name][:, d, :, :width].rearrange("p j (c i) -> p c j i", i=RUN),
+                out=made[d][:, :width, tokens(b)].rearrange("p (c i) j -> p c j i", i=RUN),
+                in0=st[in0_name][:, d, tokens(b), :width].rearrange("p j (c i) -> p c j i", i=RUN),
+                in1=st[in1_name][:, d, tokens(b), :width].rearrange("p j (c i) -> p c j i", i=RUN),
                 op=ALU.mult,
             )
-            st.setdefault("grouped_" + name, []).append(grouped)
 
         def regroup_gate(i, name, d):
             st = state[i]
@@ -326,29 +339,29 @@ def tile_graphconvolution_pb_v_kernel(
                 nc.sync.dma_start(out=out[first : first + M_TILE, :], in_=result[:])
 
 
-        def add_c_to_tot(i, d):
+        def add_c_to_tot(i, d, halves=(0, 1)):
             if i >= n_chunks:
                 return
             st = state[i]
-            for fb in range(M_TILES):
+            for b in halves:
                 if d == 0:
-                    st.setdefault("tot_t", {})[fb] = bank("x", fb)
-                add_transposed(st["tot_t"][fb], fb, st["c"], slice(d, d + 1), d == 0, False)
+                    st.setdefault("tot_t", {})[b] = bank("x", b)
+                add_transposed(st["tot_t"][b], b, st["c"], slice(d, d + 1), d == 0, False)
 
-        def add_to_tot(i, ds):
+        def add_to_tot(i, ds, halves=(0, 1)):
             st = state[i]
-            for fb in range(M_TILES):
-                add_transposed(st["tot_t"][fb], fb, st["zch"], ds, False, ds.stop == DIRS)
+            for b in halves:
+                add_transposed(st["tot_t"][b], b, st["zch"], ds, False, ds.stop == DIRS)
 
         def new_dh(i):
             state[i]["dh"] = work_pool.tile([P, PACK, COLS], F32, name="dh", tag="dh", bufs=1)
             state[i]["tot"] = {}
 
-        def times_t(i):
+        def times_t(i, b=None):
             st = state[i]
             nc.vector.scalar_tensor_tensor(
-                out=st["gt"][:].rearrange("p j o -> p (j o)"), in0=st["g"][:].rearrange("p j o -> p (j o)"),
-                scalar=-1.0, in1=st["gt"][:].rearrange("p j o -> p (j o)"), op0=ALU.mult, op1=ALU.mult,
+                out=flat(st["gt"], b), in0=flat(st["g"], b), scalar=-1.0, in1=flat(st["gt"], b),
+                op0=ALU.mult, op1=ALU.mult,
             )
 
         def times_hn(i):
@@ -379,45 +392,83 @@ def tile_graphconvolution_pb_v_kernel(
                 if d + 1 < DIRS:
                     add_c_to_tot(i, d + 1)
 
-        load_h(0)
-        load_gate(0, "c", C)
-        load_gate(0, "z", Z)
-        load_dh_inputs(0)
+        for b in range(HALVES):
+            load_h(0, b)
+            load_gate(0, "c", C, b=b)
+            load_gate(0, "z", Z, b=b)
+            load_dh_inputs(0, b)
         load_h(1)
         load_gate(1, "c", C, (0,))
         load_gate(1, "z", Z, (0,))
+        load_gate(0, "r", R)
         load_gate(1, "c", C, (1,))
         load_gate(1, "z", Z, (1,))
-        load_gate(0, "r", R)
+        load_hn(0)
         load_gate(1, "c", C, (2,))
         load_gate(1, "z", Z, (2,))
-        load_hn(0)
         load_h(2)
-        load_h(3)
-        load_dh_inputs(1)
         load_r(1)
+        load_dh_inputs(1)
+        load_h(3)
 
         st = state[0]
-        for d in range(DIRS):
-            add_c_to_tot(0, d)
         new_zch(0)
-        for ds in pieces(True):
-            nc.vector.tensor_tensor(
-                out=wide(st["zch"], ds), in0=shared(st["h"], ds), in1=wide(st["c"], ds), op=ALU.subtract
-            )
-        square(0, "c", 0.0)
-        for ds in pieces(True):
-            nc.vector.tensor_tensor(
-                out=wide(st["zch"], ds), in0=wide(st["z"], ds), in1=wide(st["zch"], ds), op=ALU.mult
-            )
-            add_to_tot(0, ds)
-        times_t(0)
         new_dh(0)
-        for fb in range(M_TILES):
-            tot_back(0, fb)
-            mask(0, fb)
+
+        def first_differences(b):
+            for ds in pieces(True):
+                nc.vector.tensor_tensor(
+                    out=wide(st["zch"], ds, b), in0=shared(st["h"], ds, b), in1=wide(st["c"], ds, b),
+                    op=ALU.subtract,
+                )
+            for ds in pieces(True):
+                nc.scalar.activation(
+                    out=wide(st["c"], ds, b), in_=wide(st["c"], ds, b), func=ACT.Square,
+                )
+
+        def first_gated(b):
+            for ds in pieces(True):
+                nc.vector.tensor_tensor(
+                    out=wide(st["zch"], ds, b), in0=wide(st["z"], ds, b), in1=wide(st["zch"], ds, b),
+                    op=ALU.mult,
+                )
+                add_to_tot(0, ds, (b,))
+            times_t(0, b)
+            tot_back(0, b)
+
+        def first_products(b):
+            for d in range(DIRS):
+                product_grouped(0, "zch", "z", "zch", d, COLS, b)
+            product(0, "c", "c", 1.0, ALU.subtract, "z", all_dirs, b=b)
+
+        def first_dh(b):
+            mask(0, b)
+            product(0, "z", "z", 1.0, ALU.subtract, "dh", all_dirs, in1_shared=True, b=b)
+
+        for d in range(DIRS):
+            add_c_to_tot(0, d, (0,))
+        first_differences(0)
+        first_gated(0)
+        for d in range(DIRS):
+            add_c_to_tot(0, d, (1,))
+        first_differences(1)
+        first_dh(0)
+        first_gated(1)
         transpose_h(1)
         differences(1, 0)
+        first_products(0)
+        first_dh(1)
+        square(0, "r", -0.5)
+        add_c_to_tot(1, 0)
+        new_zch(1)
+        for d in range(DIRS):
+            product_grouped(0, "zch", "z", "zch", d, COLS, 1)
+        gated_differences(1, 0)
+        product(0, "c", "c", 1.0, ALU.subtract, "z", all_dirs, b=1)
+        load_gate(2, "z", Z)
+        for d in range(DIRS):
+            regroup_gate(0, "c", d)
+        times_hn(0)
 
         for i in range(n_chunks):
             nxt = i + 1
@@ -425,44 +476,44 @@ def tile_graphconvolution_pb_v_kernel(
             split = not has_next
             agg_due = i > 0 and chunks[i - 1][0] == 0
 
-            if has_next:
-                add_c_to_tot(nxt, 0)
-                new_zch(nxt)
             if i > 0:
-                square(i, "c", 0.0)
-            product(i, "z", "z", 1.0, ALU.subtract, "dh", all_dirs, in1_shared=True)
-            if i == 0:
-                square(0, "r", -0.5)
-            if agg_due:
+                if has_next:
+                    add_c_to_tot(nxt, 0)
+                    new_zch(nxt)
+                if i > 0:
+                    square(i, "c", 0.0)
+                product(i, "z", "z", 1.0, ALU.subtract, "dh", all_dirs, in1_shared=True)
+                if i == 0:
+                    square(0, "r", -0.5)
+                if agg_due:
+                    for d in range(DIRS):
+                        regroup_agg(i - 1, d)
+                if i > 0 and has_next:
+                    square(nxt, "r", -0.5)
+                if has_next:
+                    dz_part = side_product(i, "z", "zch", DIRS - 1)
+                gated_differences(nxt, 0)
                 for d in range(DIRS):
-                    regroup_agg(i - 1, d)
-            if i > 0 and has_next:
-                square(nxt, "r", -0.5)
-            if has_next:
-                dz_part = side_product(i, "z", "zch", DIRS - 1)
-            gated_differences(nxt, 0)
-            for d in range(DIRS):
-                shared_work = has_next and d == DIRS - 1
-                product_grouped(i, "zch", "z", "zch", d, COLS - SIDE if shared_work else COLS)
-            if has_next:
-                side_regroup(i, "zch", DIRS - 1, dz_part)
-            for ds in pieces(split):
-                product(i, "c", "c", 1.0, ALU.subtract, "z", ds)
-                if split:
-                    regroup_gate(i, "c", ds.start)
-            if i + 2 < n_chunks:
-                load_gate(i + 2, "z", Z)
-            if not split:
-                for d in range(DIRS):
-                    regroup_gate(i, "c", d)
-            if i > 0 and has_next:
-                dr_part = side_product(i, "r", "c", DIRS - 1)
+                    shared_work = has_next and d == DIRS - 1
+                    product_grouped(i, "zch", "z", "zch", d, COLS - SIDE if shared_work else COLS)
+                if has_next:
+                    side_regroup(i, "zch", DIRS - 1, dz_part)
+                for ds in pieces(split):
+                    product(i, "c", "c", 1.0, ALU.subtract, "z", ds)
+                    if split:
+                        regroup_gate(i, "c", ds.start)
+                if i + 2 < n_chunks:
+                    load_gate(i + 2, "z", Z)
+                if not split:
+                    for d in range(DIRS):
+                        regroup_gate(i, "c", d)
+                if i > 0 and has_next:
+                    dr_part = side_product(i, "r", "c", DIRS - 1)
             gated_differences(nxt, 1)
             if i == 0:
                 square(nxt, "r", -0.5)
                 transpose_h(2)
                 transpose_h(3)
-                times_hn(0)
             if agg_due:
                 quantise_agg(i - 1)
             for d in range(DIRS):
@@ -499,8 +550,8 @@ def tile_graphconvolution_pb_v_kernel(
             gated_differences(nxt, 2)
             if has_next:
                 new_dh(nxt)
-                for fb in range(M_TILES):
-                    tot_back(nxt, fb)
+                for b in range(HALVES):
+                    tot_back(nxt, b)
             if i == 2:
                 open_acc(R, "m", 0)
                 passes(0, R)
@@ -514,8 +565,8 @@ def tile_graphconvolution_pb_v_kernel(
                 times_hn(nxt)
                 for d in range(DIRS - 1):
                     quantise_gate(i, R, "r", d)
-                for fb in range(M_TILES):
-                    mask(nxt, fb)
+                for b in range(HALVES):
+                    mask(nxt, b)
                 quantise_gate(i, R, "r", DIRS - 1)
         last = n_chunks - 1
         passes(last, Z)

@@ -507,8 +507,8 @@ def tile_graphconvolution_pb_v_kernel(
                 if not split:
                     for d in range(DIRS):
                         regroup_gate(i, "c", d)
-                if i > 0 and has_next:
-                    dr_part = side_product(i, "r", "c", DIRS - 1)
+            if has_next:
+                dr_part = side_product(i, "r", "c", DIRS - 1)
             gated_differences(nxt, 1)
             if i == 0:
                 square(nxt, "r", -0.5)
@@ -520,10 +520,8 @@ def tile_graphconvolution_pb_v_kernel(
                 quantise_gate(i, Z, "zch", d)
             if has_next:
                 for d in range(DIRS):
-                    shared_work = i > 0 and d == DIRS - 1
-                    product_grouped(i, "r", "r", "c", d, COLS - SIDE if shared_work else COLS)
-                if i > 0:
-                    side_regroup(i, "r", DIRS - 1, dr_part)
+                    product_grouped(i, "r", "r", "c", d, COLS - SIDE if d == DIRS - 1 else COLS)
+                side_regroup(i, "r", DIRS - 1, dr_part)
             if i + 2 < n_chunks:
                 load_gate(i + 2, "c", C)
                 load_agg(i)
@@ -572,13 +570,14 @@ def tile_graphconvolution_pb_v_kernel(
         passes(last, Z)
         store(last, Z)
         for d in range(DIRS):
-            product_grouped(last, "r", "r", "c", d)
             quantise_gate(last, C, "c", d)
             multiply(last, C, d)
+            product_grouped(last, "r", "r", "c", d)
             if d > 0:
                 quantise_gate(last, R, "r", d - 1)
                 multiply(last, R, d - 1)
-        store(last, C)
+            if d == DIRS - 1:
+                store(last, C)
         quantise_gate(last, R, "r", DIRS - 1)
         multiply(last, R, DIRS - 1)
         store(last, R, shared_out=True)

@@ -28,10 +28,10 @@ COL_BLOCKS = FEAT // COLS
 M_TILE = 128
 M_TILES = COLS // M_TILE
 BANK = 512
-WIDTH = PACK * COLS
-HALVES = WIDTH // BANK
+HALVES = PACK * COLS // BANK
 RUN = 4
-SIDE = 96
+SIDE_Z = 192
+SIDE_N = 64
 
 FLOPS = 2 * DIRS * NODES * GATES * FEAT * FEAT
 BYTES = (
@@ -49,14 +49,15 @@ def tile_graphconvolution_pb_v_kernel(
     nc = tc.nc
     chunks = [(cb, nb) for cb in range(COL_BLOCKS) for nb in range(NODE_BLOCKS)]
     n_chunks = len(chunks)
-    all_dirs = slice(0, DIRS)
+    last = n_chunks - 1
     with ExitStack() as ctx:
         gate_pool = ctx.enter_context(tc.tile_pool(name="gate", bufs=2))
         node_pool = ctx.enter_context(tc.tile_pool(name="node", bufs=2))
-        work_pool = ctx.enter_context(tc.tile_pool(name="work", bufs=2))
+        work_pool = ctx.enter_context(tc.tile_pool(name="work", bufs=1))
+        part_pool = ctx.enter_context(tc.tile_pool(name="part", bufs=2))
         grouped_pool = ctx.enter_context(tc.tile_pool(name="grouped", bufs=3 * DIRS))
         agg_pool = ctx.enter_context(tc.tile_pool(name="agg", bufs=DIRS))
-        mx_pool = ctx.enter_context(tc.tile_pool(name="dgi_mx", bufs=2 * GATES * DIRS))
+        mx_pool = ctx.enter_context(tc.tile_pool(name="dgi_mx", bufs=22))
         keep_pool = ctx.enter_context(tc.tile_pool(name="keep", bufs=1))
         result_pool = ctx.enter_context(tc.tile_pool(name="result", bufs=4))
         psum = ctx.enter_context(tc.psum_pool(name="psum", bufs=1))
@@ -84,7 +85,15 @@ def tile_graphconvolution_pb_v_kernel(
         def tokens(b):
             if b is None:
                 return slice(0, PACK)
+            if isinstance(b, slice):
+                return b
             return slice(b * PACK // HALVES, (b + 1) * PACK // HALVES)
+
+        def flat(held, b=None):
+            return held[:, tokens(b)].rearrange("p j o -> p (j o)")
+
+        def bank(kind, k, dtype=F32, width=BANK):
+            return psum.tile([P, width], dtype, name="%s%d" % (kind, k), tag="%s%d" % (kind, k))
 
         def load_node(i, name, dtype, src, bufs, b=None):
             if name not in state[i]:
@@ -93,89 +102,49 @@ def tile_graphconvolution_pb_v_kernel(
 
         def load_h(i, b=None):
             rows, cols = where(i)
-            load_node(i, "h", BF16, x[rows, 0, cols], n_chunks, b)
+            load_node(i, "h", BF16, x[rows, 0, cols], 2, b)
 
-        def load_gate(i, name, gate, dirs=(0, 1, 2), b=None):
-            cb, nb = chunks[i]
-            rows, cols = where(i)
-            if name not in state[i]:
-                state[i][name] = gate_pool.tile([P, DIRS, PACK, COLS], F32, name=name, tag=name)
-            first = gate * FEAT + cb * COLS
-            for d in dirs:
-                nc.sync.dma_start(
-                    out=state[i][name][:, d, tokens(b)],
-                    in_=rows_view(gates[d, 0, rows, first : first + COLS])[:, tokens(b), :],
-                )
-
-        def load_dh_inputs(i, b=None):
+        def load_gt(i, b=None):
             rows, cols = where(i)
             load_node(i, "g", BF16, grad_out[rows, 0, cols], 2, b)
-            load_node(i, "gt", F32, t[rows, 0, cols], 2, b)
+            load_node(i, "t", F32, t[rows, 0, cols], 2, b)
 
         def load_hn(i):
             rows, cols = where(i)
             load_node(i, "h_n", F32, hn[0, rows, cols], 2)
 
-        def load_r(i):
-            load_gate(i, "r", R)
-            load_hn(i)
-
-        def load_agg(i, dirs=(0, 1, 2)):
+        def load_gate(i, name, gate, d, b=None):
             cb, nb = chunks[i]
             rows, cols = where(i)
-            if cb > 0:
-                return
-            state[i].setdefault("agg_rows", [])
-            for d in dirs:
-                agg_rows = agg_pool.tile([P, PACK, FEAT], BF16, name="agg_rows", tag="agg_rows")
-                nc.sync.dma_start(out=agg_rows[:], in_=rows_view(agg[d, 0, rows, :]))
-                state[i]["agg_rows"].append(agg_rows)
-
-        def pieces(split):
-            if split:
-                return [slice(d, d + 1) for d in range(DIRS)]
-            return [all_dirs]
-
-        def wide(held, ds, b=None):
-            return held[:, ds, tokens(b)].rearrange("p d j o -> p d (j o)")
-
-        def flat(held, b=None):
-            return held[:, tokens(b)].rearrange("p j o -> p (j o)")
-
-        def shared(held, ds, b=None):
-            n = ds.stop - ds.start
-            width = WIDTH if b is None else BANK
-            return flat(held, b).unsqueeze(1).to_broadcast([P, n, width])
-
-        def regroup(pool, values, tag, factor):
-            width = values.shape[2]
-            grouped = pool.tile([P, width, PACK], BF16, name=tag, tag=tag, align_bytes=64)
-            nc.scalar.activation(
-                out=grouped[:].rearrange("p (c i) j -> p c j i", i=RUN),
-                in_=values.rearrange("p j (c i) -> p c j i", i=RUN),
-                func=ACT.Copy, scale=factor,
-            )
-            return grouped
-
-        def quantise(grouped, x4_dtype, codes, scales):
-            nc.vector.quantize_mx(
-                out=codes.bitcast(x4_dtype), scales=scales,
-                in_=grouped[:].rearrange("p o j -> p (o j)"),
+            key = (name, d)
+            if key not in state[i]:
+                state[i][key] = gate_pool.tile([P, PACK, COLS], F32, name=name, tag="%s%d" % (name, d))
+            first = gate * FEAT + cb * COLS
+            nc.sync.dma_start(
+                out=state[i][key][:, tokens(b)],
+                in_=rows_view(gates[d, 0, rows, first : first + COLS])[:, tokens(b), :],
             )
 
-        def bank(kind, k, dtype=F32, width=BANK):
-            return psum.tile([P, width], dtype, name="%s%d" % (kind, k), tag="%s%d" % (kind, k))
+        def load_cz(i, d, b=None):
+            load_gate(i, "c", C, d, b)
+            load_gate(i, "z", Z, d, b)
 
-        def transpose_h(i):
+        def load_agg(i, d):
+            rows, cols = where(i)
+            agg_rows = agg_pool.tile([P, PACK, FEAT], BF16, name="agg_rows", tag="agg_rows", bufs=DIRS)
+            nc.sync.dma_start(out=agg_rows[:], in_=rows_view(agg[d, 0, rows, :]))
+            state[i].setdefault("agg_rows", []).append(agg_rows)
+
+        def transpose_h(i, spare):
             h = state[i]["h"]
-            turned = bank("m", i, BF16, 2 * BANK)
+            turned = bank("m", spare, BF16, 2 * BANK)
             for fb in range(M_TILES):
                 for j in range(PACK):
                     k = fb * PACK + j
                     nc.tensor.transpose(
                         turned[:, k * P : (k + 1) * P], h[:, j, fb * P : (fb + 1) * P], identity_bf[:]
                     )
-            h_t = work_pool.tile([P, M_TILES, PACK, P], F32, name="h_t", tag="h_t", bufs=n_chunks - 1)
+            h_t = work_pool.tile([P, M_TILES, PACK, P], F32, name="h_t", tag="h_t", bufs=2)
             nc.scalar.copy(out=h_t[:].rearrange("p f j q -> p (f j q)"), in_=turned[:])
             state[i]["h_t"] = h_t
 
@@ -183,9 +152,7 @@ def tile_graphconvolution_pb_v_kernel(
             st = state[i]
             diff = bank("a", b)
             nc.tensor.matmul(
-                out=diff[:], lhsT=minus_identity[:],
-                rhs=st["c"][:, d].rearrange("p j o -> p (j o)")[:, b * BANK : (b + 1) * BANK],
-                start=True, stop=False,
+                out=diff[:], lhsT=minus_identity[:], rhs=flat(st[("c", d)], b), start=True, stop=False,
             )
             per_bank = PACK // HALVES
             for jj in range(per_bank):
@@ -198,117 +165,184 @@ def tile_graphconvolution_pb_v_kernel(
                     )
             return diff
 
-        def new_zch(i):
-            state[i]["zch"] = work_pool.tile([P, DIRS, PACK, COLS], F32, name="zch", tag="zch")
+        diffs = {}
 
-        def gated_difference(i, d, b, diff):
-            st = state[i]
-            part = slice(b * BANK, (b + 1) * BANK)
-            nc.vector.tensor_tensor(
-                out=st["zch"][:, d].rearrange("p j o -> p (j o)")[:, part],
-                in0=st["z"][:, d].rearrange("p j o -> p (j o)")[:, part],
-                in1=diff[:], op=ALU.mult,
-            )
+        def differences(i, d):
+            if i < n_chunks:
+                for b in range(HALVES):
+                    diffs[b] = difference(i, d, b)
 
-        def add_transposed(tot_t, b, held, ds, first, last):
-            blocks = [(j, fb) for j in range(tokens(b).start, tokens(b).stop) for fb in range(M_TILES)]
-            for d in range(ds.start, ds.stop):
-                for k, (j, fb) in enumerate(blocks):
-                    nc.tensor.matmul(
-                        out=tot_t[:, k * P : (k + 1) * P],
-                        lhsT=held[:, d, j, fb * P : (fb + 1) * P],
-                        rhs=identity[:],
-                        is_transpose=True,
-                        start=(first and d == ds.start and k == 0),
-                        stop=(last and d == ds.stop - 1 and k == len(blocks) - 1),
-                    )
+        def blocks(b):
+            return [(j, fb) for j in range(tokens(b).start, tokens(b).stop) for fb in range(M_TILES)]
 
-        def square(i, name, bias, b=None):
-            held = state[i][name]
-            nc.scalar.activation(
-                out=wide(held, all_dirs, b), in_=wide(held, all_dirs, b), func=ACT.Square, bias=bias
-            )
-
-        def tot_back(i, b):
-            st = state[i]
-            tot_t_sb = work_pool.tile([P, BANK], F32, name="tot_t_sb", tag="tot_t_sb")
-            nc.scalar.copy(out=tot_t_sb[:], in_=st["tot_t"][b][:])
-            tot = bank("x", b)
-            for k in range(BANK // P):
-                nc.tensor.transpose(
-                    tot[:, k * P : (k + 1) * P], tot_t_sb[:, k * P : (k + 1) * P], identity[:]
+        def add_transposed(tot_t, b, held, first, stop):
+            todo = blocks(b)
+            for k, (j, fb) in enumerate(todo):
+                nc.tensor.matmul(
+                    out=tot_t[:, k * P : (k + 1) * P], lhsT=held[:, j, fb * P : (fb + 1) * P],
+                    rhs=identity[:], is_transpose=True,
+                    start=(first and k == 0), stop=(stop and k == len(todo) - 1),
                 )
-            st["tot"][b] = tot
 
-        def mask(i, b):
+        def add_c(i, d, halves=(0, 1)):
+            if i < n_chunks:
+                for b in halves:
+                    if d == 0:
+                        state[i][("tot_t", b)] = bank("x", b)
+                    add_transposed(state[i][("tot_t", b)], b, state[i][("c", d)], d == 0, False)
+
+        def add_a(i, d, halves=(0, 1)):
+            if i < n_chunks:
+                for b in halves:
+                    add_transposed(state[i][("tot_t", b)], b, state[i][("a", d)], False, d == DIRS - 1)
+
+        def turn_gt(i, b, kind, k, part=None):
             st = state[i]
+            source = st[("gt", b if part is None else None)]
+            turned = bank(kind, k)
+            todo = blocks(b if part is None else part)
+            width = len(todo) * P
+            for k, (j, fb) in enumerate(todo):
+                nc.tensor.transpose(
+                    turned[:, k * P : (k + 1) * P], source[:, j, fb * P : (fb + 1) * P], identity[:]
+                )
+            gt_t = work_pool.tile([P, BANK], F32, name="gt_t", tag="gt_t%d" % (b % 2))
+            nc.scalar.mul(out=gt_t[:, :width], in_=turned[:, :width], mul=-1.0)
+            st[("gt_t", b)] = gt_t
+
+        def turn_dh(i, b, where_to=None, width=BANK):
+            st = state[i]
+            kind, number = ("x", b) if where_to is None else where_to
+            dh = bank(kind, number)
+            for k in range(width // P):
+                nc.tensor.transpose(
+                    dh[:, k * P : (k + 1) * P], st[("dh_t", b)][:, k * P : (k + 1) * P], identity[:]
+                )
+            st[("dh", b)] = dh[:, :width]
+
+        def times_t(i, b=None):
+            st = state[i]
+            st[("gt", None)] = st["t"]
+            nc.vector.tensor_tensor(out=flat(st["t"], b), in0=flat(st["g"], b), in1=flat(st["t"], b), op=ALU.mult)
+
+        def mask(i, b, width=BANK):
+            st = state[i]
+            dh_t = work_pool.tile([P, BANK], F32, name="dh_t", tag="dh_t%d" % (b % 2))
             nc.vector.scalar_tensor_tensor(
-                out=flat(st["dh"], b), in0=st["tot"][b][:], scalar=0.0, in1=flat(st["gt"], b),
+                out=dh_t[:, :width], in0=st[("tot_t", b)][:, :width], scalar=0.0, in1=st[("gt_t", b)][:, :width],
                 op0=ALU.is_gt, op1=ALU.mult,
             )
+            st[("dh_t", b)] = dh_t
 
-        def regroup_agg(i, d):
+        def new_a(i, d):
+            if ("a", d) not in state[i]:
+                state[i][("a", d)] = gate_pool.tile([P, PACK, COLS], F32, name="a", tag="a%d" % d)
+
+        def gated_difference(i, d):
+            if i < n_chunks:
+                st = state[i]
+                new_a(i, d)
+                for b in range(HALVES):
+                    nc.vector.tensor_tensor(
+                        out=flat(st[("a", d)], b), in0=flat(st[("z", d)], b), in1=diffs[b][:], op=ALU.mult,
+                    )
+
+        def make_u(i, d, b, dh=None):
             st = state[i]
-            st.setdefault("agg_grouped", []).append(regroup(agg_pool, st["agg_rows"][d][:], "agg_grouped", 1.0))
-
-        def quantise_agg(i):
-            cb, nb = chunks[i]
-            if cb > 0:
-                return
-            for d in range(DIRS):
-                quantise(
-                    state[i]["agg_grouped"][d], E4M3_X4,
-                    agg_codes[:, nb, d, :], agg_scales[:, nb, d, :],
-                )
-
-        def product(i, out_name, in0_name, scalar, op0, in1_name, ds, in1_shared=False, b=None):
-            st = state[i]
-            in1 = shared(st[in1_name], ds, b) if in1_shared else wide(st[in1_name], ds, b)
             nc.vector.scalar_tensor_tensor(
-                out=wide(st[out_name], ds, b), in0=wide(st[in0_name], ds, b), scalar=scalar, in1=in1,
-                op0=op0, op1=ALU.mult,
+                out=flat(st[("z", d)], b), in0=flat(st[("z", d)], b), scalar=1.0, in1=st[("dh", b)] if dh is None else dh,
+                op0=ALU.subtract, op1=ALU.mult,
             )
 
-        def side_product(i, in0_name, in1_name, d):
+        def make_dc(i, d, b=None):
             st = state[i]
-            part = work_pool.tile([P, PACK, SIDE], F32, name="part", tag="part")
-            nc.gpsimd.tensor_tensor(
-                out=part[:], in0=st[in0_name][:, d, :, COLS - SIDE :], in1=st[in1_name][:, d, :, COLS - SIDE :],
-                op=ALU.mult,
-            )
-            return part
-
-        def side_regroup(i, name, d, part):
-            grouped = state[i]["grouped_" + name][d]
-            nc.scalar.activation(
-                out=grouped[:, COLS - SIDE :, :].rearrange("p (c i) j -> p c j i", i=RUN),
-                in_=part[:].rearrange("p j (c i) -> p c j i", i=RUN),
-                func=ACT.Copy, scale=1.0,
+            nc.vector.scalar_tensor_tensor(
+                out=flat(st[("a", d)], b), in0=flat(st[("c", d)], b), scalar=1.0, in1=flat(st[("z", d)], b),
+                op0=ALU.subtract, op1=ALU.mult,
             )
 
-        def product_grouped(i, name, in0_name, in1_name, d, width=COLS, b=None):
+        def make_e(i, d):
             st = state[i]
-            made = st.setdefault("grouped_" + name, [])
-            if len(made) <= d:
-                made.append(
-                    grouped_pool.tile([P, COLS, PACK], BF16, name="grouped", tag="grouped", align_bytes=64)
-                )
+            nc.vector.scalar_tensor_tensor(
+                out=flat(st[("r", d)]), in0=flat(st[("r", d)]), scalar=0.25, in1=flat(st["h_n"]),
+                op0=ALU.subtract, op1=ALU.mult,
+            )
+
+        def new_grouped(i, name, d):
+            key = ("grouped_" + name, d)
+            if key not in state[i]:
+                state[i][key] = grouped_pool.tile([P, COLS, PACK], BF16, name="grouped", tag="grouped", align_bytes=64)
+            return state[i][key]
+
+        def product_grouped(i, name, in0, in1, d, width=COLS, b=None):
+            st = state[i]
+            made = new_grouped(i, name, d)
             nc.vector.tensor_tensor(
-                out=made[d][:, :width, tokens(b)].rearrange("p (c i) j -> p c j i", i=RUN),
-                in0=st[in0_name][:, d, tokens(b), :width].rearrange("p j (c i) -> p c j i", i=RUN),
-                in1=st[in1_name][:, d, tokens(b), :width].rearrange("p j (c i) -> p c j i", i=RUN),
+                out=made[:, :width, tokens(b)].rearrange("p (c i) j -> p c j i", i=RUN),
+                in0=st[(in0, d)][:, tokens(b), :width].rearrange("p j (c i) -> p c j i", i=RUN),
+                in1=st[(in1, d)][:, tokens(b), :width].rearrange("p j (c i) -> p c j i", i=RUN),
                 op=ALU.mult,
             )
 
-        def regroup_gate(i, name, d):
-            st = state[i]
-            st.setdefault("grouped_" + name, []).append(regroup(grouped_pool, st[name][:, d], "grouped", -1.0))
+        def quantise(grouped, x4_dtype, codes, scales):
+            nc.vector.quantize_mx(
+                out=codes.bitcast(x4_dtype), scales=scales, in_=grouped[:].rearrange("p o j -> p (o j)"),
+            )
 
         def quantise_gate(i, gate, name, d):
             codes = mx_pool.tile([P, COLS], U32, name="codes", tag="codes", align_bytes=64)
             scales = mx_pool.tile([P, COLS], U8, name="scales", tag="scales", align_bytes=64)
-            quantise(state[i]["grouped_" + name][d], E5M2_X4, codes[:], scales[:])
+            quantise(state[i][("grouped_" + name, d)], E5M2_X4, codes[:], scales[:])
             state[i][(gate, d)] = (codes, scales)
+
+        def quantise_agg(i):
+            cb, nb = chunks[i]
+            for d in range(DIRS):
+                quantise(state[i]["agg_grouped"][d], E4M3_X4, agg_codes[:, nb, d, :], agg_scales[:, nb, d, :])
+
+        def square(i, name, d, bias, b=None):
+            held = state[i][(name, d)]
+            nc.scalar.activation(out=flat(held, b), in_=flat(held, b), func=ACT.Square, bias=bias)
+
+        def regroup(grouped, values, factor):
+            nc.scalar.activation(
+                out=grouped.rearrange("p (c i) j -> p c j i", i=RUN),
+                in_=values.rearrange("p j (c i) -> p c j i", i=RUN),
+                func=ACT.Copy, scale=factor,
+            )
+
+        def regroup_dc(i, d):
+            regroup(new_grouped(i, "c", d)[:], state[i][("a", d)][:], -1.0)
+
+        def regroup_agg(i, d):
+            grouped = agg_pool.tile([P, FEAT, PACK], BF16, name="agg_grouped", tag="agg_grouped", align_bytes=64)
+            regroup(grouped[:], state[i]["agg_rows"][d][:], 1.0)
+            state[i].setdefault("agg_grouped", []).append(grouped)
+
+        def side_gt(i, held, b=None):
+            st = state[i]
+            nc.gpsimd.tensor_tensor(out=flat(held, b), in0=flat(st["g"], b), in1=flat(st["t"], b), op=ALU.mult)
+            for half in range(HALVES) if b is None else (b,):
+                st[("gt", half)] = held
+
+        def side_product(i, in0, in1, d, width, held=None):
+            st = state[i]
+            if held is None:
+                part = part_pool.tile([P, PACK, SIDE_Z], F32, name="part", tag="part")
+                part = part[:, :, :width]
+            else:
+                part = held[:, :, :width]
+            nc.gpsimd.tensor_tensor(
+                out=part, in0=st[(in0, d)][:, :, COLS - width :], in1=st[(in1, d)][:, :, COLS - width :], op=ALU.mult,
+            )
+            return part
+
+        def side_regroup(i, name, d, part, width):
+            regroup(new_grouped(i, name, d)[:, COLS - width :, :], part, 1.0)
+
+        def open_acc(gate, kind, first):
+            for m in range(M_TILES):
+                acc[(gate, m)] = bank(kind, first + m)
 
         def multiply(i, gate, d):
             cb, nb = chunks[i]
@@ -317,20 +351,22 @@ def tile_graphconvolution_pb_v_kernel(
                 m_cols = slice(m * M_TILE, (m + 1) * M_TILE)
                 nc.tensor.matmul_mx(
                     out=acc[(gate, m)][:],
-                    lhsT=codes[:, m_cols].bitcast(E5M2_X4),
-                    lhsT_scale=scales[:, m_cols],
-                    rhs=agg_codes[:, nb, d, :].bitcast(E4M3_X4),
-                    rhs_scale=agg_scales[:, nb, d, :],
-                    start=(nb == 0 and d == 0),
-                    stop=(nb == NODE_BLOCKS - 1 and d == DIRS - 1),
+                    lhsT=codes[:, m_cols].bitcast(E5M2_X4), lhsT_scale=scales[:, m_cols],
+                    rhs=agg_codes[:, nb, d, :].bitcast(E4M3_X4), rhs_scale=agg_scales[:, nb, d, :],
+                    start=(nb == 0 and d == 0), stop=(nb == NODE_BLOCKS - 1 and d == DIRS - 1),
                 )
 
-        def store(i, gate, shared_out=False):
+        def passes(i, gate):
+            for d in range(DIRS):
+                multiply(i, gate, d)
+
+        def store(i, gate, shared_out=False, spare=False):
             cb, nb = chunks[i]
-            if nb < NODE_BLOCKS - 1:
-                return
             for m in range(M_TILES):
-                result = result_pool.tile([M_TILE, FEAT], F32, name="result", tag="result")
+                if spare:
+                    result = part_pool.tile([M_TILE, FEAT], F32, name="part", tag="part")
+                else:
+                    result = result_pool.tile([M_TILE, FEAT], F32, name="result", tag="result")
                 if shared_out and m == 0:
                     nc.vector.tensor_copy(out=result[:], in_=acc[(gate, m)][:])
                 else:
@@ -338,241 +374,275 @@ def tile_graphconvolution_pb_v_kernel(
                 first = gate * FEAT + cb * COLS + m * M_TILE
                 nc.sync.dma_start(out=out[first : first + M_TILE, :], in_=result[:])
 
+        pieces = [slice(0, 1), slice(1, 2), slice(2, 4)]
+        for b in pieces:
+            load_h(0, b)
+            for d in range(DIRS):
+                load_gate(0, "c", C, d, b)
+            load_gt(0, b)
+            for d in range(DIRS):
+                load_gate(0, "z", Z, d, b)
+        load_h(1)
+        load_gt(1)
+        for d in range(DIRS):
+            load_cz(1, d)
+        load_gate(0, "r", R, 0)
+        load_hn(0)
+        load_gate(0, "r", R, 1)
+        load_gate(0, "r", R, 2)
+        load_h(2)
 
-        def add_c_to_tot(i, d, halves=(0, 1)):
-            if i >= n_chunks:
-                return
-            st = state[i]
-            for b in halves:
-                if d == 0:
-                    st.setdefault("tot_t", {})[b] = bank("x", b)
-                add_transposed(st["tot_t"][b], b, st["c"], slice(d, d + 1), d == 0, False)
+        tot_banks = [("m", 0), ("m", 1), ("x", 1)]
+        gt_banks = [("a", 0), ("a", 1), ("m", 2)]
+        st0 = state[0]
 
-        def add_to_tot(i, ds, halves=(0, 1)):
-            st = state[i]
-            for b in halves:
-                add_transposed(st["tot_t"][b], b, st["zch"], ds, False, ds.stop == DIRS)
+        def first_c(p):
+            b = pieces[p]
+            tot = bank(tot_banks[p][0], tot_banks[p][1])
+            st0[("tot_t", p)] = tot
+            for d in range(DIRS):
+                add_transposed(tot, b, st0[("c", d)], d == 0, False)
 
-        def new_dh(i):
-            state[i]["dh"] = work_pool.tile([P, PACK, COLS], F32, name="dh", tag="dh", bufs=1)
-            state[i]["tot"] = {}
-
-        def times_t(i, b=None):
-            st = state[i]
-            nc.vector.scalar_tensor_tensor(
-                out=flat(st["gt"], b), in0=flat(st["g"], b), scalar=-1.0, in1=flat(st["gt"], b),
-                op0=ALU.mult, op1=ALU.mult,
+        def first_difference(p, d):
+            new_a(0, d)
+            nc.vector.tensor_tensor(
+                out=flat(st0[("a", d)], pieces[p]), in0=flat(st0["h"], pieces[p]), in1=flat(st0[("c", d)], pieces[p]),
+                op=ALU.subtract,
             )
 
-        def times_hn(i):
-            product(i, "r", "r", 0.25, ALU.subtract, "h_n", all_dirs, in1_shared=True)
+        def first_a(p, d):
+            b = pieces[p]
+            nc.vector.tensor_tensor(
+                out=flat(st0[("a", d)], b), in0=flat(st0[("z", d)], b),
+                in1=flat(st0[("a", d)], b), op=ALU.mult,
+            )
+            add_transposed(st0[("tot_t", p)], b, st0[("a", d)], False, d == DIRS - 1)
 
-        def open_acc(gate, kind, first):
-            for m in range(M_TILES):
-                acc[(gate, m)] = bank(kind, first + m)
-
-        def passes(i, gate):
+        def first_u(p):
             for d in range(DIRS):
-                multiply(i, gate, d)
+                make_u(0, d, pieces[p], st0[("dh", p)])
 
-        diffs = {}
+        def first_mask(p):
+            width = (pieces[p].stop - pieces[p].start) * COLS
+            mask(0, p, width)
+            turn_dh(0, p, tot_banks[p], width)
 
-        def differences(i, d):
-            if i < n_chunks:
-                for b in range(HALVES):
-                    diffs[b] = difference(i, d, b)
-
-        def gated_differences(i, d):
-            if i < n_chunks:
-                for b in range(HALVES):
-                    gated_difference(i, d, b, diffs[b])
-                if d + 1 < DIRS:
-                    differences(i, d + 1)
-                add_to_tot(i, slice(d, d + 1))
-                if d + 1 < DIRS:
-                    add_c_to_tot(i, d + 1)
-
-        for b in range(HALVES):
-            load_h(0, b)
-            load_gate(0, "c", C, b=b)
-            load_gate(0, "z", Z, b=b)
-            load_dh_inputs(0, b)
-        load_h(1)
-        load_gate(1, "c", C, (0,))
-        load_gate(1, "z", Z, (0,))
-        load_gate(0, "r", R)
-        load_gate(1, "c", C, (1,))
-        load_gate(1, "z", Z, (1,))
-        load_hn(0)
-        load_gate(1, "c", C, (2,))
-        load_gate(1, "z", Z, (2,))
-        load_h(2)
-        load_r(1)
-        load_dh_inputs(1)
-        load_h(3)
-
-        st = state[0]
-        new_zch(0)
-        new_dh(0)
-
-        def first_differences(b):
-            for ds in pieces(True):
-                nc.vector.tensor_tensor(
-                    out=wide(st["zch"], ds, b), in0=shared(st["h"], ds, b), in1=wide(st["c"], ds, b),
-                    op=ALU.subtract,
-                )
-            for ds in pieces(True):
-                nc.scalar.activation(
-                    out=wide(st["c"], ds, b), in_=wide(st["c"], ds, b), func=ACT.Square,
-                )
-
-        def first_gated(b):
-            for ds in pieces(True):
-                nc.vector.tensor_tensor(
-                    out=wide(st["zch"], ds, b), in0=wide(st["z"], ds, b), in1=wide(st["zch"], ds, b),
-                    op=ALU.mult,
-                )
-                add_to_tot(0, ds, (b,))
-            times_t(0, b)
-            tot_back(0, b)
-
-        def first_products(b):
+        def first_dz(p):
             for d in range(DIRS):
-                product_grouped(0, "zch", "z", "zch", d, COLS, b)
-            product(0, "c", "c", 1.0, ALU.subtract, "z", all_dirs, b=b)
+                product_grouped(0, "z", "z", "a", d, COLS, pieces[p])
 
-        def first_dh(b):
-            mask(0, b)
-            product(0, "z", "z", 1.0, ALU.subtract, "dh", all_dirs, in1_shared=True, b=b)
-
+        first_c(0)
         for d in range(DIRS):
-            add_c_to_tot(0, d, (0,))
-        first_differences(0)
-        first_gated(0)
+            first_difference(0, d)
+        times_t(0, pieces[0])
+        turn_gt(0, 0, "a", 0, pieces[0])
         for d in range(DIRS):
-            add_c_to_tot(0, d, (1,))
-        first_differences(1)
-        first_dh(0)
-        first_gated(1)
-        transpose_h(1)
+            square(0, "c", d, 0.0, pieces[0])
+        for d in range(DIRS):
+            first_a(0, d)
+        first_c(1)
+        for d in range(DIRS):
+            first_difference(1, d)
+        first_mask(0)
+        times_t(0, pieces[1])
+        turn_gt(0, 1, "a", 1, pieces[1])
+        for d in range(DIRS):
+            square(0, "c", d, 0.0, pieces[1])
+        first_u(0)
+        for d in range(DIRS):
+            first_a(1, d)
+        first_dz(0)
+        first_mask(1)
+        for d in range(DIRS):
+            make_dc(0, d, pieces[0])
+        first_u(1)
+        first_c(2)
+        for d in range(DIRS):
+            first_difference(2, d)
+        times_t(0, pieces[2])
+        turn_gt(0, 2, "m", 2, pieces[2])
+        for d in range(DIRS):
+            square(0, "c", d, 0.0, pieces[2])
+        product_grouped(0, "z", "z", "a", 0, COLS, pieces[1])
+        transpose_h(1, 3)
+        for d in range(DIRS):
+            first_a(2, d)
+        for d in range(DIRS - 1):
+            product_grouped(0, "z", "z", "a", d + 1, COLS, pieces[1])
+        make_dc(0, 0, pieces[1])
+        first_mask(2)
+        add_c(1, 0, (0,))
         differences(1, 0)
-        first_products(0)
-        first_dh(1)
-        square(0, "r", -0.5)
-        add_c_to_tot(1, 0)
-        new_zch(1)
+        make_dc(0, 1, pieces[1])
+        make_dc(0, 2, pieces[1])
+        side_gt(1, st0[("c", 2)], 0)
+        turn_gt(1, 0, "m", 0)
+        first_u(2)
         for d in range(DIRS):
-            product_grouped(0, "zch", "z", "zch", d, COLS, 1)
-        gated_differences(1, 0)
-        product(0, "c", "c", 1.0, ALU.subtract, "z", all_dirs, b=1)
-        load_gate(2, "z", Z)
+            product_grouped(0, "z", "z", "a", d, COLS, pieces[2])
+            if d == 1:
+                gated_difference(1, 0)
+                differences(1, 1)
         for d in range(DIRS):
-            regroup_gate(0, "c", d)
-        times_hn(0)
+            make_dc(0, d, pieces[2])
+            regroup_dc(0, d)
+            if d == 1:
+                side_gt(1, st0[("c", 1)], 1)
+                gated_difference(1, 1)
+                turn_gt(1, 1, "m", 1)
+                differences(1, 2)
+                square(0, "r", 0, -0.5)
+        add_c(1, 0, (1,))
+        add_a(1, 0)
+        add_c(1, 1)
+        load_cz(2, 0)
+        load_gt(2)
+        for d in range(DIRS):
+            load_gate(1, "r", R, d)
+        load_hn(1)
+        load_cz(2, 1)
+        load_cz(2, 2)
+        load_h(3)
+        for d in range(DIRS):
+            load_agg(0, d)
+        add_a(1, 1)
+        add_c(1, 2)
+        for d in range(1, DIRS):
+            square(0, "r", d, -0.5)
+        for d in range(DIRS):
+            quantise_gate(0, Z, "z", d)
+        make_e(0, 0)
+        gated_difference(1, 2)
+        add_a(1, 2)
+        for d in range(DIRS):
+            quantise_gate(0, C, "c", d)
+        square(1, "c", 0, 0.0)
+        square(1, "c", 1, 0.0)
 
-        for i in range(n_chunks):
+        for i in range(1, n_chunks):
             nxt = i + 1
             has_next = nxt < n_chunks
-            split = not has_next
-            agg_due = i > 0 and chunks[i - 1][0] == 0
-
-            if i > 0:
-                if has_next:
-                    add_c_to_tot(nxt, 0)
-                    new_zch(nxt)
-                if i > 0:
-                    square(i, "c", 0.0)
-                product(i, "z", "z", 1.0, ALU.subtract, "dh", all_dirs, in1_shared=True)
-                if i == 0:
-                    square(0, "r", -0.5)
-                if agg_due:
-                    for d in range(DIRS):
-                        regroup_agg(i - 1, d)
-                if i > 0 and has_next:
-                    square(nxt, "r", -0.5)
-                if has_next:
-                    dz_part = side_product(i, "z", "zch", DIRS - 1)
-                gated_differences(nxt, 0)
-                for d in range(DIRS):
-                    shared_work = has_next and d == DIRS - 1
-                    product_grouped(i, "zch", "z", "zch", d, COLS - SIDE if shared_work else COLS)
-                if has_next:
-                    side_regroup(i, "zch", DIRS - 1, dz_part)
-                for ds in pieces(split):
-                    product(i, "c", "c", 1.0, ALU.subtract, "z", ds)
-                    if split:
-                        regroup_gate(i, "c", ds.start)
-                if i + 2 < n_chunks:
-                    load_gate(i + 2, "z", Z)
-                if not split:
-                    for d in range(DIRS):
-                        regroup_gate(i, "c", d)
             if has_next:
-                dr_part = side_product(i, "r", "c", DIRS - 1)
-            gated_differences(nxt, 1)
-            if i == 0:
-                square(nxt, "r", -0.5)
-                transpose_h(2)
-                transpose_h(3)
-            if agg_due:
-                quantise_agg(i - 1)
-            for d in range(DIRS):
-                quantise_gate(i, Z, "zch", d)
-            if has_next:
-                for d in range(DIRS):
-                    product_grouped(i, "r", "r", "c", d, COLS - SIDE if d == DIRS - 1 else COLS)
-                side_regroup(i, "r", DIRS - 1, dr_part)
-            if i + 2 < n_chunks:
-                load_gate(i + 2, "c", C)
-                load_agg(i)
-                load_gate(i + 2, "r", R)
-                load_dh_inputs(i + 2)
-                load_hn(i + 2)
+                load_gate(nxt, "r", R, 0)
+                load_gate(nxt, "r", R, 2)
+            if has_next and i > 1:
+                side_gt(nxt, state[i - 1][("r", 1)])
+            for b in range(HALVES):
+                mask(i, b)
+            for b in range(HALVES):
+                turn_dh(i, b)
+            square(i, "c", 2, 0.0)
             if i == 1:
+                for d in range(1, DIRS):
+                    make_e(0, d)
+                transpose_h(2, 2)
+                differences(2, 0)
+                for d in (0, 2, 1):
+                    product_grouped(0, "r", "r", "a", d)
+                side_gt(nxt, state[0][("r", 1)])
+            elif has_next:
+                gated_difference(nxt, 0)
+                differences(nxt, 1)
+            if not has_next:
+                quantise_gate(i - 1, R, "r", 2)
+                quantise_gate(i - 1, R, "r", 1)
+            for d in range(DIRS):
+                square(i, "r", d, -0.5)
+            for d, b in ((2, 0), (0, 0), (2, 1), (0, 1), (1, 0), (1, 1)):
+                make_u(i, d, b)
+            part_z = side_product(i, "z", "a", 2, SIDE_Z)
+            if i == 1:
+                gated_difference(nxt, 0)
+                differences(nxt, 1)
+                quantise_gate(0, R, "r", 0)
+            if has_next:
+                for b in range(HALVES):
+                    turn_gt(nxt, b, "x", b)
+                load_gate(nxt, "r", R, 1)
+                quantise_gate(i - 1, R, "r", 2)
+                quantise_gate(i - 1, R, "r", 1)
+            if i > 1:
+                quantise_agg(i - 2)
+            if i == 2:
                 open_acc(Z, "m", 0)
                 open_acc(C, "m", 2)
                 passes(0, Z)
                 passes(0, C)
-            if i == 2:
+            if i == 1:
+                transpose_h(3, 3)
+            product_grouped(i, "z", "z", "a", 0)
+            product_grouped(i, "z", "z", "a", 1, COLS - SIDE_N if has_next else COLS)
+            product_grouped(i, "z", "z", "a", 2, COLS - SIDE_Z)
+            side_regroup(i, "z", 2, part_z, SIDE_Z)
+            add_c(nxt, 0)
+            add_a(nxt, 0)
+            add_c(nxt, 1)
+            for d in range(DIRS):
+                make_e(i, d)
+            if has_next:
+                part_z1 = side_product(i, "z", "a", 1, SIDE_N, state[i]["h_n"])
+                side_regroup(i, "z", 1, part_z1, SIDE_N)
+                gated_difference(nxt, 1)
+                differences(nxt, 2)
+                add_a(nxt, 1)
+                add_c(nxt, 2)
+            if i > 1 and has_next:
+                load_hn(nxt)
+            if i == 1:
+                load_hn(2)
+            if i == last:
                 passes(1, Z)
                 store(1, Z)
                 passes(1, C)
                 store(1, C)
-            if i == 3:
-                open_acc(Z, "m", 0)
-                open_acc(C, "m", 2)
                 open_acc(R, "a", 0)
-                passes(2, Z)
-                passes(2, C)
-                passes(2, R)
-            gated_differences(nxt, 2)
-            if has_next:
-                new_dh(nxt)
-                for b in range(HALVES):
-                    tot_back(nxt, b)
-            if i == 2:
-                open_acc(R, "m", 0)
                 passes(0, R)
                 passes(1, R)
+            for d in range(DIRS):
+                make_dc(i, d)
+                regroup_dc(i, d)
+            if not has_next:
                 store(1, R)
-            differences(i + 2, 0)
-            if has_next:
+                open_acc(R, "x", 0)
+                passes(2, R)
+                open_acc(Z, "m", 0)
+                open_acc(C, "m", 2)
+                passes(2, Z)
+                passes(2, C)
+                break
+            if i == 1:
+                load_cz(3, 0)
+                load_gt(3)
+                load_cz(3, 1)
+                load_cz(3, 2)
                 for d in range(DIRS):
-                    quantise_gate(i, C, "c", d)
-                times_t(nxt)
-                times_hn(nxt)
-                for d in range(DIRS - 1):
-                    quantise_gate(i, R, "r", d)
-                for b in range(HALVES):
-                    mask(nxt, b)
-                quantise_gate(i, R, "r", DIRS - 1)
-        last = n_chunks - 1
+                    load_agg(1, d)
+            part_r = side_product(i, "r", "a", 2, SIDE_N)
+            gated_difference(nxt, 2)
+            add_a(nxt, 2)
+            differences(nxt + 1, 0)
+            for d in range(DIRS):
+                quantise_gate(i, Z, "z", d)
+            product_grouped(i, "r", "r", "a", 0)
+            product_grouped(i, "r", "r", "a", 2, COLS - SIDE_N)
+            side_regroup(i, "r", 2, part_r, SIDE_N)
+            for d in range(DIRS):
+                regroup_agg(i - 1, d)
+            for d in range(DIRS):
+                quantise_gate(i, C, "c", d)
+            quantise_gate(i, R, "r", 0)
+            product_grouped(i, "r", "r", "a", 1)
+            square(nxt, "c", 0, 0.0)
+            square(nxt, "c", 1, 0.0)
+
+        for d in range(DIRS):
+            quantise_gate(last, Z, "z", d)
         passes(last, Z)
         store(last, Z)
         for d in range(DIRS):
             quantise_gate(last, C, "c", d)
             multiply(last, C, d)
-            product_grouped(last, "r", "r", "c", d)
+            product_grouped(last, "r", "r", "a", d)
             if d > 0:
                 quantise_gate(last, R, "r", d - 1)
                 multiply(last, R, d - 1)
@@ -580,4 +650,4 @@ def tile_graphconvolution_pb_v_kernel(
                 store(last, C)
         quantise_gate(last, R, "r", DIRS - 1)
         multiply(last, R, DIRS - 1)
-        store(last, R, shared_out=True)
+        store(last, R, True, True)

@@ -30,8 +30,7 @@ M_TILES = COLS // M_TILE
 BANK = 512
 HALVES = PACK * COLS // BANK
 RUN = 4
-SIDE_Z = 192
-SIDE_N = 64
+SIDE = 64
 
 FLOPS = 2 * DIRS * NODES * GATES * FEAT * FEAT
 BYTES = (
@@ -54,7 +53,6 @@ def tile_graphconvolution_pb_v_kernel(
         gate_pool = ctx.enter_context(tc.tile_pool(name="gate", bufs=2))
         node_pool = ctx.enter_context(tc.tile_pool(name="node", bufs=2))
         work_pool = ctx.enter_context(tc.tile_pool(name="work", bufs=1))
-        part_pool = ctx.enter_context(tc.tile_pool(name="part", bufs=2))
         grouped_pool = ctx.enter_context(tc.tile_pool(name="grouped", bufs=3 * DIRS))
         agg_pool = ctx.enter_context(tc.tile_pool(name="agg", bufs=DIRS))
         mx_pool = ctx.enter_context(tc.tile_pool(name="dgi_mx", bufs=22))
@@ -196,40 +194,41 @@ def tile_graphconvolution_pb_v_kernel(
                 for b in halves:
                     add_transposed(state[i][("tot_t", b)], b, state[i][("a", d)], False, d == DIRS - 1)
 
-        def turn_gt(i, b, kind, k, part=None):
-            st = state[i]
-            source = st[("gt", b if part is None else None)]
+        def turn(i, name, b, source, kind, k, factor):
             turned = bank(kind, k)
-            todo = blocks(b if part is None else part)
-            width = len(todo) * P
-            for k, (j, fb) in enumerate(todo):
-                nc.tensor.transpose(
-                    turned[:, k * P : (k + 1) * P], source[:, j, fb * P : (fb + 1) * P], identity[:]
-                )
-            gt_t = work_pool.tile([P, BANK], F32, name="gt_t", tag="gt_t%d" % (b % 2))
-            nc.scalar.mul(out=gt_t[:, :width], in_=turned[:, :width], mul=-1.0)
-            st[("gt_t", b)] = gt_t
+            for k, (j, fb) in enumerate(blocks(b)):
+                nc.tensor.transpose(turned[:, k * P : (k + 1) * P], source[:, j, fb * P : (fb + 1) * P], identity[:])
+            held = work_pool.tile([P, BANK], F32, name=name, tag="%s%d" % (name, b))
+            nc.scalar.mul(out=held[:], in_=turned[:], mul=factor)
+            state[i][(name, b)] = held
 
-        def turn_dh(i, b, where_to=None, width=BANK):
-            st = state[i]
-            kind, number = ("x", b) if where_to is None else where_to
-            dh = bank(kind, number)
-            for k in range(width // P):
-                nc.tensor.transpose(
-                    dh[:, k * P : (k + 1) * P], st[("dh_t", b)][:, k * P : (k + 1) * P], identity[:]
-                )
-            st[("dh", b)] = dh[:, :width]
+        def turn_gt(i, b, kind, k):
+            turn(i, "gt_t", b, state[i][("gt", b)], kind, k, -1.0)
 
-        def times_t(i, b=None):
+        def turn_hn(i, b, kind, k):
+            turn(i, "hn_t", b, state[i]["h_n"], kind, k, 1.0)
+
+        def turn_back(i, name, b, source, kind, k):
+            held = bank(kind, k)
+            for k in range(BANK // P):
+                nc.tensor.transpose(
+                    held[:, k * P : (k + 1) * P], state[i][(source, b)][:, k * P : (k + 1) * P], identity[:]
+                )
+            state[i][(name, b)] = held
+
+        def turn_dh(i, b):
+            turn_back(i, "dh", b, "dh_t", "x", b)
+
+        def times_t(i, b):
             st = state[i]
-            st[("gt", None)] = st["t"]
+            st[("gt", b)] = st["t"]
             nc.vector.tensor_tensor(out=flat(st["t"], b), in0=flat(st["g"], b), in1=flat(st["t"], b), op=ALU.mult)
 
-        def mask(i, b, width=BANK):
+        def mask(i, b):
             st = state[i]
-            dh_t = work_pool.tile([P, BANK], F32, name="dh_t", tag="dh_t%d" % (b % 2))
+            dh_t = work_pool.tile([P, BANK], F32, name="dh_t", tag="dh_t%d" % b)
             nc.vector.scalar_tensor_tensor(
-                out=dh_t[:, :width], in0=st[("tot_t", b)][:, :width], scalar=0.0, in1=st[("gt_t", b)][:, :width],
+                out=dh_t[:], in0=st[("tot_t", b)][:], scalar=0.0, in1=st[("gt_t", b)][:],
                 op0=ALU.is_gt, op1=ALU.mult,
             )
             st[("dh_t", b)] = dh_t
@@ -247,10 +246,10 @@ def tile_graphconvolution_pb_v_kernel(
                         out=flat(st[("a", d)], b), in0=flat(st[("z", d)], b), in1=diffs[b][:], op=ALU.mult,
                     )
 
-        def make_u(i, d, b, dh=None):
+        def make_u(i, d, b):
             st = state[i]
             nc.vector.scalar_tensor_tensor(
-                out=flat(st[("z", d)], b), in0=flat(st[("z", d)], b), scalar=1.0, in1=st[("dh", b)] if dh is None else dh,
+                out=flat(st[("z", d)], b), in0=flat(st[("z", d)], b), scalar=1.0, in1=st[("dh", b)][:],
                 op0=ALU.subtract, op1=ALU.mult,
             )
 
@@ -261,10 +260,10 @@ def tile_graphconvolution_pb_v_kernel(
                 op0=ALU.subtract, op1=ALU.mult,
             )
 
-        def make_e(i, d):
+        def make_e(i, d, b):
             st = state[i]
             nc.vector.scalar_tensor_tensor(
-                out=flat(st[("r", d)]), in0=flat(st[("r", d)]), scalar=0.25, in1=flat(st["h_n"]),
+                out=flat(st[("r", d)], b), in0=flat(st[("r", d)], b), scalar=0.25, in1=st[("hn_back", b)][:],
                 op0=ALU.subtract, op1=ALU.mult,
             )
 
@@ -274,15 +273,21 @@ def tile_graphconvolution_pb_v_kernel(
                 state[i][key] = grouped_pool.tile([P, COLS, PACK], BF16, name="grouped", tag="grouped", align_bytes=64)
             return state[i][key]
 
-        def product_grouped(i, name, in0, in1, d, width=COLS, b=None):
+        def product_grouped(engine, i, name, in0, in1, d, cols=slice(0, COLS), b=None):
             st = state[i]
             made = new_grouped(i, name, d)
-            nc.vector.tensor_tensor(
-                out=made[:, :width, tokens(b)].rearrange("p (c i) j -> p c j i", i=RUN),
-                in0=st[(in0, d)][:, tokens(b), :width].rearrange("p j (c i) -> p c j i", i=RUN),
-                in1=st[(in1, d)][:, tokens(b), :width].rearrange("p j (c i) -> p c j i", i=RUN),
+            engine.tensor_tensor(
+                out=made[:, cols, tokens(b)].rearrange("p (c i) j -> p c j i", i=RUN),
+                in0=st[(in0, d)][:, tokens(b), cols].rearrange("p j (c i) -> p c j i", i=RUN),
+                in1=st[(in1, d)][:, tokens(b), cols].rearrange("p j (c i) -> p c j i", i=RUN),
                 op=ALU.mult,
             )
+
+        def dz(engine, i, d, b=None):
+            product_grouped(engine, i, "z", "z", "a", d, b=b)
+
+        def dr(engine, i, d, cols=slice(0, COLS)):
+            product_grouped(engine, i, "r", "r", "a", d, cols)
 
         def quantise(grouped, x4_dtype, codes, scales):
             nc.vector.quantize_mx(
@@ -325,21 +330,6 @@ def tile_graphconvolution_pb_v_kernel(
             for half in range(HALVES) if b is None else (b,):
                 st[("gt", half)] = held
 
-        def side_product(i, in0, in1, d, width, held=None):
-            st = state[i]
-            if held is None:
-                part = part_pool.tile([P, PACK, SIDE_Z], F32, name="part", tag="part")
-                part = part[:, :, :width]
-            else:
-                part = held[:, :, :width]
-            nc.gpsimd.tensor_tensor(
-                out=part, in0=st[(in0, d)][:, :, COLS - width :], in1=st[(in1, d)][:, :, COLS - width :], op=ALU.mult,
-            )
-            return part
-
-        def side_regroup(i, name, d, part, width):
-            regroup(new_grouped(i, name, d)[:, COLS - width :, :], part, 1.0)
-
         def open_acc(gate, kind, first):
             for m in range(M_TILES):
                 acc[(gate, m)] = bank(kind, first + m)
@@ -364,7 +354,7 @@ def tile_graphconvolution_pb_v_kernel(
             cb, nb = chunks[i]
             for m in range(M_TILES):
                 if spare:
-                    result = part_pool.tile([M_TILE, FEAT], F32, name="part", tag="part")
+                    result = result_pool.tile([M_TILE, FEAT], F32, name="last_result", tag="last_result", bufs=2)
                 else:
                     result = result_pool.tile([M_TILE, FEAT], F32, name="result", tag="result")
                 if shared_out and m == 0:
@@ -374,8 +364,9 @@ def tile_graphconvolution_pb_v_kernel(
                 first = gate * FEAT + cb * COLS + m * M_TILE
                 nc.sync.dma_start(out=out[first : first + M_TILE, :], in_=result[:])
 
-        pieces = [slice(0, 1), slice(1, 2), slice(2, 4)]
-        for b in pieces:
+        main = slice(0, COLS - SIDE)
+        side = slice(COLS - SIDE, COLS)
+        for b in range(HALVES):
             load_h(0, b)
             for d in range(DIRS):
                 load_gate(0, "c", C, d, b)
@@ -383,257 +374,242 @@ def tile_graphconvolution_pb_v_kernel(
             for d in range(DIRS):
                 load_gate(0, "z", Z, d, b)
         load_h(1)
+        load_cz(1, 0)
         load_gt(1)
-        for d in range(DIRS):
-            load_cz(1, d)
-        load_gate(0, "r", R, 0)
         load_hn(0)
-        load_gate(0, "r", R, 1)
-        load_gate(0, "r", R, 2)
+        for d in (2, 0, 1):
+            load_gate(0, "r", R, d)
+        load_cz(1, 1)
+        load_cz(1, 2)
+        load_hn(1)
         load_h(2)
+        load_h(3)
+        load_gt(2)
+        for d in (2, 0, 1):
+            load_gate(1, "r", R, d)
 
-        tot_banks = [("m", 0), ("m", 1), ("x", 1)]
-        gt_banks = [("a", 0), ("a", 1), ("m", 2)]
         st0 = state[0]
 
-        def first_c(p):
-            b = pieces[p]
-            tot = bank(tot_banks[p][0], tot_banks[p][1])
-            st0[("tot_t", p)] = tot
-            for d in range(DIRS):
-                add_transposed(tot, b, st0[("c", d)], d == 0, False)
-
-        def first_difference(p, d):
+        def first_difference(b, d):
             new_a(0, d)
             nc.vector.tensor_tensor(
-                out=flat(st0[("a", d)], pieces[p]), in0=flat(st0["h"], pieces[p]), in1=flat(st0[("c", d)], pieces[p]),
-                op=ALU.subtract,
+                out=flat(st0[("a", d)], b), in0=flat(st0["h"], b), in1=flat(st0[("c", d)], b), op=ALU.subtract,
             )
 
-        def first_a(p, d):
-            b = pieces[p]
+        def first_a(b, d, diff=None):
             nc.vector.tensor_tensor(
                 out=flat(st0[("a", d)], b), in0=flat(st0[("z", d)], b),
-                in1=flat(st0[("a", d)], b), op=ALU.mult,
+                in1=flat(st0[("a", d)], b) if diff is None else diff[:], op=ALU.mult,
             )
-            add_transposed(st0[("tot_t", p)], b, st0[("a", d)], False, d == DIRS - 1)
+            add_a(0, d, (b,))
 
-        def first_u(p):
-            for d in range(DIRS):
-                make_u(0, d, pieces[p], st0[("dh", p)])
+        def turn_first_h():
+            turned = bank("m", 1, BF16, 2 * BANK)
+            for k, (j, fb) in enumerate(blocks(1)):
+                nc.tensor.transpose(
+                    turned[:, k * P : (k + 1) * P], st0["h"][:, j, fb * P : (fb + 1) * P], identity_bf[:]
+                )
+            h_t = work_pool.tile([P, BANK // P, P], F32, name="h_t", tag="h_t", bufs=2)
+            nc.scalar.copy(out=h_t[:].rearrange("p k q -> p (k q)"), in_=turned[:, :BANK])
+            st0["h_t"] = h_t
 
-        def first_mask(p):
-            width = (pieces[p].stop - pieces[p].start) * COLS
-            mask(0, p, width)
-            turn_dh(0, p, tot_banks[p], width)
+        def pe_difference(d):
+            kind, number = (("a", 0), ("a", 1), ("m", 0))[d]
+            diff = bank(kind, number)
+            nc.tensor.matmul(
+                out=diff[:], lhsT=minus_identity[:], rhs=flat(st0[("c", d)], 1), start=True, stop=False,
+            )
+            for k in range(BANK // P):
+                nc.tensor.matmul(
+                    out=diff[:, k * P : (k + 1) * P], lhsT=st0["h_t"][:, k, :], rhs=identity[:], is_transpose=True,
+                    start=False, stop=(k == BANK // P - 1),
+                )
+            return diff
 
-        def first_dz(p):
-            for d in range(DIRS):
-                product_grouped(0, "z", "z", "a", d, COLS, pieces[p])
-
-        first_c(0)
         for d in range(DIRS):
+            add_c(0, d, (0,))
             first_difference(0, d)
-        times_t(0, pieces[0])
-        turn_gt(0, 0, "a", 0, pieces[0])
+        times_t(0, 0)
+        turn_gt(0, 0, "a", 0)
         for d in range(DIRS):
-            square(0, "c", d, 0.0, pieces[0])
+            square(0, "c", d, 0.0, 0)
         for d in range(DIRS):
             first_a(0, d)
-        first_c(1)
+        mask(0, 0)
+        turn_dh(0, 0)
+        turn_first_h()
         for d in range(DIRS):
-            first_difference(1, d)
-        first_mask(0)
-        times_t(0, pieces[1])
-        turn_gt(0, 1, "a", 1, pieces[1])
+            add_c(0, d, (1,))
+        first_diffs = [pe_difference(d) for d in range(DIRS)]
         for d in range(DIRS):
-            square(0, "c", d, 0.0, pieces[1])
-        first_u(0)
+            make_u(0, d, 0)
+        times_t(0, 1)
+        turn_gt(0, 1, "m", 2)
+        transpose_h(1, 1)
         for d in range(DIRS):
-            first_a(1, d)
-        first_dz(0)
-        first_mask(1)
+            dz(nc.vector, 0, d, 0)
         for d in range(DIRS):
-            make_dc(0, d, pieces[0])
-        first_u(1)
-        first_c(2)
+            square(0, "c", d, 0.0, 1)
         for d in range(DIRS):
-            first_difference(2, d)
-        times_t(0, pieces[2])
-        turn_gt(0, 2, "m", 2, pieces[2])
-        for d in range(DIRS):
-            square(0, "c", d, 0.0, pieces[2])
-        product_grouped(0, "z", "z", "a", 0, COLS, pieces[1])
-        transpose_h(1, 3)
-        for d in range(DIRS):
-            first_a(2, d)
-        for d in range(DIRS - 1):
-            product_grouped(0, "z", "z", "a", d + 1, COLS, pieces[1])
-        make_dc(0, 0, pieces[1])
-        first_mask(2)
-        add_c(1, 0, (0,))
+            first_a(1, d, first_diffs[d])
+            if d > 0:
+                make_dc(0, d - 1, 0)
+        for b in range(HALVES):
+            turn_hn(0, b, "m", 2 + b)
+        for d in (2, 0, 1):
+            square(0, "r", d, -0.5)
+        mask(0, 1)
+        turn_dh(0, 1)
+        make_dc(0, 2, 0)
         differences(1, 0)
-        make_dc(0, 1, pieces[1])
-        make_dc(0, 2, pieces[1])
         side_gt(1, st0[("c", 2)], 0)
-        turn_gt(1, 0, "m", 0)
-        first_u(2)
+        side_gt(1, state[1]["t"], 1)
+        for b in range(HALVES):
+            turn_back(0, "hn_back", b, "hn_t", "m", 2 + b)
         for d in range(DIRS):
-            product_grouped(0, "z", "z", "a", d, COLS, pieces[2])
-            if d == 1:
-                gated_difference(1, 0)
-                differences(1, 1)
+            make_u(0, d, 1)
+        gated_difference(1, 0)
+        differences(1, 1)
+        for b in range(HALVES):
+            turn_gt(1, b, "m", b)
         for d in range(DIRS):
-            make_dc(0, d, pieces[2])
+            dz(nc.vector, 0, d, 1)
+        for d in range(DIRS):
+            make_dc(0, d, 1)
             regroup_dc(0, d)
-            if d == 1:
-                side_gt(1, st0[("c", 1)], 1)
-                gated_difference(1, 1)
-                turn_gt(1, 1, "m", 1)
-                differences(1, 2)
-                square(0, "r", 0, -0.5)
-        add_c(1, 0, (1,))
-        add_a(1, 0)
-        add_c(1, 1)
         load_cz(2, 0)
-        load_gt(2)
-        for d in range(DIRS):
-            load_gate(1, "r", R, d)
-        load_hn(1)
         load_cz(2, 1)
-        load_cz(2, 2)
-        load_h(3)
+        load_hn(2)
         for d in range(DIRS):
             load_agg(0, d)
-        add_a(1, 1)
-        add_c(1, 2)
-        for d in range(1, DIRS):
-            square(0, "r", d, -0.5)
+        load_cz(2, 2)
+        add_c(1, 0)
+        add_a(1, 0)
+        add_c(1, 1)
+        gated_difference(1, 1)
+        differences(1, 2)
         for d in range(DIRS):
             quantise_gate(0, Z, "z", d)
-        make_e(0, 0)
+        for b in range(HALVES):
+            for d in (2, 0, 1):
+                make_e(0, d, b)
         gated_difference(1, 2)
+        add_a(1, 1)
+        add_c(1, 2)
         add_a(1, 2)
+        for b in range(HALVES):
+            turn_hn(1, b, "m", 2 + b)
+        dr(nc.vector, 0, 0)
+        dr(nc.vector, 0, 2)
         for d in range(DIRS):
             quantise_gate(0, C, "c", d)
-        square(1, "c", 0, 0.0)
-        square(1, "c", 1, 0.0)
+        quantise_gate(0, R, "r", 0)
+        dr(nc.vector, 0, 1)
+        transpose_h(2, 0)
+        differences(2, 0)
+        for d in (2, 0, 1):
+            square(1, "r", d, -0.5)
 
         for i in range(1, n_chunks):
             nxt = i + 1
             has_next = nxt < n_chunks
             if has_next:
-                load_gate(nxt, "r", R, 0)
-                load_gate(nxt, "r", R, 2)
-            if has_next and i > 1:
                 side_gt(nxt, state[i - 1][("r", 1)])
             for b in range(HALVES):
                 mask(i, b)
             for b in range(HALVES):
                 turn_dh(i, b)
-            square(i, "c", 2, 0.0)
-            if i == 1:
-                for d in range(1, DIRS):
-                    make_e(0, d)
-                transpose_h(2, 2)
-                differences(2, 0)
-                for d in (0, 2, 1):
-                    product_grouped(0, "r", "r", "a", d)
-                side_gt(nxt, state[0][("r", 1)])
-            elif has_next:
+            for d in range(DIRS):
+                square(i, "c", d, 0.0)
+            if has_next:
                 gated_difference(nxt, 0)
-                differences(nxt, 1)
-            if not has_next:
+                diffs[0] = difference(nxt, 1, 0)
+            else:
                 quantise_gate(i - 1, R, "r", 2)
                 quantise_gate(i - 1, R, "r", 1)
-            for d in range(DIRS):
-                square(i, "r", d, -0.5)
-            for d, b in ((2, 0), (0, 0), (2, 1), (0, 1), (1, 0), (1, 1)):
-                make_u(i, d, b)
-            part_z = side_product(i, "z", "a", 2, SIDE_Z)
-            if i == 1:
-                gated_difference(nxt, 0)
-                differences(nxt, 1)
-                quantise_gate(0, R, "r", 0)
-            if has_next:
-                for b in range(HALVES):
-                    turn_gt(nxt, b, "x", b)
-                load_gate(nxt, "r", R, 1)
-                quantise_gate(i - 1, R, "r", 2)
-                quantise_gate(i - 1, R, "r", 1)
-            if i > 1:
-                quantise_agg(i - 2)
-            if i == 2:
-                open_acc(Z, "m", 0)
-                open_acc(C, "m", 2)
-                passes(0, Z)
-                passes(0, C)
-            if i == 1:
-                transpose_h(3, 3)
-            product_grouped(i, "z", "z", "a", 0)
-            product_grouped(i, "z", "z", "a", 1, COLS - SIDE_N if has_next else COLS)
-            product_grouped(i, "z", "z", "a", 2, COLS - SIDE_Z)
-            side_regroup(i, "z", 2, part_z, SIDE_Z)
-            add_c(nxt, 0)
-            add_a(nxt, 0)
-            add_c(nxt, 1)
-            for d in range(DIRS):
-                make_e(i, d)
-            if has_next:
-                part_z1 = side_product(i, "z", "a", 1, SIDE_N, state[i]["h_n"])
-                side_regroup(i, "z", 1, part_z1, SIDE_N)
-                gated_difference(nxt, 1)
-                differences(nxt, 2)
-                add_a(nxt, 1)
-                add_c(nxt, 2)
-            if i > 1 and has_next:
-                load_hn(nxt)
-            if i == 1:
-                load_hn(2)
-            if i == last:
-                passes(1, Z)
-                store(1, Z)
-                passes(1, C)
-                store(1, C)
                 open_acc(R, "a", 0)
                 passes(0, R)
+            for b in range(HALVES):
+                for d in (2, 0, 1):
+                    make_u(i, d, b)
+                for d in (2, 0):
+                    dz(nc.gpsimd, i, d, b)
+                turn_back(i, "hn_back", b, "hn_t", "x", b)
+                if has_next and b == 0:
+                    regroup_agg(i - 1, 0)
+                if i == last and b == 0:
+                    passes(1, Z)
+                    store(1, Z)
+                if has_next and b == 0:
+                    diffs[1] = difference(nxt, 1, 1)
+            if i == last:
+                passes(1, C)
+                store(1, C)
                 passes(1, R)
+            for b in range(HALVES):
+                for d in (2, 0, 1):
+                    make_e(i, d, b)
+            if has_next:
+                for b in range(HALVES):
+                    turn_hn(nxt, b, "x", b)
+                for b in range(HALVES):
+                    turn_gt(nxt, b, "x", b)
+                regroup_agg(i - 1, 1)
+                regroup_agg(i - 1, 2)
+                gated_difference(nxt, 1)
+                differences(nxt, 2)
+                add_c(nxt, 0)
+                add_a(nxt, 0)
+                add_c(nxt, 1)
+                if i == 1:
+                    transpose_h(3, 1)
+                else:
+                    open_acc(Z, "m", 0)
+                    open_acc(C, "m", 2)
+                    passes(0, Z)
+                    passes(0, C)
+                add_a(nxt, 1)
+                add_c(nxt, 2)
+                quantise_gate(i - 1, R, "r", 2)
+                quantise_gate(i - 1, R, "r", 1)
+                for d in (2, 0, 1):
+                    load_gate(nxt, "r", R, d)
+            dz(nc.vector, i, 1)
             for d in range(DIRS):
                 make_dc(i, d)
                 regroup_dc(i, d)
             if not has_next:
                 store(1, R)
-                open_acc(R, "x", 0)
-                passes(2, R)
                 open_acc(Z, "m", 0)
                 open_acc(C, "m", 2)
+                open_acc(R, "x", 0)
                 passes(2, Z)
                 passes(2, C)
+                passes(2, R)
                 break
             if i == 1:
                 load_cz(3, 0)
                 load_gt(3)
                 load_cz(3, 1)
                 load_cz(3, 2)
+                load_hn(3)
                 for d in range(DIRS):
                     load_agg(1, d)
-            part_r = side_product(i, "r", "a", 2, SIDE_N)
+            dr(nc.gpsimd, i, 2, side)
             gated_difference(nxt, 2)
             add_a(nxt, 2)
             differences(nxt + 1, 0)
+            quantise_agg(i - 1)
             for d in range(DIRS):
                 quantise_gate(i, Z, "z", d)
-            product_grouped(i, "r", "r", "a", 0)
-            product_grouped(i, "r", "r", "a", 2, COLS - SIDE_N)
-            side_regroup(i, "r", 2, part_r, SIDE_N)
-            for d in range(DIRS):
-                regroup_agg(i - 1, d)
+            dr(nc.vector, i, 0)
+            dr(nc.vector, i, 2, main)
+            for d in (2, 0, 1):
+                square(nxt, "r", d, -0.5)
             for d in range(DIRS):
                 quantise_gate(i, C, "c", d)
             quantise_gate(i, R, "r", 0)
-            product_grouped(i, "r", "r", "a", 1)
-            square(nxt, "c", 0, 0.0)
-            square(nxt, "c", 1, 0.0)
+            dr(nc.vector, i, 1)
 
         for d in range(DIRS):
             quantise_gate(last, Z, "z", d)
@@ -642,7 +618,7 @@ def tile_graphconvolution_pb_v_kernel(
         for d in range(DIRS):
             quantise_gate(last, C, "c", d)
             multiply(last, C, d)
-            product_grouped(last, "r", "r", "a", d)
+            dr(nc.vector, last, d)
             if d > 0:
                 quantise_gate(last, R, "r", d - 1)
                 multiply(last, R, d - 1)

@@ -31,6 +31,7 @@ BANK = 512
 HALVES = PACK * COLS // BANK
 RUN = 4
 SIDE = 64
+HN_BY_MATMUL = (1, 2)
 
 FLOPS = 2 * DIRS * NODES * GATES * FEAT * FEAT
 BYTES = (
@@ -100,7 +101,7 @@ def tile_graphconvolution_pb_v_kernel(
 
         def load_h(i, b=None):
             rows, cols = where(i)
-            load_node(i, "h", BF16, x[rows, 0, cols], 2, b)
+            load_node(i, "h", BF16, x[rows, 0, cols], n_chunks, b)
 
         def load_gt(i, b=None):
             rows, cols = where(i)
@@ -133,35 +134,19 @@ def tile_graphconvolution_pb_v_kernel(
             nc.sync.dma_start(out=agg_rows[:], in_=rows_view(agg[d, 0, rows, :]))
             state[i].setdefault("agg_rows", []).append(agg_rows)
 
-        def transpose_h(i, spare):
-            h = state[i]["h"]
-            turned = bank("m", spare, BF16, 2 * BANK)
-            for fb in range(M_TILES):
-                for j in range(PACK):
-                    k = fb * PACK + j
-                    nc.tensor.transpose(
-                        turned[:, k * P : (k + 1) * P], h[:, j, fb * P : (fb + 1) * P], identity_bf[:]
-                    )
-            h_t = work_pool.tile([P, M_TILES, PACK, P], F32, name="h_t", tag="h_t", bufs=2)
-            nc.scalar.copy(out=h_t[:].rearrange("p f j q -> p (f j q)"), in_=turned[:])
-            state[i]["h_t"] = h_t
-
         def difference(i, d, b):
             st = state[i]
             diff = bank("a", b)
-            nc.tensor.matmul(
-                out=diff[:], lhsT=minus_identity[:], rhs=flat(st[("c", d)], b), start=True, stop=False,
-            )
-            per_bank = PACK // HALVES
-            for jj in range(per_bank):
-                for fb in range(M_TILES):
-                    first = jj * COLS + fb * P
-                    nc.tensor.matmul(
-                        out=diff[:, first : first + P], lhsT=st["h_t"][:, fb, b * per_bank + jj, :],
-                        rhs=identity[:], is_transpose=True,
-                        start=False, stop=(jj == per_bank - 1 and fb == M_TILES - 1),
-                    )
+            nc.tensor.matmul(out=diff[:], lhsT=identity_bf[:], rhs=flat(st["h"], b), start=True, stop=False)
+            nc.tensor.matmul(out=diff[:], lhsT=minus_identity[:], rhs=flat(st[("c", d)], b), start=False, stop=True)
             return diff
+
+        def some_passes(i, k):
+            if i == 2:
+                if k == 0:
+                    open_acc(Z, "m", 0)
+                    open_acc(C, "m", 2)
+                multiply(0, (Z, C)[k // DIRS], k % DIRS)
 
         diffs = {}
 
@@ -216,6 +201,14 @@ def tile_graphconvolution_pb_v_kernel(
                 )
             state[i][(name, b)] = held
 
+        def hn_to_psum(i, b, kind, k):
+            if i in HN_BY_MATMUL:
+                held = bank(kind, k)
+                nc.tensor.matmul(out=held[:], lhsT=identity[:], rhs=flat(state[i]["h_n"], b), start=True, stop=True)
+                state[i][("hn_back", b)] = held
+            else:
+                turn_back(i, "hn_back", b, "hn_t", kind, k)
+
         def turn_dh(i, b):
             turn_back(i, "dh", b, "dh_t", "x", b)
 
@@ -241,10 +234,15 @@ def tile_graphconvolution_pb_v_kernel(
             if i < n_chunks:
                 st = state[i]
                 new_a(i, d)
-                for b in range(HALVES):
+                if ("side", d) in st:
                     nc.vector.tensor_tensor(
-                        out=flat(st[("a", d)], b), in0=flat(st[("z", d)], b), in1=diffs[b][:], op=ALU.mult,
+                        out=flat(st[("a", d)]), in0=flat(st[("z", d)]), in1=flat(st[("a", d)]), op=ALU.mult,
                     )
+                else:
+                    for b in range(HALVES):
+                        nc.vector.tensor_tensor(
+                            out=flat(st[("a", d)], b), in0=flat(st[("z", d)], b), in1=diffs[b][:], op=ALU.mult,
+                        )
 
         def make_u(i, d, b):
             st = state[i]
@@ -283,8 +281,8 @@ def tile_graphconvolution_pb_v_kernel(
                 op=ALU.mult,
             )
 
-        def dz(engine, i, d, b=None):
-            product_grouped(engine, i, "z", "z", "a", d, b=b)
+        def dz(engine, i, d, b=None, cols=slice(0, COLS)):
+            product_grouped(engine, i, "z", "z", "a", d, cols, b)
 
         def dr(engine, i, d, cols=slice(0, COLS)):
             product_grouped(engine, i, "r", "r", "a", d, cols)
@@ -330,6 +328,14 @@ def tile_graphconvolution_pb_v_kernel(
             for half in range(HALVES) if b is None else (b,):
                 st[("gt", half)] = held
 
+        def side_difference(i, d):
+            new_a(i, d)
+            st = state[i]
+            st[("side", d)] = True
+            nc.gpsimd.tensor_tensor(
+                out=flat(st[("a", d)]), in0=flat(st["h"]), in1=flat(st[("c", d)]), op=ALU.subtract
+            )
+
         def open_acc(gate, kind, first):
             for m in range(M_TILES):
                 acc[(gate, m)] = bank(kind, first + m)
@@ -374,16 +380,16 @@ def tile_graphconvolution_pb_v_kernel(
             for d in range(DIRS):
                 load_gate(0, "z", Z, d, b)
         load_h(1)
-        load_cz(1, 0)
         load_gt(1)
         load_hn(0)
-        for d in (2, 0, 1):
-            load_gate(0, "r", R, d)
+        load_gate(0, "r", R, 2)
+        load_cz(1, 0)
+        load_gate(0, "r", R, 0)
+        load_gate(0, "r", R, 1)
         load_cz(1, 1)
         load_cz(1, 2)
         load_hn(1)
         load_h(2)
-        load_h(3)
         load_gt(2)
         for d in (2, 0, 1):
             load_gate(1, "r", R, d)
@@ -396,35 +402,11 @@ def tile_graphconvolution_pb_v_kernel(
                 out=flat(st0[("a", d)], b), in0=flat(st0["h"], b), in1=flat(st0[("c", d)], b), op=ALU.subtract,
             )
 
-        def first_a(b, d, diff=None):
+        def first_a(b, d):
             nc.vector.tensor_tensor(
-                out=flat(st0[("a", d)], b), in0=flat(st0[("z", d)], b),
-                in1=flat(st0[("a", d)], b) if diff is None else diff[:], op=ALU.mult,
+                out=flat(st0[("a", d)], b), in0=flat(st0[("z", d)], b), in1=flat(st0[("a", d)], b), op=ALU.mult,
             )
             add_a(0, d, (b,))
-
-        def turn_first_h():
-            turned = bank("m", 1, BF16, 2 * BANK)
-            for k, (j, fb) in enumerate(blocks(1)):
-                nc.tensor.transpose(
-                    turned[:, k * P : (k + 1) * P], st0["h"][:, j, fb * P : (fb + 1) * P], identity_bf[:]
-                )
-            h_t = work_pool.tile([P, BANK // P, P], F32, name="h_t", tag="h_t", bufs=2)
-            nc.scalar.copy(out=h_t[:].rearrange("p k q -> p (k q)"), in_=turned[:, :BANK])
-            st0["h_t"] = h_t
-
-        def pe_difference(d):
-            kind, number = (("a", 0), ("a", 1), ("m", 0))[d]
-            diff = bank(kind, number)
-            nc.tensor.matmul(
-                out=diff[:], lhsT=minus_identity[:], rhs=flat(st0[("c", d)], 1), start=True, stop=False,
-            )
-            for k in range(BANK // P):
-                nc.tensor.matmul(
-                    out=diff[:, k * P : (k + 1) * P], lhsT=st0["h_t"][:, k, :], rhs=identity[:], is_transpose=True,
-                    start=False, stop=(k == BANK // P - 1),
-                )
-            return diff
 
         for d in range(DIRS):
             add_c(0, d, (0,))
@@ -437,76 +419,76 @@ def tile_graphconvolution_pb_v_kernel(
             first_a(0, d)
         mask(0, 0)
         turn_dh(0, 0)
-        turn_first_h()
         for d in range(DIRS):
             add_c(0, d, (1,))
-        first_diffs = [pe_difference(d) for d in range(DIRS)]
+            first_difference(1, d)
         for d in range(DIRS):
             make_u(0, d, 0)
         times_t(0, 1)
-        turn_gt(0, 1, "m", 2)
-        transpose_h(1, 1)
-        for d in range(DIRS):
+        turn_gt(0, 1, "a", 1)
+        for d in range(DIRS - 1):
             dz(nc.vector, 0, d, 0)
         for d in range(DIRS):
             square(0, "c", d, 0.0, 1)
         for d in range(DIRS):
-            first_a(1, d, first_diffs[d])
-            if d > 0:
-                make_dc(0, d - 1, 0)
-        for b in range(HALVES):
-            turn_hn(0, b, "m", 2 + b)
-        for d in (2, 0, 1):
-            square(0, "r", d, -0.5)
+            first_a(1, d)
+        for d in range(DIRS - 1):
+            make_dc(0, d, 0)
         mask(0, 1)
         turn_dh(0, 1)
-        make_dc(0, 2, 0)
-        differences(1, 0)
-        side_gt(1, st0[("c", 2)], 0)
+        square(0, "r", 2, -0.5)
+        for b in range(HALVES):
+            turn_hn(0, b, "m", 2 + b)
+        for d in (0, 1):
+            square(0, "r", d, -0.5)
+        for b in range(HALVES):
+            hn_to_psum(0, b, "m", 2 + b)
+        side_gt(1, st0[("c", 1)], 0)
+        side_difference(1, 0)
         side_gt(1, state[1]["t"], 1)
-        for b in range(HALVES):
-            turn_back(0, "hn_back", b, "hn_t", "m", 2 + b)
-        for d in range(DIRS):
+        turn_gt(1, 0, "m", 0)
+        for d in (2, 0, 1):
             make_u(0, d, 1)
+        dz(nc.gpsimd, 0, 2)
+        side_difference(1, 2)
+        diffs[0] = difference(1, 1, 0)
+        turn_gt(1, 1, "m", 1)
+        diffs[1] = difference(1, 1, 1)
+        for d in (2, 0, 1):
+            for b in range(HALVES):
+                make_e(0, d, b)
         gated_difference(1, 0)
-        differences(1, 1)
-        for b in range(HALVES):
-            turn_gt(1, b, "m", b)
-        for d in range(DIRS):
-            dz(nc.vector, 0, d, 1)
-        for d in range(DIRS):
-            make_dc(0, d, 1)
-            regroup_dc(0, d)
-        load_cz(2, 0)
-        load_cz(2, 1)
-        load_hn(2)
-        for d in range(DIRS):
-            load_agg(0, d)
-        load_cz(2, 2)
+        gated_difference(1, 1)
         add_c(1, 0)
         add_a(1, 0)
         add_c(1, 1)
-        gated_difference(1, 1)
-        differences(1, 2)
-        for d in range(DIRS):
-            quantise_gate(0, Z, "z", d)
-        for b in range(HALVES):
-            for d in (2, 0, 1):
-                make_e(0, d, b)
-        gated_difference(1, 2)
         add_a(1, 1)
+        for d in range(DIRS - 1):
+            dz(nc.vector, 0, d, 1)
+        for d in range(DIRS - 1):
+            make_dc(0, d, 1)
+            regroup_dc(0, d)
+        make_dc(0, 2)
+        regroup_dc(0, 2)
+        load_cz(2, 0)
+        load_cz(2, 1)
+        load_hn(2)
+        load_cz(2, 2)
+        for d in range(DIRS):
+            load_agg(0, d)
+        load_h(3)
+        gated_difference(1, 2)
         add_c(1, 2)
         add_a(1, 2)
-        for b in range(HALVES):
-            turn_hn(1, b, "m", 2 + b)
+        differences(2, 0)
+        for d in range(DIRS):
+            quantise_gate(0, Z, "z", d)
         dr(nc.vector, 0, 0)
         dr(nc.vector, 0, 2)
         for d in range(DIRS):
             quantise_gate(0, C, "c", d)
         quantise_gate(0, R, "r", 0)
         dr(nc.vector, 0, 1)
-        transpose_h(2, 0)
-        differences(2, 0)
         for d in (2, 0, 1):
             square(1, "r", d, -0.5)
 
@@ -515,6 +497,7 @@ def tile_graphconvolution_pb_v_kernel(
             has_next = nxt < n_chunks
             if has_next:
                 side_gt(nxt, state[i - 1][("r", 1)])
+                side_difference(nxt, 2)
             for b in range(HALVES):
                 mask(i, b)
             for b in range(HALVES):
@@ -524,58 +507,53 @@ def tile_graphconvolution_pb_v_kernel(
             if has_next:
                 gated_difference(nxt, 0)
                 diffs[0] = difference(nxt, 1, 0)
+                regroup_agg(i - 1, 0)
             else:
                 quantise_gate(i - 1, R, "r", 2)
                 quantise_gate(i - 1, R, "r", 1)
+                passes(1, C)
+            for d, b in ((2, 0), (2, 1), (0, 0), (1, 0), (0, 1), (1, 1)):
+                make_u(i, d, b)
+            dz(nc.gpsimd, i, 2)
+            dz(nc.gpsimd, i, 0)
+            for b in range(HALVES):
+                hn_to_psum(i, b, "x", b)
+            if has_next:
+                diffs[1] = difference(nxt, 1, 1)
+            else:
+                store(1, Z)
+                store(1, C)
                 open_acc(R, "a", 0)
                 passes(0, R)
-            for b in range(HALVES):
-                for d in (2, 0, 1):
-                    make_u(i, d, b)
-                for d in (2, 0):
-                    dz(nc.gpsimd, i, d, b)
-                turn_back(i, "hn_back", b, "hn_t", "x", b)
-                if has_next and b == 0:
-                    regroup_agg(i - 1, 0)
-                if i == last and b == 0:
-                    passes(1, Z)
-                    store(1, Z)
-                if has_next and b == 0:
-                    diffs[1] = difference(nxt, 1, 1)
-            if i == last:
-                passes(1, C)
-                store(1, C)
                 passes(1, R)
             for b in range(HALVES):
                 for d in (2, 0, 1):
                     make_e(i, d, b)
             if has_next:
-                for b in range(HALVES):
-                    turn_hn(nxt, b, "x", b)
+                some_passes(i, 0)
+                if nxt not in HN_BY_MATMUL:
+                    for b in range(HALVES):
+                        turn_hn(nxt, b, "x", b)
                 for b in range(HALVES):
                     turn_gt(nxt, b, "x", b)
                 regroup_agg(i - 1, 1)
                 regroup_agg(i - 1, 2)
                 gated_difference(nxt, 1)
-                differences(nxt, 2)
+                some_passes(i, 1)
                 add_c(nxt, 0)
                 add_a(nxt, 0)
+                some_passes(i, 2)
                 add_c(nxt, 1)
-                if i == 1:
-                    transpose_h(3, 1)
-                else:
-                    open_acc(Z, "m", 0)
-                    open_acc(C, "m", 2)
-                    passes(0, Z)
-                    passes(0, C)
                 add_a(nxt, 1)
+                some_passes(i, 3)
                 add_c(nxt, 2)
+                some_passes(i, 4)
                 quantise_gate(i - 1, R, "r", 2)
                 quantise_gate(i - 1, R, "r", 1)
                 for d in (2, 0, 1):
                     load_gate(nxt, "r", R, d)
             dz(nc.vector, i, 1)
-            for d in range(DIRS):
+            for d in (1, 0, 2):
                 make_dc(i, d)
                 regroup_dc(i, d)
             if not has_next:
@@ -595,15 +573,17 @@ def tile_graphconvolution_pb_v_kernel(
                 load_hn(3)
                 for d in range(DIRS):
                     load_agg(1, d)
-            dr(nc.gpsimd, i, 2, side)
             gated_difference(nxt, 2)
             add_a(nxt, 2)
             differences(nxt + 1, 0)
+            some_passes(i, 5)
             quantise_agg(i - 1)
+            if i == 2:
+                passes(1, Z)
             for d in range(DIRS):
                 quantise_gate(i, Z, "z", d)
             dr(nc.vector, i, 0)
-            dr(nc.vector, i, 2, main)
+            dr(nc.vector, i, 2)
             for d in (2, 0, 1):
                 square(nxt, "r", d, -0.5)
             for d in range(DIRS):

@@ -30,8 +30,6 @@ M_TILES = COLS // M_TILE
 BANK = 512
 HALVES = PACK * COLS // BANK
 RUN = 4
-SIDE = 64
-HN_BY_MATMUL = (1, 2)
 
 FLOPS = 2 * DIRS * NODES * GATES * FEAT * FEAT
 BYTES = (
@@ -112,72 +110,71 @@ def tile_graphconvolution_pb_v_kernel(
             rows, cols = where(i)
             load_node(i, "h_n", F32, hn[0, rows, cols], 2)
 
+        def new_gate(i, name):
+            if name not in state[i]:
+                state[i][name] = gate_pool.tile([P, DIRS, PACK, COLS], F32, name=name, tag=name)
+            return state[i][name]
+
         def load_gate(i, name, gate, d, b=None):
             cb, nb = chunks[i]
             rows, cols = where(i)
-            key = (name, d)
-            if key not in state[i]:
-                state[i][key] = gate_pool.tile([P, PACK, COLS], F32, name=name, tag="%s%d" % (name, d))
             first = gate * FEAT + cb * COLS
             nc.sync.dma_start(
-                out=state[i][key][:, tokens(b)],
+                out=new_gate(i, name)[:, d, tokens(b)],
                 in_=rows_view(gates[d, 0, rows, first : first + COLS])[:, tokens(b), :],
             )
 
-        def load_cz(i, d, b=None):
-            load_gate(i, "c", C, d, b)
-            load_gate(i, "z", Z, d, b)
+        def load_cz(i, d):
+            load_gate(i, "c", C, d)
+            load_gate(i, "z", Z, d)
+
+        def load_r(i):
+            for d in range(DIRS):
+                load_gate(i, "r", R, d)
 
         def load_agg(i, d):
             rows, cols = where(i)
-            agg_rows = agg_pool.tile([P, PACK, FEAT], BF16, name="agg_rows", tag="agg_rows", bufs=DIRS)
+            agg_rows = agg_pool.tile([P, PACK, FEAT], BF16, name="agg_rows", tag="agg_rows")
             nc.sync.dma_start(out=agg_rows[:], in_=rows_view(agg[d, 0, rows, :]))
             state[i].setdefault("agg_rows", []).append(agg_rows)
 
+        def one(i, name, d, b=None):
+            return flat(state[i][name][:, d], b)
+
+        def every(i, name, b=None):
+            return state[i][name][:, :, tokens(b)].rearrange("p d j o -> p d (j o)")
+
+        def for_every(held):
+            return held[:].unsqueeze(1).to_broadcast([P, DIRS, BANK])
+
         def difference(i, d, b):
-            st = state[i]
-            diff = bank("a", b)
-            nc.tensor.matmul(out=diff[:], lhsT=identity_bf[:], rhs=flat(st["h"], b), start=True, stop=False)
-            nc.tensor.matmul(out=diff[:], lhsT=minus_identity[:], rhs=flat(st[("c", d)], b), start=False, stop=True)
-            return diff
-
-        def some_passes(i, k):
-            if i == 2:
-                if k == 0:
-                    open_acc(Z, "m", 0)
-                    open_acc(C, "m", 2)
-                multiply(0, (Z, C)[k // DIRS], k % DIRS)
-
-        diffs = {}
-
-        def differences(i, d):
-            if i < n_chunks:
-                for b in range(HALVES):
-                    diffs[b] = difference(i, d, b)
+            diff = bank("am"[d], b)
+            nc.tensor.matmul(out=diff[:], lhsT=identity_bf[:], rhs=flat(state[i]["h"], b), start=True, stop=False)
+            nc.tensor.matmul(out=diff[:], lhsT=minus_identity[:], rhs=one(i, "c", d, b), start=False, stop=True)
+            state[i][("diff", d, b)] = diff
 
         def blocks(b):
             return [(j, fb) for j in range(tokens(b).start, tokens(b).stop) for fb in range(M_TILES)]
 
-        def add_transposed(tot_t, b, held, first, stop):
+        def add_transposed(i, b, name, d, first, stop):
             todo = blocks(b)
             for k, (j, fb) in enumerate(todo):
                 nc.tensor.matmul(
-                    out=tot_t[:, k * P : (k + 1) * P], lhsT=held[:, j, fb * P : (fb + 1) * P],
+                    out=state[i][("tot_t", b)][:, k * P : (k + 1) * P],
+                    lhsT=state[i][name][:, d, j, fb * P : (fb + 1) * P],
                     rhs=identity[:], is_transpose=True,
                     start=(first and k == 0), stop=(stop and k == len(todo) - 1),
                 )
 
         def add_c(i, d, halves=(0, 1)):
-            if i < n_chunks:
-                for b in halves:
-                    if d == 0:
-                        state[i][("tot_t", b)] = bank("x", b)
-                    add_transposed(state[i][("tot_t", b)], b, state[i][("c", d)], d == 0, False)
+            for b in halves:
+                if d == 0:
+                    state[i][("tot_t", b)] = bank("x", b)
+                add_transposed(i, b, "c", d, d == 0, False)
 
         def add_a(i, d, halves=(0, 1)):
-            if i < n_chunks:
-                for b in halves:
-                    add_transposed(state[i][("tot_t", b)], b, state[i][("a", d)], False, d == DIRS - 1)
+            for b in halves:
+                add_transposed(i, b, "a", d, False, d == DIRS - 1)
 
         def turn(i, name, b, source, kind, k, factor):
             turned = bank(kind, k)
@@ -201,21 +198,11 @@ def tile_graphconvolution_pb_v_kernel(
                 )
             state[i][(name, b)] = held
 
-        def hn_to_psum(i, b, kind, k):
-            if i in HN_BY_MATMUL:
-                held = bank(kind, k)
-                nc.tensor.matmul(out=held[:], lhsT=identity[:], rhs=flat(state[i]["h_n"], b), start=True, stop=True)
-                state[i][("hn_back", b)] = held
-            else:
-                turn_back(i, "hn_back", b, "hn_t", kind, k)
-
-        def turn_dh(i, b):
+        def dh_back(i, b):
             turn_back(i, "dh", b, "dh_t", "x", b)
 
-        def times_t(i, b):
-            st = state[i]
-            st[("gt", b)] = st["t"]
-            nc.vector.tensor_tensor(out=flat(st["t"], b), in0=flat(st["g"], b), in1=flat(st["t"], b), op=ALU.mult)
+        def hn_back(i, b, kind, k):
+            turn_back(i, "hn", b, "hn_t", kind, k)
 
         def mask(i, b):
             st = state[i]
@@ -226,42 +213,45 @@ def tile_graphconvolution_pb_v_kernel(
             )
             st[("dh_t", b)] = dh_t
 
-        def new_a(i, d):
-            if ("a", d) not in state[i]:
-                state[i][("a", d)] = gate_pool.tile([P, PACK, COLS], F32, name="a", tag="a%d" % d)
+        def subtract_c(engine, i, d, b=None):
+            new_gate(i, "a")
+            engine.tensor_tensor(
+                out=one(i, "a", d, b), in0=flat(state[i]["h"], b), in1=one(i, "c", d, b), op=ALU.subtract
+            )
 
-        def gated_difference(i, d):
-            if i < n_chunks:
-                st = state[i]
-                new_a(i, d)
-                if ("side", d) in st:
-                    nc.vector.tensor_tensor(
-                        out=flat(st[("a", d)]), in0=flat(st[("z", d)]), in1=flat(st[("a", d)]), op=ALU.mult,
-                    )
-                else:
-                    for b in range(HALVES):
-                        nc.vector.tensor_tensor(
-                            out=flat(st[("a", d)], b), in0=flat(st[("z", d)], b), in1=diffs[b][:], op=ALU.mult,
-                        )
+        def times_z(i, d, b=None):
+            nc.vector.tensor_tensor(
+                out=one(i, "a", d, b), in0=one(i, "z", d, b), in1=one(i, "a", d, b), op=ALU.mult
+            )
 
-        def make_u(i, d, b):
-            st = state[i]
+        def times_z_psum(i, d):
+            new_gate(i, "a")
+            for b in range(HALVES):
+                nc.vector.tensor_tensor(
+                    out=one(i, "a", d, b), in0=one(i, "z", d, b), in1=state[i][("diff", d, b)][:], op=ALU.mult,
+                )
+
+        def make_u(i, b):
             nc.vector.scalar_tensor_tensor(
-                out=flat(st[("z", d)], b), in0=flat(st[("z", d)], b), scalar=1.0, in1=st[("dh", b)][:],
+                out=every(i, "z", b), in0=every(i, "z", b), scalar=1.0, in1=for_every(state[i][("dh", b)]),
                 op0=ALU.subtract, op1=ALU.mult,
             )
 
-        def make_dc(i, d, b=None):
-            st = state[i]
+        def make_e_of(i, d, b):
             nc.vector.scalar_tensor_tensor(
-                out=flat(st[("a", d)], b), in0=flat(st[("c", d)], b), scalar=1.0, in1=flat(st[("z", d)], b),
+                out=one(i, "r", d, b), in0=one(i, "r", d, b), scalar=0.25, in1=state[i][("hn", b)][:],
                 op0=ALU.subtract, op1=ALU.mult,
             )
 
-        def make_e(i, d, b):
-            st = state[i]
+        def make_e(i, b):
             nc.vector.scalar_tensor_tensor(
-                out=flat(st[("r", d)], b), in0=flat(st[("r", d)], b), scalar=0.25, in1=st[("hn_back", b)][:],
+                out=every(i, "r", b), in0=every(i, "r", b), scalar=0.25, in1=for_every(state[i][("hn", b)]),
+                op0=ALU.subtract, op1=ALU.mult,
+            )
+
+        def make_dc(i, b=None):
+            nc.vector.scalar_tensor_tensor(
+                out=every(i, "a", b), in0=every(i, "c", b), scalar=1.0, in1=every(i, "z", b),
                 op0=ALU.subtract, op1=ALU.mult,
             )
 
@@ -271,13 +261,11 @@ def tile_graphconvolution_pb_v_kernel(
                 state[i][key] = grouped_pool.tile([P, COLS, PACK], BF16, name="grouped", tag="grouped", align_bytes=64)
             return state[i][key]
 
-        def product_grouped(engine, i, name, in0, in1, d, cols=slice(0, COLS), b=None):
-            st = state[i]
-            made = new_grouped(i, name, d)
+        def product_grouped(engine, i, name, in0, in1, d, cols, b):
             engine.tensor_tensor(
-                out=made[:, cols, tokens(b)].rearrange("p (c i) j -> p c j i", i=RUN),
-                in0=st[(in0, d)][:, tokens(b), cols].rearrange("p j (c i) -> p c j i", i=RUN),
-                in1=st[(in1, d)][:, tokens(b), cols].rearrange("p j (c i) -> p c j i", i=RUN),
+                out=new_grouped(i, name, d)[:, cols, tokens(b)].rearrange("p (c i) j -> p c j i", i=RUN),
+                in0=state[i][in0][:, d, tokens(b), cols].rearrange("p j (c i) -> p c j i", i=RUN),
+                in1=state[i][in1][:, d, tokens(b), cols].rearrange("p j (c i) -> p c j i", i=RUN),
                 op=ALU.mult,
             )
 
@@ -285,7 +273,7 @@ def tile_graphconvolution_pb_v_kernel(
             product_grouped(engine, i, "z", "z", "a", d, cols, b)
 
         def dr(engine, i, d, cols=slice(0, COLS)):
-            product_grouped(engine, i, "r", "r", "a", d, cols)
+            product_grouped(engine, i, "r", "r", "a", d, cols, None)
 
         def quantise(grouped, x4_dtype, codes, scales):
             nc.vector.quantize_mx(
@@ -303,9 +291,11 @@ def tile_graphconvolution_pb_v_kernel(
             for d in range(DIRS):
                 quantise(state[i]["agg_grouped"][d], E4M3_X4, agg_codes[:, nb, d, :], agg_scales[:, nb, d, :])
 
-        def square(i, name, d, bias, b=None):
-            held = state[i][(name, d)]
-            nc.scalar.activation(out=flat(held, b), in_=flat(held, b), func=ACT.Square, bias=bias)
+        def square(i, name, bias, b=None):
+            nc.scalar.activation(out=every(i, name, b), in_=every(i, name, b), func=ACT.Square, bias=bias)
+
+        def square_of(i, name, d, bias):
+            nc.scalar.activation(out=one(i, name, d), in_=one(i, name, d), func=ACT.Square, bias=bias)
 
         def regroup(grouped, values, factor):
             nc.scalar.activation(
@@ -314,27 +304,19 @@ def tile_graphconvolution_pb_v_kernel(
                 func=ACT.Copy, scale=factor,
             )
 
-        def regroup_dc(i, d):
-            regroup(new_grouped(i, "c", d)[:], state[i][("a", d)][:], -1.0)
+        def regroup_dc(i):
+            for d in range(DIRS):
+                regroup(new_grouped(i, "c", d)[:], state[i]["a"][:, d], -1.0)
 
         def regroup_agg(i, d):
             grouped = agg_pool.tile([P, FEAT, PACK], BF16, name="agg_grouped", tag="agg_grouped", align_bytes=64)
             regroup(grouped[:], state[i]["agg_rows"][d][:], 1.0)
             state[i].setdefault("agg_grouped", []).append(grouped)
 
-        def side_gt(i, held, b=None):
-            st = state[i]
-            nc.gpsimd.tensor_tensor(out=flat(held, b), in0=flat(st["g"], b), in1=flat(st["t"], b), op=ALU.mult)
+        def times_t(engine, i, b, held):
+            engine.tensor_tensor(out=flat(held, b), in0=flat(state[i]["g"], b), in1=flat(state[i]["t"], b), op=ALU.mult)
             for half in range(HALVES) if b is None else (b,):
-                st[("gt", half)] = held
-
-        def side_difference(i, d):
-            new_a(i, d)
-            st = state[i]
-            st[("side", d)] = True
-            nc.gpsimd.tensor_tensor(
-                out=flat(st[("a", d)]), in0=flat(st["h"]), in1=flat(st[("c", d)]), op=ALU.subtract
-            )
+                state[i][("gt", half)] = held
 
         def open_acc(gate, kind, first):
             for m in range(M_TILES):
@@ -356,22 +338,20 @@ def tile_graphconvolution_pb_v_kernel(
             for d in range(DIRS):
                 multiply(i, gate, d)
 
-        def store(i, gate, shared_out=False, spare=False):
+        def store(i, gate, last_of_all=False):
             cb, nb = chunks[i]
             for m in range(M_TILES):
-                if spare:
+                if last_of_all:
                     result = result_pool.tile([M_TILE, FEAT], F32, name="last_result", tag="last_result", bufs=2)
                 else:
                     result = result_pool.tile([M_TILE, FEAT], F32, name="result", tag="result")
-                if shared_out and m == 0:
+                if last_of_all and m == 0:
                     nc.vector.tensor_copy(out=result[:], in_=acc[(gate, m)][:])
                 else:
                     nc.scalar.copy(out=result[:], in_=acc[(gate, m)][:])
                 first = gate * FEAT + cb * COLS + m * M_TILE
                 nc.sync.dma_start(out=out[first : first + M_TILE, :], in_=result[:])
 
-        main = slice(0, COLS - SIDE)
-        side = slice(COLS - SIDE, COLS)
         for b in range(HALVES):
             load_h(0, b)
             for d in range(DIRS):
@@ -382,180 +362,157 @@ def tile_graphconvolution_pb_v_kernel(
         load_h(1)
         load_gt(1)
         load_hn(0)
-        load_gate(0, "r", R, 2)
         load_cz(1, 0)
-        load_gate(0, "r", R, 0)
-        load_gate(0, "r", R, 1)
+        load_r(0)
         load_cz(1, 1)
         load_cz(1, 2)
         load_hn(1)
-        load_h(2)
         load_gt(2)
-        for d in (2, 0, 1):
-            load_gate(1, "r", R, d)
-
-        st0 = state[0]
-
-        def first_difference(b, d):
-            new_a(0, d)
-            nc.vector.tensor_tensor(
-                out=flat(st0[("a", d)], b), in0=flat(st0["h"], b), in1=flat(st0[("c", d)], b), op=ALU.subtract,
-            )
-
-        def first_a(b, d):
-            nc.vector.tensor_tensor(
-                out=flat(st0[("a", d)], b), in0=flat(st0[("z", d)], b), in1=flat(st0[("a", d)], b), op=ALU.mult,
-            )
-            add_a(0, d, (b,))
+        load_h(2)
+        load_r(1)
 
         for d in range(DIRS):
             add_c(0, d, (0,))
-            first_difference(0, d)
-        times_t(0, 0)
+            subtract_c(nc.vector, 0, d, 0)
+        times_t(nc.vector, 0, 0, state[0]["t"])
         turn_gt(0, 0, "a", 0)
+        square(0, "c", 0.0, 0)
         for d in range(DIRS):
-            square(0, "c", d, 0.0, 0)
-        for d in range(DIRS):
-            first_a(0, d)
+            times_z(0, d, 0)
+            add_a(0, d, (0,))
         mask(0, 0)
-        turn_dh(0, 0)
+        dh_back(0, 0)
         for d in range(DIRS):
             add_c(0, d, (1,))
-            first_difference(1, d)
-        for d in range(DIRS):
-            make_u(0, d, 0)
-        times_t(0, 1)
+            subtract_c(nc.vector, 0, d, 1)
+        make_u(0, 0)
+        times_t(nc.vector, 0, 1, state[0]["t"])
         turn_gt(0, 1, "a", 1)
-        for d in range(DIRS - 1):
-            dz(nc.vector, 0, d, 0)
+        square(0, "c", 0.0, 1)
         for d in range(DIRS):
-            square(0, "c", d, 0.0, 1)
-        for d in range(DIRS):
-            first_a(1, d)
-        for d in range(DIRS - 1):
-            make_dc(0, d, 0)
+            times_z(0, d, 1)
+            add_a(0, d, (1,))
         mask(0, 1)
-        turn_dh(0, 1)
-        square(0, "r", 2, -0.5)
+        dh_back(0, 1)
         for b in range(HALVES):
             turn_hn(0, b, "m", 2 + b)
-        for d in (0, 1):
-            square(0, "r", d, -0.5)
-        for b in range(HALVES):
-            hn_to_psum(0, b, "m", 2 + b)
-        side_gt(1, st0[("c", 1)], 0)
-        side_difference(1, 0)
-        side_gt(1, state[1]["t"], 1)
-        turn_gt(1, 0, "m", 0)
-        for d in (2, 0, 1):
-            make_u(0, d, 1)
-        dz(nc.gpsimd, 0, 2)
-        side_difference(1, 2)
-        diffs[0] = difference(1, 1, 0)
-        turn_gt(1, 1, "m", 1)
-        diffs[1] = difference(1, 1, 1)
-        for d in (2, 0, 1):
-            for b in range(HALVES):
-                make_e(0, d, b)
-        gated_difference(1, 0)
-        gated_difference(1, 1)
-        add_c(1, 0)
-        add_a(1, 0)
-        add_c(1, 1)
-        add_a(1, 1)
-        for d in range(DIRS - 1):
-            dz(nc.vector, 0, d, 1)
-        for d in range(DIRS - 1):
-            make_dc(0, d, 1)
-            regroup_dc(0, d)
-        make_dc(0, 2)
-        regroup_dc(0, 2)
-        load_cz(2, 0)
-        load_cz(2, 1)
-        load_hn(2)
-        load_cz(2, 2)
         for d in range(DIRS):
-            load_agg(0, d)
-        load_h(3)
-        gated_difference(1, 2)
-        add_c(1, 2)
-        add_a(1, 2)
-        differences(2, 0)
+            square_of(0, "r", d, -0.5)
+        for b in range(HALVES):
+            hn_back(0, b, "m", 2 + b)
+        for d in range(DIRS - 1):
+            for b in range(HALVES):
+                difference(1, d, b)
+        times_t(nc.gpsimd, 1, 0, state[1]["t"])
+        turn_gt(1, 0, "x", 0)
+        make_u(0, 1)
+        for d in range(DIRS):
+            dz(nc.vector, 0, d)
+        make_dc(0)
+        times_t(nc.gpsimd, 1, 1, state[0]["c"][:, 2])
+        turn_gt(1, 1, "x", 1)
+        regroup_dc(0)
+        for d in range(DIRS):
+            for b in range(HALVES):
+                make_e_of(0, d, b)
+        times_z_psum(1, 0)
+        for d in range(DIRS):
+            add_c(1, d)
+        add_a(1, 0)
         for d in range(DIRS):
             quantise_gate(0, Z, "z", d)
         dr(nc.vector, 0, 0)
+        times_z_psum(1, 1)
+        add_a(1, 1)
         dr(nc.vector, 0, 2)
+        subtract_c(nc.vector, 1, 2)
+        times_z(1, 2)
+        add_a(1, 2)
+        load_cz(2, 0)
+        load_gate(2, "c", C, 2)
+        load_cz(2, 1)
+        load_gate(2, "z", Z, 2)
+        load_hn(2)
+        load_h(3)
+        load_gt(3)
+        for d in range(DIRS):
+            load_agg(0, d)
         for d in range(DIRS):
             quantise_gate(0, C, "c", d)
         quantise_gate(0, R, "r", 0)
+        quantise_gate(0, R, "r", 2)
+        for b in range(HALVES):
+            turn_hn(1, b, "m", 2 + b)
         dr(nc.vector, 0, 1)
-        for d in (2, 0, 1):
-            square(1, "r", d, -0.5)
+        for b in range(HALVES):
+            square(1, "r", -0.5, b)
+
+        def some_passes(i, k):
+            if i == 2:
+                if k == 0:
+                    open_acc(Z, "m", 0)
+                    open_acc(C, "m", 2)
+                multiply(0, (Z, C)[k // DIRS], k % DIRS)
 
         for i in range(1, n_chunks):
             nxt = i + 1
             has_next = nxt < n_chunks
             if has_next:
-                side_gt(nxt, state[i - 1][("r", 1)])
-                side_difference(nxt, 2)
+                times_t(nc.gpsimd, nxt, None, state[i - 1]["r"][:, 1])
+                subtract_c(nc.gpsimd, nxt, 2)
             for b in range(HALVES):
                 mask(i, b)
             for b in range(HALVES):
-                turn_dh(i, b)
-            for d in range(DIRS):
-                square(i, "c", d, 0.0)
-            if has_next:
-                gated_difference(nxt, 0)
-                diffs[0] = difference(nxt, 1, 0)
-                regroup_agg(i - 1, 0)
-            else:
-                quantise_gate(i - 1, R, "r", 2)
+                dh_back(i, b)
+            square(i, "c", 0.0)
+            if not has_next:
                 quantise_gate(i - 1, R, "r", 1)
-                passes(1, C)
-            for d, b in ((2, 0), (2, 1), (0, 0), (1, 0), (0, 1), (1, 1)):
-                make_u(i, d, b)
+                quantise_agg(1)
+                passes(1, Z)
+            for b in range(HALVES):
+                make_u(i, b)
             dz(nc.gpsimd, i, 2)
-            dz(nc.gpsimd, i, 0)
-            for b in range(HALVES):
-                hn_to_psum(i, b, "x", b)
             if has_next:
-                diffs[1] = difference(nxt, 1, 1)
-            else:
-                store(1, Z)
-                store(1, C)
-                open_acc(R, "a", 0)
-                passes(0, R)
-                passes(1, R)
+                dz(nc.gpsimd, i, 0)
             for b in range(HALVES):
-                for d in (2, 0, 1):
-                    make_e(i, d, b)
+                if has_next:
+                    difference(nxt, 0, b)
+                hn_back(i, b, "x", b)
+            for b in range(HALVES):
+                make_e(i, b)
             if has_next:
-                some_passes(i, 0)
-                if nxt not in HN_BY_MATMUL:
-                    for b in range(HALVES):
-                        turn_hn(nxt, b, "x", b)
+                load_r(nxt)
+                for b in range(HALVES):
+                    difference(nxt, 1, b)
                 for b in range(HALVES):
                     turn_gt(nxt, b, "x", b)
-                regroup_agg(i - 1, 1)
-                regroup_agg(i - 1, 2)
-                gated_difference(nxt, 1)
-                some_passes(i, 1)
+                for b in range(HALVES):
+                    turn_hn(nxt, b, "x", b)
+                if i == 2:
+                    regroup_agg(1, 0)
+                    regroup_agg(1, 1)
+                times_z_psum(nxt, 0)
+                times_z_psum(nxt, 1)
                 add_c(nxt, 0)
                 add_a(nxt, 0)
-                some_passes(i, 2)
                 add_c(nxt, 1)
                 add_a(nxt, 1)
-                some_passes(i, 3)
                 add_c(nxt, 2)
-                some_passes(i, 4)
-                quantise_gate(i - 1, R, "r", 2)
                 quantise_gate(i - 1, R, "r", 1)
-                for d in (2, 0, 1):
-                    load_gate(nxt, "r", R, d)
+                if i == 2:
+                    quantise_agg(0)
+                for k in range(4):
+                    some_passes(i, k)
+            else:
+                store(1, Z)
+                passes(1, C)
+                store(1, C)
+                passes(1, R)
             dz(nc.vector, i, 1)
-            for d in (1, 0, 2):
-                make_dc(i, d)
-                regroup_dc(i, d)
+            if not has_next:
+                dz(nc.vector, i, 0)
+            make_dc(i)
+            regroup_dc(i)
             if not has_next:
                 store(1, R)
                 open_acc(Z, "m", 0)
@@ -567,28 +524,33 @@ def tile_graphconvolution_pb_v_kernel(
                 break
             if i == 1:
                 load_cz(3, 0)
-                load_gt(3)
+                load_gate(3, "c", C, 2)
                 load_cz(3, 1)
-                load_cz(3, 2)
+                load_gate(3, "z", Z, 2)
                 load_hn(3)
                 for d in range(DIRS):
                     load_agg(1, d)
-            gated_difference(nxt, 2)
-            add_a(nxt, 2)
-            differences(nxt + 1, 0)
-            some_passes(i, 5)
-            quantise_agg(i - 1)
-            if i == 2:
-                passes(1, Z)
             for d in range(DIRS):
                 quantise_gate(i, Z, "z", d)
             dr(nc.vector, i, 0)
+            times_z(nxt, 2)
+            add_a(nxt, 2)
+            some_passes(i, 4)
+            some_passes(i, 5)
+            if i == 2:
+                open_acc(R, "a", 0)
+                passes(0, R)
             dr(nc.vector, i, 2)
-            for d in (2, 0, 1):
-                square(nxt, "r", d, -0.5)
+            if i == 1:
+                regroup_agg(0, 0)
+                regroup_agg(0, 1)
+            for b in range(HALVES):
+                square(nxt, "r", -0.5, b)
+            regroup_agg(i - 1, 2)
             for d in range(DIRS):
                 quantise_gate(i, C, "c", d)
             quantise_gate(i, R, "r", 0)
+            quantise_gate(i, R, "r", 2)
             dr(nc.vector, i, 1)
 
         for d in range(DIRS):
@@ -606,4 +568,4 @@ def tile_graphconvolution_pb_v_kernel(
                 store(last, C)
         quantise_gate(last, R, "r", DIRS - 1)
         multiply(last, R, DIRS - 1)
-        store(last, R, True, True)
+        store(last, R, True)

@@ -56,7 +56,7 @@ def tile_graphconvolution_pb_v_kernel(
         agg_pool = ctx.enter_context(tc.tile_pool(name="agg", bufs=DIRS))
         mx_pool = ctx.enter_context(tc.tile_pool(name="dgi_mx", bufs=22))
         keep_pool = ctx.enter_context(tc.tile_pool(name="keep", bufs=1))
-        result_pool = ctx.enter_context(tc.tile_pool(name="result", bufs=4))
+        result_pool = ctx.enter_context(tc.tile_pool(name="result", bufs=6))
         psum = ctx.enter_context(tc.psum_pool(name="psum", bufs=1))
         ctx.enter_context(tc.manual_schedule())
 
@@ -237,6 +237,12 @@ def tile_graphconvolution_pb_v_kernel(
                 op0=ALU.subtract, op1=ALU.mult,
             )
 
+        def make_u_of(i, d, b):
+            nc.vector.scalar_tensor_tensor(
+                out=one(i, "z", d, b), in0=one(i, "z", d, b), scalar=1.0, in1=state[i][("dh", b)][:],
+                op0=ALU.subtract, op1=ALU.mult,
+            )
+
         def make_e_of(i, d, b):
             nc.vector.scalar_tensor_tensor(
                 out=one(i, "r", d, b), in0=one(i, "r", d, b), scalar=0.25, in1=state[i][("hn", b)][:],
@@ -246,6 +252,12 @@ def tile_graphconvolution_pb_v_kernel(
         def make_e(i, b):
             nc.vector.scalar_tensor_tensor(
                 out=every(i, "r", b), in0=every(i, "r", b), scalar=0.25, in1=for_every(state[i][("hn", b)]),
+                op0=ALU.subtract, op1=ALU.mult,
+            )
+
+        def make_dc_of(i, d):
+            nc.vector.scalar_tensor_tensor(
+                out=one(i, "a", d), in0=one(i, "c", d), scalar=1.0, in1=one(i, "z", d),
                 op0=ALU.subtract, op1=ALU.mult,
             )
 
@@ -304,8 +316,8 @@ def tile_graphconvolution_pb_v_kernel(
                 func=ACT.Copy, scale=factor,
             )
 
-        def regroup_dc(i):
-            for d in range(DIRS):
+        def regroup_dc(i, dirs=range(DIRS)):
+            for d in dirs:
                 regroup(new_grouped(i, "c", d)[:], state[i]["a"][:, d], -1.0)
 
         def regroup_agg(i, d):
@@ -338,14 +350,11 @@ def tile_graphconvolution_pb_v_kernel(
             for d in range(DIRS):
                 multiply(i, gate, d)
 
-        def store(i, gate, last_of_all=False):
+        def store(i, gate, shared=False):
             cb, nb = chunks[i]
             for m in range(M_TILES):
-                if last_of_all:
-                    result = result_pool.tile([M_TILE, FEAT], F32, name="last_result", tag="last_result", bufs=2)
-                else:
-                    result = result_pool.tile([M_TILE, FEAT], F32, name="result", tag="result")
-                if last_of_all and m == 0:
+                result = result_pool.tile([M_TILE, FEAT], F32, name="result", tag="result")
+                if shared and m == 0:
                     nc.vector.tensor_copy(out=result[:], in_=acc[(gate, m)][:])
                 else:
                     nc.scalar.copy(out=result[:], in_=acc[(gate, m)][:])
@@ -362,8 +371,8 @@ def tile_graphconvolution_pb_v_kernel(
         load_h(1)
         load_gt(1)
         load_hn(0)
-        load_cz(1, 0)
         load_r(0)
+        load_cz(1, 0)
         load_cz(1, 1)
         load_cz(1, 2)
         load_hn(1)
@@ -406,16 +415,20 @@ def tile_graphconvolution_pb_v_kernel(
         times_t(nc.gpsimd, 1, 0, state[1]["t"])
         turn_gt(1, 0, "x", 0)
         make_u(0, 1)
-        for d in range(DIRS):
+        for d in range(DIRS - 1):
             dz(nc.vector, 0, d)
-        make_dc(0)
-        times_t(nc.gpsimd, 1, 1, state[0]["c"][:, 2])
+        for d in range(DIRS - 1):
+            make_dc_of(0, d)
+        times_t(nc.gpsimd, 1, 1, state[0]["c"][:, 1])
+        dz(nc.gpsimd, 0, 2)
         turn_gt(1, 1, "x", 1)
-        regroup_dc(0)
+        regroup_dc(0, (0, 1))
         for d in range(DIRS):
             for b in range(HALVES):
                 make_e_of(0, d, b)
         times_z_psum(1, 0)
+        make_dc_of(0, 2)
+        regroup_dc(0, (2,))
         for d in range(DIRS):
             add_c(1, d)
         add_a(1, 0)
@@ -459,7 +472,6 @@ def tile_graphconvolution_pb_v_kernel(
             has_next = nxt < n_chunks
             if has_next:
                 times_t(nc.gpsimd, nxt, None, state[i - 1]["r"][:, 1])
-                subtract_c(nc.gpsimd, nxt, 2)
             for b in range(HALVES):
                 mask(i, b)
             for b in range(HALVES):
@@ -469,11 +481,12 @@ def tile_graphconvolution_pb_v_kernel(
                 quantise_gate(i - 1, R, "r", 1)
                 quantise_agg(1)
                 passes(1, Z)
-            for b in range(HALVES):
-                make_u(i, b)
+            for d, b in ((2, 0), (2, 1), (0, 0), (1, 0), (0, 1), (1, 1)):
+                make_u_of(i, d, b)
             dz(nc.gpsimd, i, 2)
             if has_next:
-                dz(nc.gpsimd, i, 0)
+                subtract_c(nc.gpsimd, nxt, 2)
+            dz(nc.gpsimd, i, 0)
             for b in range(HALVES):
                 if has_next:
                     difference(nxt, 0, b)
@@ -508,13 +521,11 @@ def tile_graphconvolution_pb_v_kernel(
                 passes(1, C)
                 store(1, C)
                 passes(1, R)
+                store(1, R)
             dz(nc.vector, i, 1)
-            if not has_next:
-                dz(nc.vector, i, 0)
             make_dc(i)
             regroup_dc(i)
             if not has_next:
-                store(1, R)
                 open_acc(Z, "m", 0)
                 open_acc(C, "m", 2)
                 open_acc(R, "x", 0)
@@ -557,15 +568,16 @@ def tile_graphconvolution_pb_v_kernel(
             quantise_gate(last, Z, "z", d)
         passes(last, Z)
         store(last, Z)
+        dr(nc.vector, last, 0)
+        dr(nc.vector, last, 1)
         for d in range(DIRS):
             quantise_gate(last, C, "c", d)
             multiply(last, C, d)
-            dr(nc.vector, last, d)
-            if d > 0:
-                quantise_gate(last, R, "r", d - 1)
-                multiply(last, R, d - 1)
-            if d == DIRS - 1:
-                store(last, C)
-        quantise_gate(last, R, "r", DIRS - 1)
-        multiply(last, R, DIRS - 1)
+        quantise_gate(last, R, "r", 0)
+        multiply(last, R, 0)
+        dr(nc.vector, last, 2)
+        for d in (1, 2):
+            quantise_gate(last, R, "r", d)
+            multiply(last, R, d)
+        store(last, C, True)
         store(last, R, True)

@@ -69,6 +69,7 @@ def tile_graphconvolution_pb_v_kernel(
         agg_codes = keep_pool.tile([P, NODE_BLOCKS, DIRS, FEAT], U32, name="agg_codes", align_bytes=64)
         agg_scales = keep_pool.tile([P, NODE_BLOCKS, DIRS, FEAT], U8, name="agg_scales", align_bytes=64)
 
+        ALL_DIRS = slice(0, DIRS)
         state = [dict() for i in range(n_chunks)]
         acc = {}
 
@@ -141,14 +142,14 @@ def tile_graphconvolution_pb_v_kernel(
         def one(i, name, d, b=None):
             return flat(state[i][name][:, d], b)
 
-        def every(i, name, b=None):
-            return state[i][name][:, :, tokens(b)].rearrange("p d j o -> p d (j o)")
+        def some(i, name, dirs, b=None):
+            return state[i][name][:, dirs, tokens(b)].rearrange("p d j o -> p d (j o)")
 
-        def for_every(held):
-            return held[:].unsqueeze(1).to_broadcast([P, DIRS, BANK])
+        def for_some(held, dirs):
+            return held[:].unsqueeze(1).to_broadcast([P, dirs.stop - dirs.start, BANK])
 
         def difference(i, d, b):
-            diff = bank("am"[d], b)
+            diff = bank("ama"[d], b)
             nc.tensor.matmul(out=diff[:], lhsT=identity_bf[:], rhs=flat(state[i]["h"], b), start=True, stop=False)
             nc.tensor.matmul(out=diff[:], lhsT=minus_identity[:], rhs=one(i, "c", d, b), start=False, stop=True)
             state[i][("diff", d, b)] = diff
@@ -231,39 +232,21 @@ def tile_graphconvolution_pb_v_kernel(
                     out=one(i, "a", d, b), in0=one(i, "z", d, b), in1=state[i][("diff", d, b)][:], op=ALU.mult,
                 )
 
-        def make_u(i, b):
+        def make_u(i, b, dirs=ALL_DIRS):
             nc.vector.scalar_tensor_tensor(
-                out=every(i, "z", b), in0=every(i, "z", b), scalar=1.0, in1=for_every(state[i][("dh", b)]),
+                out=some(i, "z", dirs, b), in0=some(i, "z", dirs, b), scalar=1.0, in1=for_some(state[i][("dh", b)], dirs),
                 op0=ALU.subtract, op1=ALU.mult,
             )
 
-        def make_u_of(i, d, b):
+        def make_e(i, b, dirs=ALL_DIRS):
             nc.vector.scalar_tensor_tensor(
-                out=one(i, "z", d, b), in0=one(i, "z", d, b), scalar=1.0, in1=state[i][("dh", b)][:],
+                out=some(i, "r", dirs, b), in0=some(i, "r", dirs, b), scalar=0.25, in1=for_some(state[i][("hn", b)], dirs),
                 op0=ALU.subtract, op1=ALU.mult,
             )
 
-        def make_e_of(i, d, b):
+        def make_dc(i, dirs=ALL_DIRS):
             nc.vector.scalar_tensor_tensor(
-                out=one(i, "r", d, b), in0=one(i, "r", d, b), scalar=0.25, in1=state[i][("hn", b)][:],
-                op0=ALU.subtract, op1=ALU.mult,
-            )
-
-        def make_e(i, b):
-            nc.vector.scalar_tensor_tensor(
-                out=every(i, "r", b), in0=every(i, "r", b), scalar=0.25, in1=for_every(state[i][("hn", b)]),
-                op0=ALU.subtract, op1=ALU.mult,
-            )
-
-        def make_dc_of(i, d):
-            nc.vector.scalar_tensor_tensor(
-                out=one(i, "a", d), in0=one(i, "c", d), scalar=1.0, in1=one(i, "z", d),
-                op0=ALU.subtract, op1=ALU.mult,
-            )
-
-        def make_dc(i, b=None):
-            nc.vector.scalar_tensor_tensor(
-                out=every(i, "a", b), in0=every(i, "c", b), scalar=1.0, in1=every(i, "z", b),
+                out=some(i, "a", dirs), in0=some(i, "c", dirs), scalar=1.0, in1=some(i, "z", dirs),
                 op0=ALU.subtract, op1=ALU.mult,
             )
 
@@ -289,25 +272,26 @@ def tile_graphconvolution_pb_v_kernel(
 
         def quantise(grouped, x4_dtype, codes, scales):
             nc.vector.quantize_mx(
-                out=codes.bitcast(x4_dtype), scales=scales, in_=grouped[:].rearrange("p o j -> p (o j)"),
+                out=codes.bitcast(x4_dtype), scales=scales, in_=grouped.rearrange("p o j -> p (o j)"),
             )
 
-        def quantise_gate(i, gate, name, d):
-            codes = mx_pool.tile([P, COLS], U32, name="codes", tag="codes", align_bytes=64)
-            scales = mx_pool.tile([P, COLS], U8, name="scales", tag="scales", align_bytes=64)
-            quantise(state[i][("grouped_" + name, d)], E5M2_X4, codes[:], scales[:])
-            state[i][(gate, d)] = (codes, scales)
+        def quantise_gate(i, gate, name, d, cols=slice(0, COLS)):
+            if (gate, d) not in state[i]:
+                codes = mx_pool.tile([P, COLS], U32, name="codes", tag="codes", align_bytes=64)
+                scales = mx_pool.tile([P, COLS], U8, name="scales", tag="scales", align_bytes=64)
+                state[i][(gate, d)] = (codes, scales)
+            codes, scales = state[i][(gate, d)]
+            quantise(state[i][("grouped_" + name, d)][:, cols], E5M2_X4, codes[:, cols], scales[:, cols])
 
         def quantise_agg(i):
             cb, nb = chunks[i]
             for d in range(DIRS):
-                quantise(state[i]["agg_grouped"][d], E4M3_X4, agg_codes[:, nb, d, :], agg_scales[:, nb, d, :])
+                quantise(state[i]["agg_grouped"][d][:], E4M3_X4, agg_codes[:, nb, d, :], agg_scales[:, nb, d, :])
 
-        def square(i, name, bias, b=None):
-            nc.scalar.activation(out=every(i, name, b), in_=every(i, name, b), func=ACT.Square, bias=bias)
-
-        def square_of(i, name, d, bias):
-            nc.scalar.activation(out=one(i, name, d), in_=one(i, name, d), func=ACT.Square, bias=bias)
+        def square(i, name, bias, b=None, dirs=ALL_DIRS):
+            nc.scalar.activation(
+                out=some(i, name, dirs, b), in_=some(i, name, dirs, b), func=ACT.Square, bias=bias
+            )
 
         def regroup(grouped, values, factor):
             nc.scalar.activation(
@@ -334,10 +318,10 @@ def tile_graphconvolution_pb_v_kernel(
             for m in range(M_TILES):
                 acc[(gate, m)] = bank(kind, first + m)
 
-        def multiply(i, gate, d):
+        def multiply(i, gate, d, tiles=range(M_TILES)):
             cb, nb = chunks[i]
             codes, scales = state[i][(gate, d)]
-            for m in range(M_TILES):
+            for m in tiles:
                 m_cols = slice(m * M_TILE, (m + 1) * M_TILE)
                 nc.tensor.matmul_mx(
                     out=acc[(gate, m)][:],
@@ -350,14 +334,20 @@ def tile_graphconvolution_pb_v_kernel(
             for d in range(DIRS):
                 multiply(i, gate, d)
 
-        def store(i, gate, shared=False):
+        def store_halves(i, gate, m):
+            cb, nb = chunks[i]
+            first = gate * FEAT + cb * COLS + m * M_TILE
+            result = result_pool.tile([M_TILE, FEAT], F32, name="result", tag="result")
+            for k, copy in enumerate((nc.vector.tensor_copy, nc.scalar.copy)):
+                half = slice(k * FEAT // 2, (k + 1) * FEAT // 2)
+                copy(out=result[:, half], in_=acc[(gate, m)][:, half])
+                nc.sync.dma_start(out=out[first : first + M_TILE, half], in_=result[:, half])
+
+        def store(i, gate):
             cb, nb = chunks[i]
             for m in range(M_TILES):
                 result = result_pool.tile([M_TILE, FEAT], F32, name="result", tag="result")
-                if shared and m == 0:
-                    nc.vector.tensor_copy(out=result[:], in_=acc[(gate, m)][:])
-                else:
-                    nc.scalar.copy(out=result[:], in_=acc[(gate, m)][:])
+                nc.scalar.copy(out=result[:], in_=acc[(gate, m)][:])
                 first = gate * FEAT + cb * COLS + m * M_TILE
                 nc.sync.dma_start(out=out[first : first + M_TILE, :], in_=result[:])
 
@@ -406,7 +396,7 @@ def tile_graphconvolution_pb_v_kernel(
         for b in range(HALVES):
             turn_hn(0, b, "m", 2 + b)
         for d in range(DIRS):
-            square_of(0, "r", d, -0.5)
+            square(0, "r", -0.5, None, slice(d, d + 1))
         for b in range(HALVES):
             hn_back(0, b, "m", 2 + b)
         for d in range(DIRS - 1):
@@ -417,17 +407,16 @@ def tile_graphconvolution_pb_v_kernel(
         make_u(0, 1)
         for d in range(DIRS - 1):
             dz(nc.vector, 0, d)
-        for d in range(DIRS - 1):
-            make_dc_of(0, d)
+        make_dc(0, slice(0, 2))
         times_t(nc.gpsimd, 1, 1, state[0]["c"][:, 1])
         dz(nc.gpsimd, 0, 2)
         turn_gt(1, 1, "x", 1)
         regroup_dc(0, (0, 1))
         for d in range(DIRS):
             for b in range(HALVES):
-                make_e_of(0, d, b)
+                make_e(0, b, slice(d, d + 1))
         times_z_psum(1, 0)
-        make_dc_of(0, 2)
+        make_dc(0, slice(2, 3))
         regroup_dc(0, (2,))
         for d in range(DIRS):
             add_c(1, d)
@@ -481,12 +470,16 @@ def tile_graphconvolution_pb_v_kernel(
                 quantise_gate(i - 1, R, "r", 1)
                 quantise_agg(1)
                 passes(1, Z)
-            for d, b in ((2, 0), (2, 1), (0, 0), (1, 0), (0, 1), (1, 1)):
-                make_u_of(i, d, b)
+                passes(1, C)
+            for dirs in (slice(2, 3), slice(0, 2)):
+                for b in range(HALVES):
+                    make_u(i, b, dirs)
             dz(nc.gpsimd, i, 2)
-            if has_next:
+            if i == 2:
                 subtract_c(nc.gpsimd, nxt, 2)
             dz(nc.gpsimd, i, 0)
+            if i == 1:
+                dz(nc.gpsimd, i, 1)
             for b in range(HALVES):
                 if has_next:
                     difference(nxt, 0, b)
@@ -507,6 +500,9 @@ def tile_graphconvolution_pb_v_kernel(
                 times_z_psum(nxt, 0)
                 times_z_psum(nxt, 1)
                 add_c(nxt, 0)
+                if i == 1:
+                    for b in range(HALVES):
+                        difference(nxt, 2, b)
                 add_a(nxt, 0)
                 add_c(nxt, 1)
                 add_a(nxt, 1)
@@ -518,11 +514,11 @@ def tile_graphconvolution_pb_v_kernel(
                     some_passes(i, k)
             else:
                 store(1, Z)
-                passes(1, C)
                 store(1, C)
                 passes(1, R)
                 store(1, R)
-            dz(nc.vector, i, 1)
+            if i > 1:
+                dz(nc.vector, i, 1)
             make_dc(i)
             regroup_dc(i)
             if not has_next:
@@ -544,14 +540,18 @@ def tile_graphconvolution_pb_v_kernel(
             for d in range(DIRS):
                 quantise_gate(i, Z, "z", d)
             dr(nc.vector, i, 0)
-            times_z(nxt, 2)
+            if i == 1:
+                dr(nc.vector, i, 2)
+                times_z_psum(nxt, 2)
+            else:
+                times_z(nxt, 2)
+                dr(nc.vector, i, 2)
             add_a(nxt, 2)
             some_passes(i, 4)
             some_passes(i, 5)
             if i == 2:
                 open_acc(R, "a", 0)
                 passes(0, R)
-            dr(nc.vector, i, 2)
             if i == 1:
                 regroup_agg(0, 0)
                 regroup_agg(0, 1)
@@ -573,11 +573,14 @@ def tile_graphconvolution_pb_v_kernel(
         for d in range(DIRS):
             quantise_gate(last, C, "c", d)
             multiply(last, C, d)
-        quantise_gate(last, R, "r", 0)
-        multiply(last, R, 0)
-        dr(nc.vector, last, 2)
-        for d in (1, 2):
+        store(last, C)
+        for d in (0, 1):
             quantise_gate(last, R, "r", d)
             multiply(last, R, d)
-        store(last, C, True)
-        store(last, R, True)
+        for m in range(M_TILES):
+            m_cols = slice(m * M_TILE, (m + 1) * M_TILE)
+            dr(nc.vector, last, 2, m_cols)
+            quantise_gate(last, R, "r", 2, m_cols)
+            multiply(last, R, 2, (m,))
+        for m in range(M_TILES):
+            store_halves(last, R, m)

@@ -256,19 +256,22 @@ def tile_graphconvolution_pb_v_kernel(
                 state[i][key] = grouped_pool.tile([P, COLS, PACK], BF16, name="grouped", tag="grouped", align_bytes=64)
             return state[i][key]
 
-        def product_grouped(engine, i, name, in0, in1, d, cols, b):
+        def product_grouped(engine, i, name, d, cols=slice(0, COLS)):
             engine.tensor_tensor(
-                out=new_grouped(i, name, d)[:, cols, tokens(b)].rearrange("p (c i) j -> p c j i", i=RUN),
-                in0=state[i][in0][:, d, tokens(b), cols].rearrange("p j (c i) -> p c j i", i=RUN),
-                in1=state[i][in1][:, d, tokens(b), cols].rearrange("p j (c i) -> p c j i", i=RUN),
+                out=new_grouped(i, name, d)[:, cols].rearrange("p (c i) j -> p c j i", i=RUN),
+                in0=state[i][name][:, d, :, cols].rearrange("p j (c i) -> p c j i", i=RUN),
+                in1=state[i]["a"][:, d, :, cols].rearrange("p j (c i) -> p c j i", i=RUN),
                 op=ALU.mult,
             )
 
-        def dz(engine, i, d, b=None, cols=slice(0, COLS)):
-            product_grouped(engine, i, "z", "z", "a", d, cols, b)
+        def side_dz(i, d, cols=slice(0, COLS)):
+            product_grouped(nc.gpsimd, i, "z", d, cols)
 
-        def dr(engine, i, d, cols=slice(0, COLS)):
-            product_grouped(engine, i, "r", "r", "a", d, cols, None)
+        def dz(i, d, cols=slice(0, COLS)):
+            product_grouped(nc.vector, i, "z", d, cols)
+
+        def dr(i, d, cols=slice(0, COLS)):
+            product_grouped(nc.vector, i, "r", d, cols)
 
         def quantise(grouped, x4_dtype, codes, scales):
             nc.vector.quantize_mx(
@@ -406,10 +409,10 @@ def tile_graphconvolution_pb_v_kernel(
         turn_gt(1, 0, "x", 0)
         make_u(0, 1)
         for d in range(DIRS - 1):
-            dz(nc.vector, 0, d)
+            dz(0, d)
         make_dc(0, slice(0, 2))
         times_t(nc.gpsimd, 1, 1, state[0]["c"][:, 1])
-        dz(nc.gpsimd, 0, 2)
+        side_dz(0, 2)
         turn_gt(1, 1, "x", 1)
         regroup_dc(0, (0, 1))
         for d in range(DIRS):
@@ -423,13 +426,13 @@ def tile_graphconvolution_pb_v_kernel(
         add_a(1, 0)
         for d in range(DIRS):
             quantise_gate(0, Z, "z", d)
-        dr(nc.vector, 0, 0)
+        dr(0, 0)
         times_z_psum(1, 1)
         add_a(1, 1)
-        dr(nc.vector, 0, 2)
         subtract_c(nc.vector, 1, 2)
         times_z(1, 2)
         add_a(1, 2)
+        dr(0, 2)
         load_cz(2, 0)
         load_gate(2, "c", C, 2)
         load_cz(2, 1)
@@ -445,7 +448,7 @@ def tile_graphconvolution_pb_v_kernel(
         quantise_gate(0, R, "r", 2)
         for b in range(HALVES):
             turn_hn(1, b, "m", 2 + b)
-        dr(nc.vector, 0, 1)
+        dr(0, 1)
         for b in range(HALVES):
             square(1, "r", -0.5, b)
 
@@ -470,20 +473,22 @@ def tile_graphconvolution_pb_v_kernel(
                 quantise_gate(i - 1, R, "r", 1)
                 quantise_agg(1)
                 passes(1, Z)
-                passes(1, C)
+                multiply(1, C, 0)
             for dirs in (slice(2, 3), slice(0, 2)):
                 for b in range(HALVES):
                     make_u(i, b, dirs)
-            dz(nc.gpsimd, i, 2)
+            side_dz(i, 2)
             if i == 2:
                 subtract_c(nc.gpsimd, nxt, 2)
-            dz(nc.gpsimd, i, 0)
+            side_dz(i, 0)
             if i == 1:
-                dz(nc.gpsimd, i, 1)
+                side_dz(i, 1)
             for b in range(HALVES):
                 if has_next:
                     difference(nxt, 0, b)
                 hn_back(i, b, "x", b)
+                if i == last:
+                    multiply(1, C, 1 + b)
             for b in range(HALVES):
                 make_e(i, b)
             if has_next:
@@ -517,10 +522,14 @@ def tile_graphconvolution_pb_v_kernel(
                 store(1, C)
                 passes(1, R)
                 store(1, R)
-            if i > 1:
-                dz(nc.vector, i, 1)
-            make_dc(i)
-            regroup_dc(i)
+            if i == 1:
+                for d in (2, 0, 1):
+                    make_dc(i, slice(d, d + 1))
+                regroup_dc(i, (2, 0, 1))
+            else:
+                dz(i, 1)
+                make_dc(i)
+                regroup_dc(i)
             if not has_next:
                 open_acc(Z, "m", 0)
                 open_acc(C, "m", 2)
@@ -539,13 +548,13 @@ def tile_graphconvolution_pb_v_kernel(
                     load_agg(1, d)
             for d in range(DIRS):
                 quantise_gate(i, Z, "z", d)
-            dr(nc.vector, i, 0)
+            dr(i, 0)
             if i == 1:
-                dr(nc.vector, i, 2)
+                dr(i, 2)
                 times_z_psum(nxt, 2)
             else:
                 times_z(nxt, 2)
-                dr(nc.vector, i, 2)
+                dr(i, 2)
             add_a(nxt, 2)
             some_passes(i, 4)
             some_passes(i, 5)
@@ -562,14 +571,14 @@ def tile_graphconvolution_pb_v_kernel(
                 quantise_gate(i, C, "c", d)
             quantise_gate(i, R, "r", 0)
             quantise_gate(i, R, "r", 2)
-            dr(nc.vector, i, 1)
+            dr(i, 1)
 
         for d in range(DIRS):
             quantise_gate(last, Z, "z", d)
         passes(last, Z)
         store(last, Z)
-        dr(nc.vector, last, 0)
-        dr(nc.vector, last, 1)
+        dr(last, 0)
+        dr(last, 1)
         for d in range(DIRS):
             quantise_gate(last, C, "c", d)
             multiply(last, C, d)
@@ -579,7 +588,7 @@ def tile_graphconvolution_pb_v_kernel(
             multiply(last, R, d)
         for m in range(M_TILES):
             m_cols = slice(m * M_TILE, (m + 1) * M_TILE)
-            dr(nc.vector, last, 2, m_cols)
+            dr(last, 2, m_cols)
             quantise_gate(last, R, "r", 2, m_cols)
             multiply(last, R, 2, (m,))
         for m in range(M_TILES):

from contextlib import ExitStack

import concourse.mybir as mybir
from concourse.masks import make_identity

F32 = mybir.dt.float32
BF16 = mybir.dt.bfloat16
U32 = mybir.dt.uint32
U8 = mybir.dt.uint8
E4M3_X4 = mybir.dt.float8_e4m3fn_x4
E5M2_X4 = mybir.dt.float8_e5m2_x4
ALU = mybir.AluOpType
ACT = mybir.ActivationFunctionType

P = 128
PACK = 4
K_PASS = P * PACK
DIRS = 3
NODES = 1024
FEAT = 512
GATES = 3
R = 0
Z = 1
C = 2
NODE_BLOCKS = NODES // K_PASS
COLS = 256
COL_BLOCKS = FEAT // COLS
M_TILE = 128
M_TILES = COLS // M_TILE
BANK = 512
HALVES = PACK * COLS // BANK
RUN = 4

FLOPS = 2 * DIRS * NODES * GATES * FEAT * FEAT
BYTES = (
    2 * DIRS * NODES * FEAT
    + 2 * 2 * NODES * FEAT
    + 4 * DIRS * NODES * GATES * FEAT
    + 2 * 4 * NODES * FEAT
    + 4 * GATES * FEAT * FEAT
)


def tile_graphconvolution_pb_v_kernel(
    tc, agg, x, wih, whh, bih, bhh, wh, bh, gates, hn, t, grad_out, out
):
    nc = tc.nc
    chunks = [(cb, nb) for cb in range(COL_BLOCKS) for nb in range(NODE_BLOCKS)]
    n_chunks = len(chunks)
    last = n_chunks - 1
    with ExitStack() as ctx:
        gate_pool = ctx.enter_context(tc.tile_pool(name="gate", bufs=2))
        node_pool = ctx.enter_context(tc.tile_pool(name="node", bufs=2))
        work_pool = ctx.enter_context(tc.tile_pool(name="work", bufs=1))
        grouped_pool = ctx.enter_context(tc.tile_pool(name="grouped", bufs=3 * DIRS))
        agg_pool = ctx.enter_context(tc.tile_pool(name="agg", bufs=DIRS))
        mx_pool = ctx.enter_context(tc.tile_pool(name="dgi_mx", bufs=22))
        keep_pool = ctx.enter_context(tc.tile_pool(name="keep", bufs=1))
        result_pool = ctx.enter_context(tc.tile_pool(name="result", bufs=6))
        psum = ctx.enter_context(tc.psum_pool(name="psum", bufs=1))
        ctx.enter_context(tc.manual_schedule())

        identity = keep_pool.tile([P, P], F32, name="identity")
        make_identity(nc, identity[:])
        identity_bf = keep_pool.tile([P, P], BF16, name="identity_bf")
        make_identity(nc, identity_bf[:])
        minus_identity = keep_pool.tile([P, P], F32, name="minus_identity")
        nc.scalar.mul(out=minus_identity[:], in_=identity[:], mul=-1.0)
        agg_codes = keep_pool.tile([P, NODE_BLOCKS, DIRS, FEAT], U32, name="agg_codes", align_bytes=64)
        agg_scales = keep_pool.tile([P, NODE_BLOCKS, DIRS, FEAT], U8, name="agg_scales", align_bytes=64)

        ALL_DIRS = slice(0, DIRS)
        state = [dict() for i in range(n_chunks)]
        acc = {}

        def rows_view(rows):
            return rows.rearrange("(p j) o -> p j o", j=PACK)

        def where(i):
            cb, nb = chunks[i]
            return slice(nb * K_PASS, (nb + 1) * K_PASS), slice(cb * COLS, (cb + 1) * COLS)

        def tokens(b):
            if b is None:
                return slice(0, PACK)
            if isinstance(b, slice):
                return b
            return slice(b * PACK // HALVES, (b + 1) * PACK // HALVES)

        def flat(held, b=None):
            return held[:, tokens(b)].rearrange("p j o -> p (j o)")

        def bank(kind, k, dtype=F32, width=BANK):
            return psum.tile([P, width], dtype, name="%s%d" % (kind, k), tag="%s%d" % (kind, k))

        def load_node(i, name, dtype, src, bufs, b=None):
            if name not in state[i]:
                state[i][name] = node_pool.tile([P, PACK, COLS], dtype, name=name, tag=name, bufs=bufs)
            nc.sync.dma_start(out=state[i][name][:, tokens(b)], in_=rows_view(src)[:, tokens(b), :])

        def load_h(i, b=None):
            rows, cols = where(i)
            load_node(i, "h", BF16, x[rows, 0, cols], n_chunks, b)

        def load_gt(i, b=None):
            rows, cols = where(i)
            load_node(i, "g", BF16, grad_out[rows, 0, cols], 2, b)
            load_node(i, "t", F32, t[rows, 0, cols], 2, b)

        def load_hn(i):
            rows, cols = where(i)
            load_node(i, "h_n", F32, hn[0, rows, cols], 2)

        def new_gate(i, name):
            if name not in state[i]:
                state[i][name] = gate_pool.tile([P, DIRS, PACK, COLS], F32, name=name, tag=name)
            return state[i][name]

        def load_gate(i, name, gate, d, b=None):
            cb, nb = chunks[i]
            rows, cols = where(i)
            first = gate * FEAT + cb * COLS
            nc.sync.dma_start(
                out=new_gate(i, name)[:, d, tokens(b)],
                in_=rows_view(gates[d, 0, rows, first : first + COLS])[:, tokens(b), :],
            )

        def load_cz(i, d):
            load_gate(i, "c", C, d)
            load_gate(i, "z", Z, d)

        def load_r(i):
            for d in range(DIRS):
                load_gate(i, "r", R, d)

        def load_agg(i, d):
            rows, cols = where(i)
            agg_rows = agg_pool.tile([P, PACK, FEAT], BF16, name="agg_rows", tag="agg_rows")
            nc.sync.dma_start(out=agg_rows[:], in_=rows_view(agg[d, 0, rows, :]))
            state[i].setdefault("agg_rows", []).append(agg_rows)

        def one(i, name, d, b=None):
            return flat(state[i][name][:, d], b)

        def some(i, name, dirs, b=None):
            return state[i][name][:, dirs, tokens(b)].rearrange("p d j o -> p d (j o)")

        def for_some(held, dirs):
            return held[:].unsqueeze(1).to_broadcast([P, dirs.stop - dirs.start, BANK])

        def difference(i, d, b):
            diff = bank("ama"[d], b)
            nc.tensor.matmul(out=diff[:], lhsT=identity_bf[:], rhs=flat(state[i]["h"], b), start=True, stop=False)
            nc.tensor.matmul(out=diff[:], lhsT=minus_identity[:], rhs=one(i, "c", d, b), start=False, stop=True)
            state[i][("diff", d, b)] = diff

        def blocks(b):
            return [(j, fb) for j in range(tokens(b).start, tokens(b).stop) for fb in range(M_TILES)]

        def add_transposed(i, b, name, d, first, stop):
            todo = blocks(b)
            for k, (j, fb) in enumerate(todo):
                nc.tensor.matmul(
                    out=state[i][("tot_t", b)][:, k * P : (k + 1) * P],
                    lhsT=state[i][name][:, d, j, fb * P : (fb + 1) * P],
                    rhs=identity[:], is_transpose=True,
                    start=(first and k == 0), stop=(stop and k == len(todo) - 1),
                )

        def add_c(i, d, halves=(0, 1)):
            for b in halves:
                if d == 0:
                    state[i][("tot_t", b)] = bank("x", b)
                add_transposed(i, b, "c", d, d == 0, False)

        def add_a(i, d, halves=(0, 1)):
            for b in halves:
                add_transposed(i, b, "a", d, False, d == DIRS - 1)

        def turn(i, name, b, source, kind, k, factor):
            turned = bank(kind, k)
            for k, (j, fb) in enumerate(blocks(b)):
                nc.tensor.transpose(turned[:, k * P : (k + 1) * P], source[:, j, fb * P : (fb + 1) * P], identity[:])
            held = work_pool.tile([P, BANK], F32, name=name, tag="%s%d" % (name, b))
            nc.scalar.mul(out=held[:], in_=turned[:], mul=factor)
            state[i][(name, b)] = held

        def turn_gt(i, b, kind, k):
            turn(i, "gt_t", b, state[i][("gt", b)], kind, k, -1.0)

        def turn_hn(i, b, kind, k):
            turn(i, "hn_t", b, state[i]["h_n"], kind, k, 1.0)

        def turn_back(i, name, b, source, kind, k):
            held = bank(kind, k)
            for k in range(BANK // P):
                nc.tensor.transpose(
                    held[:, k * P : (k + 1) * P], state[i][(source, b)][:, k * P : (k + 1) * P], identity[:]
                )
            state[i][(name, b)] = held

        def dh_back(i, b):
            turn_back(i, "dh", b, "dh_t", "x", b)

        def hn_back(i, b, kind, k):
            turn_back(i, "hn", b, "hn_t", kind, k)

        def mask(i, b):
            st = state[i]
            dh_t = work_pool.tile([P, BANK], F32, name="dh_t", tag="dh_t%d" % b)
            nc.vector.scalar_tensor_tensor(
                out=dh_t[:], in0=st[("tot_t", b)][:], scalar=0.0, in1=st[("gt_t", b)][:],
                op0=ALU.is_gt, op1=ALU.mult,
            )
            st[("dh_t", b)] = dh_t

        def subtract_c(engine, i, d, b=None):
            new_gate(i, "a")
            engine.tensor_tensor(
                out=one(i, "a", d, b), in0=flat(state[i]["h"], b), in1=one(i, "c", d, b), op=ALU.subtract
            )

        def times_z(i, d, b=None):
            nc.vector.tensor_tensor(
                out=one(i, "a", d, b), in0=one(i, "z", d, b), in1=one(i, "a", d, b), op=ALU.mult
            )

        def times_z_psum(i, d):
            new_gate(i, "a")
            for b in range(HALVES):
                nc.vector.tensor_tensor(
                    out=one(i, "a", d, b), in0=one(i, "z", d, b), in1=state[i][("diff", d, b)][:], op=ALU.mult,
                )

        def make_u(i, b, dirs=ALL_DIRS):
            nc.vector.scalar_tensor_tensor(
                out=some(i, "z", dirs, b), in0=some(i, "z", dirs, b), scalar=1.0, in1=for_some(state[i][("dh", b)], dirs),
                op0=ALU.subtract, op1=ALU.mult,
            )

        def make_e(i, b, dirs=ALL_DIRS):
            nc.vector.scalar_tensor_tensor(
                out=some(i, "r", dirs, b), in0=some(i, "r", dirs, b), scalar=0.25, in1=for_some(state[i][("hn", b)], dirs),
                op0=ALU.subtract, op1=ALU.mult,
            )

        def make_dc(i, dirs=ALL_DIRS):
            nc.vector.scalar_tensor_tensor(
                out=some(i, "a", dirs), in0=some(i, "c", dirs), scalar=1.0, in1=some(i, "z", dirs),
                op0=ALU.subtract, op1=ALU.mult,
            )

        def new_grouped(i, name, d):
            key = ("grouped_" + name, d)
            if key not in state[i]:
                state[i][key] = grouped_pool.tile([P, COLS, PACK], BF16, name="grouped", tag="grouped", align_bytes=64)
            return state[i][key]

        def product_grouped(engine, i, name, d, cols=slice(0, COLS)):
            engine.tensor_tensor(
                out=new_grouped(i, name, d)[:, cols].rearrange("p (c i) j -> p c j i", i=RUN),
                in0=state[i][name][:, d, :, cols].rearrange("p j (c i) -> p c j i", i=RUN),
                in1=state[i]["a"][:, d, :, cols].rearrange("p j (c i) -> p c j i", i=RUN),
                op=ALU.mult,
            )

        def side_dz(i, d, cols=slice(0, COLS)):
            product_grouped(nc.gpsimd, i, "z", d, cols)

        def dz(i, d, cols=slice(0, COLS)):
            product_grouped(nc.vector, i, "z", d, cols)

        def dr(i, d, cols=slice(0, COLS)):
            product_grouped(nc.vector, i, "r", d, cols)

        def quantise(grouped, x4_dtype, codes, scales):
            nc.vector.quantize_mx(
                out=codes.bitcast(x4_dtype), scales=scales, in_=grouped.rearrange("p o j -> p (o j)"),
            )

        def quantise_gate(i, gate, name, d, cols=slice(0, COLS)):
            if (gate, d) not in state[i]:
                codes = mx_pool.tile([P, COLS], U32, name="codes", tag="codes", align_bytes=64)
                scales = mx_pool.tile([P, COLS], U8, name="scales", tag="scales", align_bytes=64)
                state[i][(gate, d)] = (codes, scales)
            codes, scales = state[i][(gate, d)]
            quantise(state[i][("grouped_" + name, d)][:, cols], E5M2_X4, codes[:, cols], scales[:, cols])

        def quantise_agg(i):
            cb, nb = chunks[i]
            for d in range(DIRS):
                quantise(state[i]["agg_grouped"][d][:], E4M3_X4, agg_codes[:, nb, d, :], agg_scales[:, nb, d, :])

        def square(i, name, bias, b=None, dirs=ALL_DIRS):
            nc.scalar.activation(
                out=some(i, name, dirs, b), in_=some(i, name, dirs, b), func=ACT.Square, bias=bias
            )

        def regroup(grouped, values, factor):
            nc.scalar.activation(
                out=grouped.rearrange("p (c i) j -> p c j i", i=RUN),
                in_=values.rearrange("p j (c i) -> p c j i", i=RUN),
                func=ACT.Copy, scale=factor,
            )

        def regroup_dc(i, dirs=range(DIRS)):
            for d in dirs:
                regroup(new_grouped(i, "c", d)[:], state[i]["a"][:, d], -1.0)

        def regroup_agg(i, d):
            grouped = agg_pool.tile([P, FEAT, PACK], BF16, name="agg_grouped", tag="agg_grouped", align_bytes=64)
            regroup(grouped[:], state[i]["agg_rows"][d][:], 1.0)
            state[i].setdefault("agg_grouped", []).append(grouped)

        def times_t(engine, i, b, held):
            engine.tensor_tensor(out=flat(held, b), in0=flat(state[i]["g"], b), in1=flat(state[i]["t"], b), op=ALU.mult)
            for half in range(HALVES) if b is None else (b,):
                state[i][("gt", half)] = held

        def open_acc(gate, kind, first):
            for m in range(M_TILES):
                acc[(gate, m)] = bank(kind, first + m)

        def multiply(i, gate, d, tiles=range(M_TILES)):
            cb, nb = chunks[i]
            codes, scales = state[i][(gate, d)]
            for m in tiles:
                m_cols = slice(m * M_TILE, (m + 1) * M_TILE)
                nc.tensor.matmul_mx(
                    out=acc[(gate, m)][:],
                    lhsT=codes[:, m_cols].bitcast(E5M2_X4), lhsT_scale=scales[:, m_cols],
                    rhs=agg_codes[:, nb, d, :].bitcast(E4M3_X4), rhs_scale=agg_scales[:, nb, d, :],
                    start=(nb == 0 and d == 0), stop=(nb == NODE_BLOCKS - 1 and d == DIRS - 1),
                )

        def passes(i, gate):
            for d in range(DIRS):
                multiply(i, gate, d)

        def store_halves(i, gate, m):
            cb, nb = chunks[i]
            first = gate * FEAT + cb * COLS + m * M_TILE
            result = result_pool.tile([M_TILE, FEAT], F32, name="result", tag="result")
            for k, copy in enumerate((nc.vector.tensor_copy, nc.scalar.copy)):
                half = slice(k * FEAT // 2, (k + 1) * FEAT // 2)
                copy(out=result[:, half], in_=acc[(gate, m)][:, half])
                nc.sync.dma_start(out=out[first : first + M_TILE, half], in_=result[:, half])

        def store(i, gate):
            cb, nb = chunks[i]
            for m in range(M_TILES):
                result = result_pool.tile([M_TILE, FEAT], F32, name="result", tag="result")
                nc.scalar.copy(out=result[:], in_=acc[(gate, m)][:])
                first = gate * FEAT + cb * COLS + m * M_TILE
                nc.sync.dma_start(out=out[first : first + M_TILE, :], in_=result[:])

        for b in range(HALVES):
            load_h(0, b)
            for d in range(DIRS):
                load_gate(0, "c", C, d, b)
            load_gt(0, b)
            for d in range(DIRS):
                load_gate(0, "z", Z, d, b)
        load_h(1)
        load_gt(1)
        load_hn(0)
        load_r(0)
        load_cz(1, 0)
        load_cz(1, 1)
        load_cz(1, 2)
        load_hn(1)
        load_gt(2)
        load_h(2)
        load_r(1)

        for d in range(DIRS):
            add_c(0, d, (0,))
            subtract_c(nc.vector, 0, d, 0)
        times_t(nc.vector, 0, 0, state[0]["t"])
        turn_gt(0, 0, "a", 0)
        square(0, "c", 0.0, 0)
        for d in range(DIRS):
            times_z(0, d, 0)
            add_a(0, d, (0,))
        mask(0, 0)
        dh_back(0, 0)
        for d in range(DIRS):
            add_c(0, d, (1,))
            subtract_c(nc.vector, 0, d, 1)
        make_u(0, 0)
        times_t(nc.vector, 0, 1, state[0]["t"])
        turn_gt(0, 1, "a", 1)
        square(0, "c", 0.0, 1)
        for d in range(DIRS):
            times_z(0, d, 1)
            add_a(0, d, (1,))
        mask(0, 1)
        dh_back(0, 1)
        for b in range(HALVES):
            turn_hn(0, b, "m", 2 + b)
        for d in range(DIRS):
            square(0, "r", -0.5, None, slice(d, d + 1))
        for b in range(HALVES):
            hn_back(0, b, "m", 2 + b)
        for d in range(DIRS - 1):
            for b in range(HALVES):
                difference(1, d, b)
        times_t(nc.gpsimd, 1, 0, state[1]["t"])
        turn_gt(1, 0, "x", 0)
        make_u(0, 1)
        for d in range(DIRS - 1):
            dz(0, d)
        make_dc(0, slice(0, 2))
        times_t(nc.gpsimd, 1, 1, state[0]["c"][:, 1])
        side_dz(0, 2)
        turn_gt(1, 1, "x", 1)
        regroup_dc(0, (0, 1))
        for d in range(DIRS):
            for b in range(HALVES):
                make_e(0, b, slice(d, d + 1))
        times_z_psum(1, 0)
        make_dc(0, slice(2, 3))
        regroup_dc(0, (2,))
        for d in range(DIRS):
            add_c(1, d)
        add_a(1, 0)
        for d in range(DIRS):
            quantise_gate(0, Z, "z", d)
        dr(0, 0)
        times_z_psum(1, 1)
        add_a(1, 1)
        subtract_c(nc.vector, 1, 2)
        times_z(1, 2)
        add_a(1, 2)
        dr(0, 2)
        load_cz(2, 0)
        load_gate(2, "c", C, 2)
        load_cz(2, 1)
        load_gate(2, "z", Z, 2)
        load_hn(2)
        load_h(3)
        load_gt(3)
        for d in range(DIRS):
            load_agg(0, d)
        for d in range(DIRS):
            quantise_gate(0, C, "c", d)
        quantise_gate(0, R, "r", 0)
        quantise_gate(0, R, "r", 2)
        for b in range(HALVES):
            turn_hn(1, b, "m", 2 + b)
        dr(0, 1)
        for b in range(HALVES):
            square(1, "r", -0.5, b)

        def some_passes(i, k):
            if i == 2:
                if k == 0:
                    open_acc(Z, "m", 0)
                    open_acc(C, "m", 2)
                multiply(0, (Z, C)[k // DIRS], k % DIRS)

        for i in range(1, n_chunks):
            nxt = i + 1
            has_next = nxt < n_chunks
            if has_next:
                times_t(nc.gpsimd, nxt, None, state[i - 1]["r"][:, 1])
            for b in range(HALVES):
                mask(i, b)
            for b in range(HALVES):
                dh_back(i, b)
            square(i, "c", 0.0)
            if not has_next:
                quantise_gate(i - 1, R, "r", 1)
                quantise_agg(1)
                passes(1, Z)
                multiply(1, C, 0)
            for dirs in (slice(2, 3), slice(0, 2)):
                for b in range(HALVES):
                    make_u(i, b, dirs)
            side_dz(i, 2)
            if i == 2:
                subtract_c(nc.gpsimd, nxt, 2)
            side_dz(i, 0)
            if i == 1:
                side_dz(i, 1)
            for b in range(HALVES):
                if has_next:
                    difference(nxt, 0, b)
                hn_back(i, b, "x", b)
                if i == last:
                    multiply(1, C, 1 + b)
            for b in range(HALVES):
                make_e(i, b)
            if has_next:
                load_r(nxt)
                for b in range(HALVES):
                    difference(nxt, 1, b)
                for b in range(HALVES):
                    turn_gt(nxt, b, "x", b)
                for b in range(HALVES):
                    turn_hn(nxt, b, "x", b)
                if i == 2:
                    regroup_agg(1, 0)
                    regroup_agg(1, 1)
                times_z_psum(nxt, 0)
                times_z_psum(nxt, 1)
                add_c(nxt, 0)
                if i == 1:
                    for b in range(HALVES):
                        difference(nxt, 2, b)
                add_a(nxt, 0)
                add_c(nxt, 1)
                add_a(nxt, 1)
                add_c(nxt, 2)
                quantise_gate(i - 1, R, "r", 1)
                if i == 2:
                    quantise_agg(0)
                for k in range(4):
                    some_passes(i, k)
            else:
                store(1, Z)
                store(1, C)
                passes(1, R)
                store(1, R)
            if i == 1:
                for d in (2, 0, 1):
                    make_dc(i, slice(d, d + 1))
                regroup_dc(i, (2, 0, 1))
            else:
                dz(i, 1)
                make_dc(i)
                regroup_dc(i)
            if not has_next:
                open_acc(Z, "m", 0)
                open_acc(C, "m", 2)
                open_acc(R, "x", 0)
                passes(2, Z)
                passes(2, C)
                passes(2, R)
                break
            if i == 1:
                load_cz(3, 0)
                load_gate(3, "c", C, 2)
                load_cz(3, 1)
                load_gate(3, "z", Z, 2)
                load_hn(3)
                for d in range(DIRS):
                    load_agg(1, d)
            for d in range(DIRS):
                quantise_gate(i, Z, "z", d)
            dr(i, 0)
            if i == 1:
                dr(i, 2)
                times_z_psum(nxt, 2)
            else:
                times_z(nxt, 2)
                dr(i, 2)
            add_a(nxt, 2)
            some_passes(i, 4)
            some_passes(i, 5)
            if i == 2:
                open_acc(R, "a", 0)
                passes(0, R)
            if i == 1:
                regroup_agg(0, 0)
                regroup_agg(0, 1)
            for b in range(HALVES):
                square(nxt, "r", -0.5, b)
            regroup_agg(i - 1, 2)
            for d in range(DIRS):
                quantise_gate(i, C, "c", d)
            quantise_gate(i, R, "r", 0)
            quantise_gate(i, R, "r", 2)
            dr(i, 1)

        for d in range(DIRS):
            quantise_gate(last, Z, "z", d)
        passes(last, Z)
        store(last, Z)
        dr(last, 0)
        dr(last, 1)
        for d in range(DIRS):
            quantise_gate(last, C, "c", d)
            multiply(last, C, d)
        store(last, C)
        for d in (0, 1):
            quantise_gate(last, R, "r", d)
            multiply(last, R, d)
        for m in range(M_TILES):
            m_cols = slice(m * M_TILE, (m + 1) * M_TILE)
            dr(last, 2, m_cols)
            quantise_gate(last, R, "r", 2, m_cols)
            multiply(last, R, 2, (m,))
        for m in range(M_TILES):
            store_halves(last, R, m)
